import numpy as np
import ml_dtypes


def mxq(x, axis, fmt="e4m3"):
    dtype, down = {"e4m3": (ml_dtypes.float8_e4m3fn, 7), "e5m2": (ml_dtypes.float8_e5m2, 14)}[fmt]
    v = np.moveaxis(np.asarray(x, np.float32).astype(ml_dtypes.bfloat16).astype(np.float64), axis, -1)
    blocks = v.reshape(v.shape[:-1] + (-1, 32))
    amax = np.abs(blocks).max(-1, keepdims=True)
    byte = np.maximum(np.where(amax > 0, np.frexp(amax)[1] - 1 + 127, 0) - down, 1)
    scale = np.exp2(byte - 127.0)
    codes = (blocks / scale).astype(np.float32).astype(dtype).astype(np.float64)
    return np.moveaxis((codes * scale).reshape(v.shape), -1, axis)


WIDE = False


def mx_kscale(k):
    if not WIDE:
        return np.ones(k)
    levels = np.array([10, -10, 5, -5, 0])
    a = np.random.permutation(np.resize(levels, k // 512 * 4)).reshape(k // 512, 4)
    idx = np.arange(k)
    return np.exp2(a[idx // 512, idx % 128 // 32])


BF16 = ml_dtypes.bfloat16


def bf(x):
    return np.asarray(x, np.float32).astype(BF16)


def f64(x):
    return np.asarray(x).astype(np.float64)


T, S, B, E, Z = 1024, 1024, 4, 512, 128


def silu(v):
    return v / (1.0 + np.exp(-v))


def setup_inputs():
    s, t = mx_kscale(E), mx_kscale(E)
    return {"q_scaled": bf(np.random.standard_normal((T, B, Z)) * 1.5 / np.sqrt(Z)),
            "k": bf(np.random.standard_normal((S, B, Z)) * 1.5),
            "key": bf(np.random.standard_normal((S, B, E)) * s),
            "query": bf(np.random.standard_normal((T, B, E)) * t),
            "Wv": bf(np.random.standard_normal((E, E)) / np.sqrt(E) / s[None, :]),
            "bv": bf(np.random.standard_normal(E) * 0.3),
            "Wr": bf(np.random.standard_normal((E, E)) / np.sqrt(E) / t[None, :]),
            "br": bf(np.random.standard_normal(E) * 0.3)}


def reference(q_scaled, k, key, query, Wv, bv, Wr, br):
    v = silu((mxq(f64(key), 2, "e4m3") @ mxq(f64(Wv), 1, "e4m3").T) + f64(bv))
    r = silu((mxq(f64(query), 2, "e4m3") @ mxq(f64(Wr), 1, "e4m3").T) + f64(br))
    qk = f64(q_scaled).transpose(1, 0, 2) @ f64(k).transpose(1, 2, 0)
    e = np.exp(qk - qk.max(-1, keepdims=True))
    h = (mxq(e, 2, "e4m3") @ mxq(v.transpose(1, 0, 2), 1, "e4m3")) / e.sum(-1, keepdims=True)
    return h.transpose(1, 0, 2) * r

@@ -1,0 +1,334 @@
+from contextlib import ExitStack
+
+import concourse.mybir as mybir
+from concourse.masks import make_identity
+
+F32 = mybir.dt.float32
+BF16 = mybir.dt.bfloat16
+U32 = mybir.dt.uint32
+U8 = mybir.dt.uint8
+FP8X4 = mybir.dt.float8_e4m3fn_x4
+ACT = mybir.ActivationFunctionType
+ALU = mybir.AluOpType
+AX = mybir.AxisListType
+
+P = 128
+T, S, B, E, Z = 1024, 1024, 4, 512, 128
+FLOPS = 2 * (2 * S * B * E * E + B * T * S * Z + B * T * S * E)
+
+MANUAL = True
+XIN_BUFS = 6
+
+
+def tile_gatedcrossattention_pa_t_kernel(tc, q_scaled, k, key, query, Wv, bv, Wr, br, out):
+    nc = tc.nc
+    with ExitStack() as ctx:
+        const = ctx.enter_context(tc.tile_pool(name="const", bufs=1))
+        work = ctx.enter_context(tc.tile_pool(name="work", bufs=2))
+        psum = ctx.enter_context(tc.psum_pool(name="psum", bufs=4))
+        if MANUAL:
+            ctx.enter_context(tc.manual_schedule())
+
+        def copy_on(eng, dst, src):
+            if eng == "v":
+                nc.vector.tensor_copy(out=dst, in_=src)
+            else:
+                nc.scalar.copy(out=dst, in_=src)
+
+        ident_f = const.tile([P, P], F32, name="ident_f")
+        ident_b = const.tile([P, P], BF16, name="ident_b")
+        bias_v = const.tile([P, E], BF16, name="bias_v")
+        bias_r = const.tile([P, E], BF16, name="bias_r")
+        nc.gpsimd.dma_start(out=bias_v[:], in_=bv.partition_broadcast(P))
+        nc.gpsimd.dma_start(out=bias_r[:], in_=br.partition_broadcast(P))
+        make_identity(nc, ident_f[:])
+        make_identity(nc, ident_b[:])
+
+        q_sb = const.tile([P, 2, 4, B * Z], BF16, name="q_sb")
+        k_sb = const.tile([P, 2, 4, B * Z], BF16, name="k_sb")
+        qT = [const.tile([P, T], BF16, name="qT%d" % b) for b in range(B)]
+        kT = [const.tile([P, S], BF16, name="kT%d" % b) for b in range(B)]
+        w_codes = [const.tile([P, E], U32, name="w_codes%d" % i, align_bytes=64) for i in range(2)]
+        w_scales = [const.tile([P, E], U8, name="w_scales%d" % i, align_bytes=64) for i in range(2)]
+        v_codes = const.tile([P, 2 * B, E], U32, name="v_codes", align_bytes=64)
+        v_scales = const.tile([P, 2 * B, E], U8, name="v_scales", align_bytes=64)
+        r_sb = const.tile([P, 8 * B, E], F32, name="r_sb")
+
+        k_units = [("k", b, g) for b in range(B) for g in range(2)]
+        q_units = [("q", b, h) for b in range(B) for h in range(2)]
+        units = [("w", 0, 0)] + k_units[:6] + [("w", 1, 0)] + k_units[6:] + q_units
+        n_units = len(units)
+        st = [dict() for u in range(n_units)]
+
+        def load(u):
+            if u < 0 or u >= n_units:
+                return
+            kind, a, c = units[u]
+            xin = work.tile([P, 4, E], BF16, tag="xin", name="xin", bufs=XIN_BUFS)
+            if kind == "w":
+                src = (Wv, Wr)[a].rearrange("(m p) c -> p m c", p=P)
+            else:
+                src = (key if kind == "k" else query)[512 * c : 512 * c + 512, a, :].rearrange(
+                    "(p j) e -> p j e", j=4
+                )
+            nc.sync.dma_start(out=xin[:], in_=src)
+            st[u]["xin"] = xin
+
+        def stage_a(u):
+            if u < 0 or u >= n_units:
+                return
+            xin = st[u]["xin"]
+            tps = []
+            for half in range(2):
+                tp = psum.tile([P, 2, 2, P], F32, tag="aux", name="tp", bufs=4)
+                for r in range(2):
+                    words = xin[:, 2 * half + r, :].bitcast(F32)
+                    for w in range(2):
+                        nc.tensor.transpose(tp[:, r, w, :], words[:, w * P : (w + 1) * P], ident_f[:])
+                tps.append(tp)
+            st[u]["tps"] = tps
+
+        def stage_eva(u):
+            if u < 0 or u >= n_units:
+                return
+            kind = units[u][0]
+            grouped = work.tile([P, 4 * E], BF16, tag="grouped", name="grouped", bufs=3, align_bytes=64)
+            g32 = grouped[:].bitcast(F32).rearrange("p (r c w) -> p r c w", r=4, w=2)
+            engines = ("s", "v") if kind == "k" else ("s", "s")
+            for half in range(2):
+                copy_on(
+                    engines[half],
+                    g32[:, 2 * half : 2 * half + 2, :, :],
+                    st[u]["tps"][half][:].rearrange("p r w c -> p r c w"),
+                )
+            st[u]["grouped"] = grouped
+
+        def stage_b(u):
+            if u < 0 or u >= n_units:
+                return
+            kind, a, c = units[u]
+            if kind == "w":
+                codes, scales = w_codes[a], w_scales[a]
+            else:
+                codes = work.tile([P, E], U32, tag="x_codes", name="x_codes", bufs=2, align_bytes=64)
+                scales = work.tile([P, E], U8, tag="x_scales", name="x_scales", bufs=2, align_bytes=64)
+            nc.vector.quantize_mx(out=codes[:].bitcast(FP8X4), scales=scales[:], in_=st[u]["grouped"][:])
+            st[u]["codes"] = codes
+            st[u]["scales"] = scales
+
+        def stage_c(u, j):
+            if u < 0 or u >= n_units or units[u][0] == "w":
+                return
+            w = 0 if units[u][0] == "k" else 1
+            pj = psum.tile([P, E], F32, tag="big", name="pj", bufs=4)
+            cols = slice(j * P, (j + 1) * P)
+            nc.tensor.matmul_mx(
+                out=pj[:],
+                lhsT=st[u]["codes"][:, cols].bitcast(FP8X4),
+                lhsT_scale=st[u]["scales"][:, cols],
+                rhs=w_codes[w][:].bitcast(FP8X4),
+                rhs_scale=w_scales[w][:],
+                start=True,
+                stop=True,
+            )
+            st[u]["pj%d" % j] = pj
+
+        def stage_d(u, j):
+            if u < 0 or u >= n_units or units[u][0] == "w":
+                return
+            kind, a, c = units[u]
+            if kind == "k":
+                if j == 0:
+                    y = work.tile([P, 4, E], F32, tag="y", name="y", bufs=2)
+                    st[u]["y"] = y
+                dst = st[u]["y"][:, j, :]
+                bias = bias_v
+            else:
+                dst = r_sb[:, 4 * (2 * a + c) + j, :]
+                bias = bias_r
+            nc.vector.tensor_tensor(out=dst, in0=st[u]["pj%d" % j][:], in1=bias[:], op=ALU.add)
+
+        def stage_e(u):
+            if u < 0 or u >= n_units or units[u][0] == "w":
+                return
+            kind, a, c = units[u]
+            if kind == "k":
+                vg = work.tile([P, 4 * E], BF16, tag="vg", name="vg", bufs=2, align_bytes=64)
+                nc.scalar.activation(
+                    out=vg[:].rearrange("p (e j) -> p e j", j=4),
+                    in_=st[u]["y"][:].rearrange("p j e -> p e j"),
+                    func=ACT.Silu,
+                )
+                st[u]["vg"] = vg
+            else:
+                rr = r_sb[:, 4 * (2 * a + c) : 4 * (2 * a + c) + 4, :]
+                nc.scalar.activation(out=rr, in_=rr, func=ACT.Silu)
+
+        def stage_f(u):
+            if u < 0 or u >= n_units or units[u][0] != "k":
+                return
+            kind, a, c = units[u]
+            nc.vector.quantize_mx(
+                out=v_codes[:, 2 * a + c, :].bitcast(FP8X4),
+                scales=v_scales[:, 2 * a + c, :],
+                in_=st[u]["vg"][:],
+            )
+
+        qk_items = [(w, b) for b in range(B) for w in (1, 0)]
+        qk_ps = dict()
+
+        def qk_transpose(m):
+            if m < 0 or m >= len(qk_items):
+                return
+            w, b = qk_items[m]
+            src = (q_sb, k_sb)[w]
+            tq = psum.tile([P, 8, P], BF16, tag="aux", name="tq", bufs=4)
+            for h in range(2):
+                for i in range(4):
+                    nc.tensor.transpose(tq[:, 4 * h + i, :], src[:, h, i, b * Z : (b + 1) * Z], ident_b[:])
+            qk_ps[m] = tq
+
+        def qk_evac(m):
+            if m < 0 or m >= len(qk_items):
+                return
+            w, b = qk_items[m]
+            dst = (qT, kT)[w][b]
+            copy_on("sv"[m % 2], dst[:], qk_ps[m][:].rearrange("p n c -> p (n c)"))
+
+        for u in range(XIN_BUFS):
+            load(u)
+        nc.sync.dma_start(out=k_sb[:], in_=k.rearrange("(h p i) b z -> p h i (b z)", p=P, i=4))
+        nc.sync.dma_start(out=q_sb[:], in_=q_scaled.rearrange("(h p i) b z -> p h i (b z)", p=P, i=4))
+
+        for step in range(-3, n_units + 2):
+            stage_a(step + 3)
+            load(step + 3 + XIN_BUFS)
+            d = step - (n_units - 3)
+            if d >= 0:
+                qk_transpose(2 * d)
+                qk_transpose(2 * d + 1)
+            stage_b(step + 1)
+            stage_eva(step + 2)
+            if d >= 1:
+                qk_evac(2 * d - 2)
+                qk_evac(2 * d - 1)
+            for j in range(4):
+                stage_d(step, j)
+                stage_c(step + 1, j)
+            stage_e(step - 1)
+            stage_f(step - 2)
+
+        n_tiles = 8 * B
+        at = [dict() for i in range(n_tiles)]
+
+        def ok(i):
+            return 0 <= i < n_tiles
+
+        def scores(i):
+            b, n = i // 8, i % 8
+            at[i]["sc"] = []
+            for g in range(2):
+                sc = psum.tile([P, 512], F32, tag="big", name="sc", bufs=4)
+                nc.tensor.matmul(
+                    sc[:],
+                    lhsT=qT[b][:, n * P : (n + 1) * P],
+                    rhs=kT[b][:, g * 512 : (g + 1) * 512],
+                    start=True,
+                    stop=True,
+                )
+                at[i]["sc"].append(sc)
+
+        def rowmax(i):
+            m2 = work.tile([P, 2], F32, tag="m2", name="m2", bufs=4)
+            for g in range(2):
+                nc.vector.tensor_reduce(out=m2[:, g : g + 1], in_=at[i]["sc"][g][:], axis=AX.X, op=ALU.max)
+            negm = work.tile([P, 1], F32, tag="negm", name="negm", bufs=4)
+            nc.vector.tensor_scalar(
+                out=negm[:], in0=m2[:, 0:1], scalar1=m2[:, 1:2], scalar2=-1.0, op0=ALU.max, op1=ALU.mult
+            )
+            at[i]["negm"] = negm
+
+        def exps(i):
+            e_sb = work.tile([P, 2, 512], BF16, tag="e_sb", name="e_sb", bufs=3)
+            rs2 = work.tile([P, 2], F32, tag="rs2", name="rs2", bufs=8)
+            for g in range(2):
+                nc.scalar.activation(
+                    out=e_sb[:, g, :],
+                    in_=at[i]["sc"][g][:],
+                    func=ACT.Exp,
+                    bias=at[i]["negm"][:],
+                    scale=1.0,
+                    accum_out=rs2[:, g : g + 1],
+                )
+            at[i]["e_sb"] = e_sb
+            at[i]["rs2"] = rs2
+
+        def e_transpose(i):
+            et = psum.tile([P, 2, 4, P], BF16, tag="aux", name="et", bufs=4)
+            for g in range(2):
+                for j in range(4):
+                    nc.tensor.transpose(et[:, g, j, :], at[i]["e_sb"][:, g, j * P : (j + 1) * P], ident_b[:])
+            at[i]["et"] = et
+
+        def e_evac(i):
+            eg = work.tile([P, 2, P, 4], BF16, tag="eg", name="eg", bufs=3, align_bytes=64)
+            copy_on("s", eg[:], at[i]["et"][:].rearrange("p g j t -> p g t j"))
+            at[i]["eg"] = eg
+
+        def e_quant(i):
+            e_codes = work.tile([P, 2 * P], U32, tag="e_codes", name="e_codes", bufs=2, align_bytes=64)
+            e_scales = work.tile([P, 2 * P], U8, tag="e_scales", name="e_scales", bufs=2, align_bytes=64)
+            nc.vector.quantize_mx(
+                out=e_codes[:].bitcast(FP8X4),
+                scales=e_scales[:],
+                in_=at[i]["eg"][:].rearrange("p g t j -> p (g t j)"),
+            )
+            at[i]["e_codes"] = e_codes
+            at[i]["e_scales"] = e_scales
+
+        def e_times_v(i):
+            b = i // 8
+            h_ps = psum.tile([P, E], F32, tag="aux", name="h_ps", bufs=4)
+            for g in range(2):
+                cols = slice(g * P, (g + 1) * P)
+                nc.tensor.matmul_mx(
+                    out=h_ps[:],
+                    lhsT=at[i]["e_codes"][:, cols].bitcast(FP8X4),
+                    lhsT_scale=at[i]["e_scales"][:, cols],
+                    rhs=v_codes[:, 2 * b + g, :].bitcast(FP8X4),
+                    rhs_scale=v_scales[:, 2 * b + g, :],
+                    start=(g == 0),
+                    stop=(g == 1),
+                )
+            at[i]["h_ps"] = h_ps
+
+        def finish(i):
+            b, h, ii = i // 8, (i % 8) // 4, i % 4
+            rsum = work.tile([P, 1], F32, tag="rsum", name="rsum", bufs=4)
+            rinv = work.tile([P, 1], F32, tag="rinv", name="rinv", bufs=4)
+            rs2 = at[i]["rs2"]
+            nc.vector.tensor_tensor(out=rsum[:], in0=rs2[:, 0:1], in1=rs2[:, 1:2], op=ALU.add)
+            nc.vector.reciprocal(out=rinv[:], in_=rsum[:])
+            o_sb = work.tile([P, E], F32, tag="o_sb", name="o_sb", bufs=4)
+            nc.vector.scalar_tensor_tensor(
+                out=o_sb[:], in0=at[i]["h_ps"][:], scalar=rinv[:, 0:1], in1=r_sb[:, i, :], op0=ALU.mult, op1=ALU.mult
+            )
+            dst = out[512 * h : 512 * h + 512, b, :].rearrange("(p i) e -> p i e", i=4)
+            nc.sync.dma_start(out=dst[:, ii, :], in_=o_sb[:])
+
+        for step in range(-2, n_tiles + 3):
+            if ok(step - 2):
+                e_quant(step - 2)
+                e_times_v(step - 2)
+            if ok(step + 1):
+                rowmax(step + 1)
+            if ok(step):
+                exps(step)
+            if ok(step + 2):
+                scores(step + 2)
+            if ok(step):
+                e_transpose(step)
+            if ok(step - 1):
+                e_evac(step - 1)
+            if ok(step - 3):
+                finish(step - 3)

@@ -53,6 +53,8 @@ def tile_gatedcrossattention_pa_t_kernel(tc, q_scaled, k, key, query, Wv, bv, Wr
         v_codes = const.tile([P, 2 * B, E], U32, name="v_codes", align_bytes=64)
         v_scales = const.tile([P, 2 * B, E], U8, name="v_scales", align_bytes=64)
         r_sb = const.tile([P, 8 * B, E], F32, name="r_sb")
+        rs_all = const.tile([P, 8 * B, 2], F32, name="rs_all")
+        rinv_all = const.tile([P, 8 * B], F32, name="rinv_all")
 
         k_units = [("k", b, g) for b in range(B) for g in range(2)]
         q_units = [("q", b, h) for b in range(B) for h in range(2)]
@@ -94,7 +96,7 @@ def tile_gatedcrossattention_pa_t_kernel(tc, q_scaled, k, key, query, Wv, bv, Wr
             kind = units[u][0]
             grouped = work.tile([P, 4 * E], BF16, tag="grouped", name="grouped", bufs=3, align_bytes=64)
             g32 = grouped[:].bitcast(F32).rearrange("p (r c w) -> p r c w", r=4, w=2)
-            engines = ("s", "v") if kind == "k" else ("s", "s")
+            engines = ("s", "s")
             for half in range(2):
                 copy_on(
                     engines[half],
@@ -193,7 +195,7 @@ def tile_gatedcrossattention_pa_t_kernel(tc, q_scaled, k, key, query, Wv, bv, Wr
                 return
             w, b = qk_items[m]
             dst = (qT, kT)[w][b]
-            copy_on("sv"[m % 2], dst[:], qk_ps[m][:].rearrange("p n c -> p (n c)"))
+            copy_on("s", dst[:], qk_ps[m][:].rearrange("p n c -> p (n c)"))
 
         for u in range(XIN_BUFS):
             load(u)
@@ -243,14 +245,13 @@ def tile_gatedcrossattention_pa_t_kernel(tc, q_scaled, k, key, query, Wv, bv, Wr
             for g in range(2):
                 nc.vector.tensor_reduce(out=m2[:, g : g + 1], in_=at[i]["sc"][g][:], axis=AX.X, op=ALU.max)
             negm = work.tile([P, 1], F32, tag="negm", name="negm", bufs=4)
-            nc.vector.tensor_scalar(
+            nc.gpsimd.tensor_scalar(
                 out=negm[:], in0=m2[:, 0:1], scalar1=m2[:, 1:2], scalar2=-1.0, op0=ALU.max, op1=ALU.mult
             )
             at[i]["negm"] = negm
 
         def exps(i):
             e_sb = work.tile([P, 2, 512], BF16, tag="e_sb", name="e_sb", bufs=3)
-            rs2 = work.tile([P, 2], F32, tag="rs2", name="rs2", bufs=8)
             for g in range(2):
                 nc.scalar.activation(
                     out=e_sb[:, g, :],
@@ -258,10 +259,9 @@ def tile_gatedcrossattention_pa_t_kernel(tc, q_scaled, k, key, query, Wv, bv, Wr
                     func=ACT.Exp,
                     bias=at[i]["negm"][:],
                     scale=1.0,
-                    accum_out=rs2[:, g : g + 1],
+                    accum_out=rs_all[:, i, g : g + 1],
                 )
             at[i]["e_sb"] = e_sb
-            at[i]["rs2"] = rs2
 
         def e_transpose(i):
             et = psum.tile([P, 2, 4, P], BF16, tag="aux", name="et", bufs=4)
@@ -276,8 +276,8 @@ def tile_gatedcrossattention_pa_t_kernel(tc, q_scaled, k, key, query, Wv, bv, Wr
             at[i]["eg"] = eg
 
         def e_quant(i):
-            e_codes = work.tile([P, 2 * P], U32, tag="e_codes", name="e_codes", bufs=2, align_bytes=64)
-            e_scales = work.tile([P, 2 * P], U8, tag="e_scales", name="e_scales", bufs=2, align_bytes=64)
+            e_codes = work.tile([P, 2 * P], U32, tag="e_codes", name="e_codes", bufs=3, align_bytes=64)
+            e_scales = work.tile([P, 2 * P], U8, tag="e_scales", name="e_scales", bufs=3, align_bytes=64)
             nc.vector.quantize_mx(
                 out=e_codes[:].bitcast(FP8X4),
                 scales=e_scales[:],
@@ -302,24 +302,25 @@ def tile_gatedcrossattention_pa_t_kernel(tc, q_scaled, k, key, query, Wv, bv, Wr
                 )
             at[i]["h_ps"] = h_ps
 
+        def row_sums(i0):
+            rsum = work.tile([P, 4], F32, tag="rsum", name="rsum", bufs=2)
+            nc.vector.tensor_reduce(out=rsum[:], in_=rs_all[:, i0 : i0 + 4, :], axis=AX.X, op=ALU.add)
+            nc.vector.reciprocal(out=rinv_all[:, i0 : i0 + 4], in_=rsum[:])
+
         def finish(i):
             b, h, ii = i // 8, (i % 8) // 4, i % 4
-            rsum = work.tile([P, 1], F32, tag="rsum", name="rsum", bufs=4)
-            rinv = work.tile([P, 1], F32, tag="rinv", name="rinv", bufs=4)
-            rs2 = at[i]["rs2"]
-            nc.vector.tensor_tensor(out=rsum[:], in0=rs2[:, 0:1], in1=rs2[:, 1:2], op=ALU.add)
-            nc.vector.reciprocal(out=rinv[:], in_=rsum[:])
             o_sb = work.tile([P, E], F32, tag="o_sb", name="o_sb", bufs=4)
             nc.vector.scalar_tensor_tensor(
-                out=o_sb[:], in0=at[i]["h_ps"][:], scalar=rinv[:, 0:1], in1=r_sb[:, i, :], op0=ALU.mult, op1=ALU.mult
+                out=o_sb[:], in0=at[i]["h_ps"][:], scalar=rinv_all[:, i : i + 1], in1=r_sb[:, i, :], op0=ALU.mult, op1=ALU.mult
             )
             dst = out[512 * h : 512 * h + 512, b, :].rearrange("(p i) e -> p i e", i=4)
             nc.sync.dma_start(out=dst[:, ii, :], in_=o_sb[:])
 
-        for step in range(-2, n_tiles + 3):
+        for step in range(-2, n_tiles + 4):
+            if ok(step - 3):
+                e_times_v(step - 3)
             if ok(step - 2):
                 e_quant(step - 2)
-                e_times_v(step - 2)
             if ok(step + 1):
                 rowmax(step + 1)
             if ok(step):
@@ -330,5 +331,7 @@ def tile_gatedcrossattention_pa_t_kernel(tc, q_scaled, k, key, query, Wv, bv, Wr
                 e_transpose(step)
             if ok(step - 1):
                 e_evac(step - 1)
-            if ok(step - 3):
-                finish(step - 3)
+            if ok(step) and step % 4 == 3:
+                row_sums(step - 3)
+            if ok(step - 4):
+                finish(step - 4)

@@ -157,8 +157,8 @@ def tile_gatedcrossattention_pa_t_kernel(tc, q_scaled, k, key, query, Wv, bv, Wr
             if kind == "k":
                 vg = work.tile([P, 4 * E], BF16, tag="vg", name="vg", bufs=2, align_bytes=64)
                 nc.scalar.activation(
-                    out=vg[:].rearrange("p (e j) -> p e j", j=4),
-                    in_=st[u]["y"][:].rearrange("p j e -> p e j"),
+                    out=vg[:].rearrange("p (c i j) -> p c j i", i=4, j=4),
+                    in_=st[u]["y"][:].rearrange("p j (c i) -> p c j i", i=4),
                     func=ACT.Silu,
                 )
                 st[u]["vg"] = vg
@@ -271,8 +271,20 @@ def tile_gatedcrossattention_pa_t_kernel(tc, q_scaled, k, key, query, Wv, bv, Wr
             at[i]["et"] = et
 
         def e_evac(i):
-            eg = work.tile([P, 2, P, 4], BF16, tag="eg", name="eg", bufs=3, align_bytes=64)
-            copy_on("s", eg[:], at[i]["et"][:].rearrange("p g j t -> p g t j"))
+            ec = work.tile([P, 2, 4, P], BF16, tag="ec", name="ec", bufs=3)
+            copy_on("s", ec[:], at[i]["et"][:])
+            at[i]["ec"] = ec
+
+        def e_regroup(i):
+            eg = work.tile([P, 2, P, 4], BF16, tag="eg", name="eg", bufs=1, align_bytes=64)
+            nc.gpsimd.tensor_scalar(
+                out=eg[:],
+                in0=at[i]["ec"][:].rearrange("p g j t -> p g t j"),
+                scalar1=1.0,
+                scalar2=0.0,
+                op0=ALU.mult,
+                op1=ALU.add,
+            )
             at[i]["eg"] = eg
 
         def e_quant(i):
@@ -316,11 +328,13 @@ def tile_gatedcrossattention_pa_t_kernel(tc, q_scaled, k, key, query, Wv, bv, Wr
             dst = out[512 * h : 512 * h + 512, b, :].rearrange("(p i) e -> p i e", i=4)
             nc.sync.dma_start(out=dst[:, ii, :], in_=o_sb[:])
 
-        for step in range(-2, n_tiles + 4):
+        for step in range(-2, n_tiles + 5):
+            if ok(step - 4):
+                e_times_v(step - 4)
             if ok(step - 3):
-                e_times_v(step - 3)
+                e_quant(step - 3)
             if ok(step - 2):
-                e_quant(step - 2)
+                e_regroup(step - 2)
             if ok(step + 1):
                 rowmax(step + 1)
             if ok(step):
@@ -333,5 +347,5 @@ def tile_gatedcrossattention_pa_t_kernel(tc, q_scaled, k, key, query, Wv, bv, Wr
                 e_evac(step - 1)
             if ok(step) and step % 4 == 3:
                 row_sums(step - 3)
-            if ok(step - 4):
-                finish(step - 4)
+            if ok(step - 5):
+                finish(step - 5)

@@ -18,6 +18,7 @@ FLOPS = 2 * (2 * S * B * E * E + B * T * S * Z + B * T * S * E)
 
 MANUAL = True
 XIN_BUFS = 6
+QK_LOAD_AFTER = 10
 
 
 def tile_gatedcrossattention_pa_t_kernel(tc, q_scaled, k, key, query, Wv, bv, Wr, br, out):
@@ -58,7 +59,9 @@ def tile_gatedcrossattention_pa_t_kernel(tc, q_scaled, k, key, query, Wv, bv, Wr
 
         k_units = [("k", b, g) for b in range(B) for g in range(2)]
         q_units = [("q", b, h) for b in range(B) for h in range(2)]
-        units = [("w", 0, 0)] + k_units[:6] + [("w", 1, 0)] + k_units[6:] + q_units
+        units = [("w", 0, 0), k_units[0], ("w", 1, 0)]
+        for i in range(2 * B):
+            units += ([k_units[i]] if i > 0 else []) + [q_units[i]]
         n_units = len(units)
         st = [dict() for u in range(n_units)]
 
@@ -199,12 +202,13 @@ def tile_gatedcrossattention_pa_t_kernel(tc, q_scaled, k, key, query, Wv, bv, Wr
 
         for u in range(XIN_BUFS):
             load(u)
-        nc.sync.dma_start(out=k_sb[:], in_=k.rearrange("(h p i) b z -> p h i (b z)", p=P, i=4))
-        nc.sync.dma_start(out=q_sb[:], in_=q_scaled.rearrange("(h p i) b z -> p h i (b z)", p=P, i=4))
 
         for step in range(-3, n_units + 2):
             stage_a(step + 3)
             load(step + 3 + XIN_BUFS)
+            if step + 3 + XIN_BUFS == QK_LOAD_AFTER:
+                nc.sync.dma_start(out=k_sb[:], in_=k.rearrange("(h p i) b z -> p h i (b z)", p=P, i=4))
+                nc.sync.dma_start(out=q_sb[:], in_=q_scaled.rearrange("(h p i) b z -> p h i (b z)", p=P, i=4))
             d = step - (n_units - 3)
             if d >= 0:
                 qk_transpose(2 * d)
@@ -270,43 +274,49 @@ def tile_gatedcrossattention_pa_t_kernel(tc, q_scaled, k, key, query, Wv, bv, Wr
                     nc.tensor.transpose(et[:, g, j, :], at[i]["e_sb"][:, g, j * P : (j + 1) * P], ident_b[:])
             at[i]["et"] = et
 
-        def e_evac(i):
-            ec = work.tile([P, 2, 4, P], BF16, tag="ec", name="ec", bufs=3)
-            copy_on("s", ec[:], at[i]["et"][:])
-            at[i]["ec"] = ec
+        pairs = [dict() for a in range(n_tiles // 2)]
 
-        def e_regroup(i):
-            eg = work.tile([P, 2, P, 4], BF16, tag="eg", name="eg", bufs=1, align_bytes=64)
+        def e_evac(i):
+            if i % 2 == 0:
+                ec = work.tile([P, 2, 4, P], BF16, tag="ec", name="ec", bufs=2)
+                nc.scalar.copy(out=ec[:], in_=at[i]["et"][:])
+                at[i]["ec"] = ec
+            else:
+                nc.scalar.copy(out=pairs[i // 2]["eg"][:, 1], in_=at[i]["et"][:].rearrange("p g j t -> p g t j"))
+
+        def e_regroup(i, g):
+            if g == 0:
+                eg = work.tile([P, 2, 2, P, 4], BF16, tag="eg", name="eg", bufs=2, align_bytes=64)
+                pairs[i // 2]["eg"] = eg
             nc.gpsimd.tensor_scalar(
-                out=eg[:],
-                in0=at[i]["ec"][:].rearrange("p g j t -> p g t j"),
+                out=pairs[i // 2]["eg"][:, 0, g],
+                in0=at[i]["ec"][:, g].rearrange("p j t -> p t j"),
                 scalar1=1.0,
                 scalar2=0.0,
                 op0=ALU.mult,
                 op1=ALU.add,
             )
-            at[i]["eg"] = eg
 
-        def e_quant(i):
-            e_codes = work.tile([P, 2 * P], U32, tag="e_codes", name="e_codes", bufs=3, align_bytes=64)
-            e_scales = work.tile([P, 2 * P], U8, tag="e_scales", name="e_scales", bufs=3, align_bytes=64)
+        def e_quant(a):
+            e_codes = work.tile([P, 4 * P], U32, tag="e_codes", name="e_codes", bufs=2, align_bytes=64)
+            e_scales = work.tile([P, 4 * P], U8, tag="e_scales", name="e_scales", bufs=2, align_bytes=64)
             nc.vector.quantize_mx(
                 out=e_codes[:].bitcast(FP8X4),
                 scales=e_scales[:],
-                in_=at[i]["eg"][:].rearrange("p g t j -> p (g t j)"),
+                in_=pairs[a]["eg"][:].rearrange("p a g t j -> p (a g t j)"),
             )
-            at[i]["e_codes"] = e_codes
-            at[i]["e_scales"] = e_scales
+            pairs[a]["e_codes"] = e_codes
+            pairs[a]["e_scales"] = e_scales
 
         def e_times_v(i):
             b = i // 8
             h_ps = psum.tile([P, E], F32, tag="aux", name="h_ps", bufs=4)
             for g in range(2):
-                cols = slice(g * P, (g + 1) * P)
+                cols = slice((2 * (i % 2) + g) * P, (2 * (i % 2) + g + 1) * P)
                 nc.tensor.matmul_mx(
                     out=h_ps[:],
-                    lhsT=at[i]["e_codes"][:, cols].bitcast(FP8X4),
-                    lhsT_scale=at[i]["e_scales"][:, cols],
+                    lhsT=pairs[i // 2]["e_codes"][:, cols].bitcast(FP8X4),
+                    lhsT_scale=pairs[i // 2]["e_scales"][:, cols],
                     rhs=v_codes[:, 2 * b + g, :].bitcast(FP8X4),
                     rhs_scale=v_scales[:, 2 * b + g, :],
                     start=(g == 0),
@@ -328,24 +338,27 @@ def tile_gatedcrossattention_pa_t_kernel(tc, q_scaled, k, key, query, Wv, bv, Wr
             dst = out[512 * h : 512 * h + 512, b, :].rearrange("(p i) e -> p i e", i=4)
             nc.sync.dma_start(out=dst[:, ii, :], in_=o_sb[:])
 
-        for step in range(-2, n_tiles + 5):
-            if ok(step - 4):
+        for step in range(-2, n_tiles + 6):
+            if ok(step - 5):
+                finish(step - 5)
+            if step % 2 == 0 and ok(step - 4):
                 e_times_v(step - 4)
-            if ok(step - 3):
-                e_quant(step - 3)
-            if ok(step - 2):
-                e_regroup(step - 2)
+                e_times_v(step - 3)
+            if step % 2 == 0 and ok(step - 2):
+                e_regroup(step - 2, 0)
             if ok(step + 1):
                 rowmax(step + 1)
+            if step % 2 == 0 and ok(step - 2):
+                e_regroup(step - 2, 1)
             if ok(step):
                 exps(step)
             if ok(step + 2):
                 scores(step + 2)
-            if ok(step):
-                e_transpose(step)
             if ok(step - 1):
                 e_evac(step - 1)
+            if ok(step):
+                e_transpose(step)
+            if step % 2 == 1 and ok(step - 3):
+                e_quant((step - 3) // 2)
             if ok(step) and step % 4 == 3:
                 row_sums(step - 3)
-            if ok(step - 5):
-                finish(step - 5)

@@ -38,12 +38,21 @@ def tile_gatedcrossattention_pa_t_kernel(tc, q_scaled, k, key, query, Wv, bv, Wr
 
         ident_f = const.tile([P, P], F32, name="ident_f")
         ident_b = const.tile([P, P], BF16, name="ident_b")
-        bias_v = const.tile([P, E], BF16, name="bias_v")
-        bias_r = const.tile([P, E], BF16, name="bias_r")
-        nc.gpsimd.dma_start(out=bias_v[:], in_=bv.partition_broadcast(P))
-        nc.gpsimd.dma_start(out=bias_r[:], in_=br.partition_broadcast(P))
         make_identity(nc, ident_f[:])
         make_identity(nc, ident_b[:])
+        ones = const.tile([P, P], BF16, name="ones")
+        bias_rows = const.tile([P, 2, E], BF16, name="bias_rows")
+        nc.vector.memset(ones[:], 1.0)
+        nc.vector.memset(bias_rows[:], 0.0)
+        nc.scalar.dma_start(out=bias_rows[0:1, 0, :], in_=bv.unsqueeze(0))
+        nc.scalar.dma_start(out=bias_rows[0:1, 1, :], in_=br.unsqueeze(0))
+        bias_v = const.tile([P, E], F32, name="bias_v")
+        bias_r = const.tile([P, E], F32, name="bias_r")
+
+        def spread_bias(w):
+            bias_ps = psum.tile([P, E], F32, tag="big", name="bias_ps", bufs=4)
+            nc.tensor.matmul(bias_ps[:], lhsT=ones[:], rhs=bias_rows[:, w, :], start=True, stop=True)
+            nc.vector.tensor_copy(out=(bias_v, bias_r)[w][:], in_=bias_ps[:])
 
         q_sb = const.tile([P, 2, 4, B * Z], BF16, name="q_sb")
         k_sb = const.tile([P, 2, 4, B * Z], BF16, name="k_sb")
@@ -213,6 +222,9 @@ def tile_gatedcrossattention_pa_t_kernel(tc, q_scaled, k, key, query, Wv, bv, Wr
             if d >= 0:
                 qk_transpose(2 * d)
                 qk_transpose(2 * d + 1)
+            if step == -2:
+                spread_bias(0)
+                spread_bias(1)
             stage_b(step + 1)
             stage_eva(step + 2)
             if d >= 1:

@@ -46,6 +46,8 @@ def tile_gatedcrossattention_pa_t_kernel(tc, q_scaled, k, key, query, Wv, bv, Wr
         nc.vector.memset(bias_rows[:], 0.0)
         nc.scalar.dma_start(out=bias_rows[0:1, 0, :], in_=bv.unsqueeze(0))
         nc.scalar.dma_start(out=bias_rows[0:1, 1, :], in_=br.unsqueeze(0))
+        warm = const.tile([P, 1], F32, name="warm")
+        nc.scalar.activation(out=warm[:], in_=ones[:, 0:1], func=ACT.Silu)
         bias_v = const.tile([P, E], F32, name="bias_v")
         bias_r = const.tile([P, E], F32, name="bias_r")
 
@@ -288,18 +290,25 @@ def tile_gatedcrossattention_pa_t_kernel(tc, q_scaled, k, key, query, Wv, bv, Wr
 
         pairs = [dict() for a in range(n_tiles // 2)]
 
+        def new_eg(a):
+            eg = work.tile([P, 2, 2, P, 4], BF16, tag="eg", name="eg", bufs=2, align_bytes=64)
+            pairs[a]["eg"] = eg
+
         def e_evac(i):
-            if i % 2 == 0:
+            if i % 2 == 0 and i < n_tiles - 2:
                 ec = work.tile([P, 2, 4, P], BF16, tag="ec", name="ec", bufs=2)
                 nc.scalar.copy(out=ec[:], in_=at[i]["et"][:])
                 at[i]["ec"] = ec
             else:
-                nc.scalar.copy(out=pairs[i // 2]["eg"][:, 1], in_=at[i]["et"][:].rearrange("p g j t -> p g t j"))
+                if i % 2 == 0:
+                    new_eg(i // 2)
+                copy_on(
+                    "sv"[1 - i % 2], pairs[i // 2]["eg"][:, i % 2], at[i]["et"][:].rearrange("p g j t -> p g t j")
+                )
 
         def e_regroup(i, g):
             if g == 0:
-                eg = work.tile([P, 2, 2, P, 4], BF16, tag="eg", name="eg", bufs=2, align_bytes=64)
-                pairs[i // 2]["eg"] = eg
+                new_eg(i // 2)
             nc.gpsimd.tensor_scalar(
                 out=pairs[i // 2]["eg"][:, 0, g],
                 in0=at[i]["ec"][:, g].rearrange("p j t -> p t j"),
@@ -309,16 +318,30 @@ def tile_gatedcrossattention_pa_t_kernel(tc, q_scaled, k, key, query, Wv, bv, Wr
                 op1=ALU.add,
             )
 
-        def e_quant(a):
+        def new_codes(a):
             e_codes = work.tile([P, 4 * P], U32, tag="e_codes", name="e_codes", bufs=2, align_bytes=64)
             e_scales = work.tile([P, 4 * P], U8, tag="e_scales", name="e_scales", bufs=2, align_bytes=64)
-            nc.vector.quantize_mx(
-                out=e_codes[:].bitcast(FP8X4),
-                scales=e_scales[:],
-                in_=pairs[a]["eg"][:].rearrange("p a g t j -> p (a g t j)"),
-            )
             pairs[a]["e_codes"] = e_codes
             pairs[a]["e_scales"] = e_scales
+
+        def e_quant(a):
+            new_codes(a)
+            nc.vector.quantize_mx(
+                out=pairs[a]["e_codes"][:].bitcast(FP8X4),
+                scales=pairs[a]["e_scales"][:],
+                in_=pairs[a]["eg"][:].rearrange("p a g t j -> p (a g t j)"),
+            )
+
+        def e_quant_one(i):
+            a = i // 2
+            if i % 2 == 0:
+                new_codes(a)
+            cols = slice((i % 2) * 2 * P, (i % 2 + 1) * 2 * P)
+            nc.vector.quantize_mx(
+                out=pairs[a]["e_codes"][:, cols].bitcast(FP8X4),
+                scales=pairs[a]["e_scales"][:, cols],
+                in_=pairs[a]["eg"][:, i % 2].rearrange("p g t j -> p (g t j)"),
+            )
 
         def e_times_v(i):
             b = i // 8
@@ -350,7 +373,7 @@ def tile_gatedcrossattention_pa_t_kernel(tc, q_scaled, k, key, query, Wv, bv, Wr
             dst = out[512 * h : 512 * h + 512, b, :].rearrange("(p i) e -> p i e", i=4)
             nc.sync.dma_start(out=dst[:, ii, :], in_=o_sb[:])
 
-        for step in range(-2, n_tiles + 6):
+        for step in range(-2, n_tiles):
             if ok(step - 5):
                 finish(step - 5)
             if step % 2 == 0 and ok(step - 4):
@@ -374,3 +397,17 @@ def tile_gatedcrossattention_pa_t_kernel(tc, q_scaled, k, key, query, Wv, bv, Wr
                 e_quant((step - 3) // 2)
             if ok(step) and step % 4 == 3:
                 row_sums(step - 3)
+
+        n = n_tiles
+        finish(n - 5)
+        e_times_v(n - 4)
+        e_times_v(n - 3)
+        e_quant_one(n - 2)
+        e_evac(n - 1)
+        e_times_v(n - 2)
+        finish(n - 4)
+        e_quant_one(n - 1)
+        e_times_v(n - 1)
+        finish(n - 3)
+        finish(n - 2)
+        finish(n - 1)

@@ -209,7 +209,14 @@ def tile_gatedcrossattention_pa_t_kernel(tc, q_scaled, k, key, query, Wv, bv, Wr
                 return
             w, b = qk_items[m]
             dst = (qT, kT)[w][b]
-            copy_on("s", dst[:], qk_ps[m][:].rearrange("p n c -> p (n c)"))
+            if w == 0:
+                copy_on("s", dst[:], qk_ps[m][:].rearrange("p n c -> p (n c)"))
+            else:
+                copy_on(
+                    "s",
+                    dst[:].rearrange("z (x p e) -> z x p e", x=4, e=2),
+                    qk_ps[m][:].rearrange("z (x e) p -> z x p e", e=2),
+                )
 
         for u in range(XIN_BUFS):
             load(u)
@@ -282,41 +289,21 @@ def tile_gatedcrossattention_pa_t_kernel(tc, q_scaled, k, key, query, Wv, bv, Wr
             at[i]["e_sb"] = e_sb
 
         def e_transpose(i):
-            et = psum.tile([P, 2, 4, P], BF16, tag="aux", name="et", bufs=4)
+            et = psum.tile([P, 2, 2, P], F32, tag="aux", name="et", bufs=4)
             for g in range(2):
-                for j in range(4):
-                    nc.tensor.transpose(et[:, g, j, :], at[i]["e_sb"][:, g, j * P : (j + 1) * P], ident_b[:])
+                words = at[i]["e_sb"][:, g, :].bitcast(F32)
+                for u in range(2):
+                    nc.tensor.transpose(et[:, g, u, :], words[:, u * P : (u + 1) * P], ident_f[:])
             at[i]["et"] = et
 
         pairs = [dict() for a in range(n_tiles // 2)]
 
-        def new_eg(a):
-            eg = work.tile([P, 2, 2, P, 4], BF16, tag="eg", name="eg", bufs=2, align_bytes=64)
-            pairs[a]["eg"] = eg
-
         def e_evac(i):
-            if i % 2 == 0 and i < n_tiles - 2:
-                ec = work.tile([P, 2, 4, P], BF16, tag="ec", name="ec", bufs=2)
-                nc.scalar.copy(out=ec[:], in_=at[i]["et"][:])
-                at[i]["ec"] = ec
-            else:
-                if i % 2 == 0:
-                    new_eg(i // 2)
-                copy_on(
-                    "sv"[1 - i % 2], pairs[i // 2]["eg"][:, i % 2], at[i]["et"][:].rearrange("p g j t -> p g t j")
-                )
-
-        def e_regroup(i, g):
-            if g == 0:
-                new_eg(i // 2)
-            nc.gpsimd.tensor_scalar(
-                out=pairs[i // 2]["eg"][:, 0, g],
-                in0=at[i]["ec"][:, g].rearrange("p j t -> p t j"),
-                scalar1=1.0,
-                scalar2=0.0,
-                op0=ALU.mult,
-                op1=ALU.add,
-            )
+            if i % 2 == 0:
+                eg = work.tile([P, 2, 2, P, 4], BF16, tag="eg", name="eg", bufs=2, align_bytes=64)
+                pairs[i // 2]["eg"] = eg
+            dst = pairs[i // 2]["eg"][:, i % 2].rearrange("p g t j -> p (g t j)").bitcast(F32)
+            copy_on("s", dst.rearrange("p (g t u) -> p g t u", g=2, u=2), at[i]["et"][:].rearrange("p g u t -> p g t u"))
 
         def new_codes(a):
             e_codes = work.tile([P, 4 * P], U32, tag="e_codes", name="e_codes", bufs=2, align_bytes=64)
@@ -379,12 +366,8 @@ def tile_gatedcrossattention_pa_t_kernel(tc, q_scaled, k, key, query, Wv, bv, Wr
             if step % 2 == 0 and ok(step - 4):
                 e_times_v(step - 4)
                 e_times_v(step - 3)
-            if step % 2 == 0 and ok(step - 2):
-                e_regroup(step - 2, 0)
             if ok(step + 1):
                 rowmax(step + 1)
-            if step % 2 == 0 and ok(step - 2):
-                e_regroup(step - 2, 1)
             if ok(step):
                 exps(step)
             if ok(step + 2):

@@ -17,8 +17,8 @@ T, S, B, E, Z = 1024, 1024, 4, 512, 128
 FLOPS = 2 * (2 * S * B * E * E + B * T * S * Z + B * T * S * E)
 
 MANUAL = True
-XIN_BUFS = 6
-QK_LOAD_AFTER = 10
+XIN_BUFS = 10
+QK_LOAD_AFTER = 5
 
 
 def tile_gatedcrossattention_pa_t_kernel(tc, q_scaled, k, key, query, Wv, bv, Wr, br, out):
@@ -41,20 +41,25 @@ def tile_gatedcrossattention_pa_t_kernel(tc, q_scaled, k, key, query, Wv, bv, Wr
         make_identity(nc, ident_f[:])
         make_identity(nc, ident_b[:])
         ones = const.tile([P, P], BF16, name="ones")
-        bias_rows = const.tile([P, 2, E], BF16, name="bias_rows")
+        bias_rows = const.tile([P, E], BF16, name="bias_rows")
+        bv_rows = const.tile([P, P], BF16, name="bv_rows")
         nc.vector.memset(ones[:], 1.0)
         nc.vector.memset(bias_rows[:], 0.0)
-        nc.scalar.dma_start(out=bias_rows[0:1, 0, :], in_=bv.unsqueeze(0))
-        nc.scalar.dma_start(out=bias_rows[0:1, 1, :], in_=br.unsqueeze(0))
+        nc.vector.memset(bv_rows[:], 0.0)
+        nc.scalar.dma_start(out=bv_rows[0:4, :], in_=bv.rearrange("(j p) -> j p", p=P))
+        nc.scalar.dma_start(out=bias_rows[0:1, :], in_=br.unsqueeze(0))
         warm = const.tile([P, 1], F32, name="warm")
         nc.scalar.activation(out=warm[:], in_=ones[:, 0:1], func=ACT.Silu)
-        bias_v = const.tile([P, E], F32, name="bias_v")
         bias_r = const.tile([P, E], F32, name="bias_r")
+        bias_v = const.tile([P, 4], F32, name="bias_v")
 
-        def spread_bias(w):
-            bias_ps = psum.tile([P, E], F32, tag="big", name="bias_ps", bufs=4)
-            nc.tensor.matmul(bias_ps[:], lhsT=ones[:], rhs=bias_rows[:, w, :], start=True, stop=True)
-            nc.vector.tensor_copy(out=(bias_v, bias_r)[w][:], in_=bias_ps[:])
+        def spread_biases():
+            bv_ps = psum.tile([P, P], BF16, tag="big", name="bv_ps", bufs=4)
+            nc.tensor.transpose(bv_ps[:], bv_rows[:], ident_b[:])
+            nc.vector.tensor_copy(out=bias_v[:], in_=bv_ps[:, 0:4])
+            br_ps = psum.tile([P, E], F32, tag="big", name="br_ps", bufs=4)
+            nc.tensor.matmul(br_ps[:], lhsT=ones[:], rhs=bias_rows[:], start=True, stop=True)
+            nc.vector.tensor_copy(out=bias_r[:], in_=br_ps[:])
 
         q_sb = const.tile([P, 2, 4, B * Z], BF16, name="q_sb")
         k_sb = const.tile([P, 2, 4, B * Z], BF16, name="k_sb")
@@ -90,36 +95,36 @@ def tile_gatedcrossattention_pa_t_kernel(tc, q_scaled, k, key, query, Wv, bv, Wr
             nc.sync.dma_start(out=xin[:], in_=src)
             st[u]["xin"] = xin
 
-        def stage_a(u):
-            if u < 0 or u >= n_units:
+        def is_kind(u, kind):
+            return 0 <= u < n_units and units[u][0] == kind
+
+        def x_transpose(u):
+            if u >= n_units:
                 return
             xin = st[u]["xin"]
-            tps = []
+            st[u]["tps"] = []
             for half in range(2):
                 tp = psum.tile([P, 2, 2, P], F32, tag="aux", name="tp", bufs=4)
                 for r in range(2):
                     words = xin[:, 2 * half + r, :].bitcast(F32)
                     for w in range(2):
                         nc.tensor.transpose(tp[:, r, w, :], words[:, w * P : (w + 1) * P], ident_f[:])
-                tps.append(tp)
-            st[u]["tps"] = tps
+                st[u]["tps"].append(tp)
 
-        def stage_eva(u):
-            if u < 0 or u >= n_units:
+        def x_evac(u, half, eng):
+            if u >= n_units:
                 return
-            kind = units[u][0]
-            grouped = work.tile([P, 4 * E], BF16, tag="grouped", name="grouped", bufs=3, align_bytes=64)
-            g32 = grouped[:].bitcast(F32).rearrange("p (r c w) -> p r c w", r=4, w=2)
-            engines = ("s", "s")
-            for half in range(2):
-                copy_on(
-                    engines[half],
-                    g32[:, 2 * half : 2 * half + 2, :, :],
-                    st[u]["tps"][half][:].rearrange("p r w c -> p r c w"),
-                )
-            st[u]["grouped"] = grouped
+            if half == 0:
+                grouped = work.tile([P, 4 * E], BF16, tag="grouped", name="grouped", bufs=3, align_bytes=64)
+                st[u]["grouped"] = grouped
+            words = st[u]["grouped"][:].bitcast(F32)[:, half * E : (half + 1) * E]
+            tp = st[u]["tps"][half]
+            if units[u][0] == "k":
+                copy_on(eng, words.rearrange("p (c r w) -> p c r w", r=2, w=2), tp[:].rearrange("p r w c -> p c r w"))
+            else:
+                copy_on(eng, words.rearrange("p (r c w) -> p r c w", r=2, w=2), tp[:].rearrange("p r w c -> p r c w"))
 
-        def stage_b(u):
+        def x_quant(u):
             if u < 0 or u >= n_units:
                 return
             kind, a, c = units[u]
@@ -132,56 +137,60 @@ def tile_gatedcrossattention_pa_t_kernel(tc, q_scaled, k, key, query, Wv, bv, Wr
             st[u]["codes"] = codes
             st[u]["scales"] = scales
 
-        def stage_c(u, j):
-            if u < 0 or u >= n_units or units[u][0] == "w":
+        def project(u, j):
+            if not (is_kind(u, "k") or is_kind(u, "q")):
                 return
-            w = 0 if units[u][0] == "k" else 1
             pj = psum.tile([P, E], F32, tag="big", name="pj", bufs=4)
             cols = slice(j * P, (j + 1) * P)
+            x = (st[u]["codes"], st[u]["scales"])
+            w = (w_codes[0], w_scales[0]) if units[u][0] == "k" else (w_codes[1], w_scales[1])
+            sta, mov = (w, x) if units[u][0] == "k" else (x, w)
             nc.tensor.matmul_mx(
                 out=pj[:],
-                lhsT=st[u]["codes"][:, cols].bitcast(FP8X4),
-                lhsT_scale=st[u]["scales"][:, cols],
-                rhs=w_codes[w][:].bitcast(FP8X4),
-                rhs_scale=w_scales[w][:],
+                lhsT=sta[0][:, cols].bitcast(FP8X4),
+                lhsT_scale=sta[1][:, cols],
+                rhs=mov[0][:].bitcast(FP8X4),
+                rhs_scale=mov[1][:],
                 start=True,
                 stop=True,
             )
             st[u]["pj%d" % j] = pj
 
-        def stage_d(u, j):
-            if u < 0 or u >= n_units or units[u][0] == "w":
-                return
-            kind, a, c = units[u]
-            if kind == "k":
-                if j == 0:
-                    y = work.tile([P, 4, E], F32, tag="y", name="y", bufs=2)
-                    st[u]["y"] = y
-                dst = st[u]["y"][:, j, :]
-                bias = bias_v
-            else:
-                dst = r_sb[:, 4 * (2 * a + c) + j, :]
-                bias = bias_r
-            nc.vector.tensor_tensor(out=dst, in0=st[u]["pj%d" % j][:], in1=bias[:], op=ALU.add)
+        def key_silu(u, j):
+            if j == 0:
+                yT = work.tile([P, 4, E], BF16, tag="yT", name="yT", bufs=2)
+                st[u]["yT"] = yT
+            nc.scalar.activation(
+                out=st[u]["yT"][:, j, :], in_=st[u]["pj%d" % j][:], func=ACT.Silu, bias=bias_v[:, j : j + 1], scale=1.0
+            )
 
-        def stage_e(u):
-            if u < 0 or u >= n_units or units[u][0] == "w":
+        def v_transpose(u):
+            if not is_kind(u, "k"):
                 return
-            kind, a, c = units[u]
-            if kind == "k":
+            st[u]["vps"] = []
+            for half in range(2):
+                vp = psum.tile([P, 2, 2, P], F32, tag="aux", name="vp", bufs=4)
+                for jj in range(2):
+                    words = st[u]["yT"][:, 2 * half + jj, :].bitcast(F32)
+                    for w in range(2):
+                        nc.tensor.transpose(vp[:, jj, w, :], words[:, w * P : (w + 1) * P], ident_f[:])
+                st[u]["vps"].append(vp)
+
+        def v_evac(u, half, eng):
+            if not is_kind(u, "k"):
+                return
+            if half == 0:
                 vg = work.tile([P, 4 * E], BF16, tag="vg", name="vg", bufs=2, align_bytes=64)
-                nc.scalar.activation(
-                    out=vg[:].rearrange("p (c i j) -> p c j i", i=4, j=4),
-                    in_=st[u]["y"][:].rearrange("p j (c i) -> p c j i", i=4),
-                    func=ACT.Silu,
-                )
                 st[u]["vg"] = vg
-            else:
-                rr = r_sb[:, 4 * (2 * a + c) : 4 * (2 * a + c) + 4, :]
-                nc.scalar.activation(out=rr, in_=rr, func=ACT.Silu)
+            words = st[u]["vg"][:].bitcast(F32)[:, half * E : (half + 1) * E]
+            copy_on(
+                eng,
+                words.rearrange("p (j c w) -> p j c w", j=2, w=2),
+                st[u]["vps"][half][:].rearrange("p j w c -> p j c w"),
+            )
 
-        def stage_f(u):
-            if u < 0 or u >= n_units or units[u][0] != "k":
+        def v_quant(u):
+            if not is_kind(u, "k"):
                 return
             kind, a, c = units[u]
             nc.vector.quantize_mx(
@@ -189,6 +198,20 @@ def tile_gatedcrossattention_pa_t_kernel(tc, q_scaled, k, key, query, Wv, bv, Wr
                 scales=v_scales[:, 2 * a + c, :],
                 in_=st[u]["vg"][:],
             )
+
+        def query_add(u, j):
+            kind, a, c = units[u]
+            nc.vector.tensor_tensor(
+                out=r_sb[:, 4 * (2 * a + c) + j, :], in0=st[u]["pj%d" % j][:], in1=bias_r[:], op=ALU.add
+            )
+
+        def query_silu(u, half):
+            if not is_kind(u, "q"):
+                return
+            kind, a, c = units[u]
+            i0 = 4 * (2 * a + c) + 2 * half
+            rr = r_sb[:, i0 : i0 + 2, :]
+            nc.scalar.activation(out=rr, in_=rr, func=ACT.Silu)
 
         qk_items = [(w, b) for b in range(B) for w in (1, 0)]
         qk_ps = dict()
@@ -210,40 +233,61 @@ def tile_gatedcrossattention_pa_t_kernel(tc, q_scaled, k, key, query, Wv, bv, Wr
             w, b = qk_items[m]
             dst = (qT, kT)[w][b]
             if w == 0:
-                copy_on("s", dst[:], qk_ps[m][:].rearrange("p n c -> p (n c)"))
+                copy_on("v", dst[:], qk_ps[m][:].rearrange("p n c -> p (n c)"))
             else:
                 copy_on(
-                    "s",
+                    "v",
                     dst[:].rearrange("z (x p e) -> z x p e", x=4, e=2),
                     qk_ps[m][:].rearrange("z (x e) p -> z x p e", e=2),
                 )
 
         for u in range(XIN_BUFS):
             load(u)
-
-        for step in range(-3, n_units + 2):
-            stage_a(step + 3)
-            load(step + 3 + XIN_BUFS)
-            if step + 3 + XIN_BUFS == QK_LOAD_AFTER:
+            if u == QK_LOAD_AFTER:
                 nc.sync.dma_start(out=k_sb[:], in_=k.rearrange("(h p i) b z -> p h i (b z)", p=P, i=4))
                 nc.sync.dma_start(out=q_sb[:], in_=q_scaled.rearrange("(h p i) b z -> p h i (b z)", p=P, i=4))
-            d = step - (n_units - 3)
-            if d >= 0:
-                qk_transpose(2 * d)
-                qk_transpose(2 * d + 1)
-            if step == -2:
-                spread_bias(0)
-                spread_bias(1)
-            stage_b(step + 1)
-            stage_eva(step + 2)
-            if d >= 1:
-                qk_evac(2 * d - 2)
-                qk_evac(2 * d - 1)
-            for j in range(4):
-                stage_d(step, j)
-                stage_c(step + 1, j)
-            stage_e(step - 1)
-            stage_f(step - 2)
+
+        qk_at = {6: 0, 8: 1, 10: 2, 12: 3, 14: 4, 16: 5, 18: 6, 19: 7}
+        for step in range(-2, n_units + 2):
+            x_transpose(step + 2)
+            load(step + 2 + XIN_BUFS)
+            if step == -1:
+                spread_biases()
+            x_quant(step + 1)
+            m = qk_at.get(step, -1)
+            qk_transpose(m)
+            if is_kind(step, "k"):
+                for j in range(4):
+                    key_silu(step, j)
+                    project(step + 1, j)
+                x_evac(step + 2, 0, "v")
+                x_evac(step + 2, 1, "v")
+                v_quant(step - 2)
+                query_silu(step - 1, 1)
+                qk_evac(m)
+            elif is_kind(step, "q"):
+                v_transpose(step - 1)
+                x_evac(step + 2, 0, "s")
+                x_evac(step + 2, 1, "s")
+                v_evac(step - 1, 0, "s")
+                for j in range(4):
+                    if j == 2:
+                        v_evac(step - 1, 1, "v")
+                    query_add(step, j)
+                    project(step + 1, j)
+                v_quant(step - 2)
+                query_silu(step, 0)
+            else:
+                v_transpose(step - 1)
+                x_evac(step + 2, 0, "s")
+                x_evac(step + 2, 1, "v")
+                v_evac(step - 1, 0, "s")
+                v_evac(step - 1, 1, "v")
+                for j in range(4):
+                    project(step + 1, j)
+                v_quant(step - 2)
+                query_silu(step - 1, 1)
+                qk_evac(m)
 
         n_tiles = 8 * B
         at = [dict() for i in range(n_tiles)]

@@ -26,15 +26,29 @@ def tile_gatedcrossattention_pa_t_kernel(tc, q_scaled, k, key, query, Wv, bv, Wr
     with ExitStack() as ctx:
         const = ctx.enter_context(tc.tile_pool(name="const", bufs=1))
         work = ctx.enter_context(tc.tile_pool(name="work", bufs=2))
-        psum = ctx.enter_context(tc.psum_pool(name="psum", bufs=4))
+        psum = ctx.enter_context(tc.psum_pool(name="psum", bufs=1))
         if MANUAL:
             ctx.enter_context(tc.manual_schedule())
+
+        def ring(banks):
+            taken = []
+
+            def take(shape, dtype, name):
+                b = banks[len(taken) % len(banks)]
+                taken.append(b)
+                bank = psum.tile(shape, dtype, tag="bank%d" % b, name=name, bufs=1)
+                return bank
+
+            return take
 
         def copy_on(eng, dst, src):
             if eng == "v":
                 nc.vector.tensor_copy(out=dst, in_=src)
             else:
                 nc.scalar.copy(out=dst, in_=src)
+
+        big = ring([0, 1, 2, 3])
+        aux = ring([4, 5, 6, 7])
 
         ident_f = const.tile([P, P], F32, name="ident_f")
         ident_b = const.tile([P, P], BF16, name="ident_b")
@@ -54,10 +68,10 @@ def tile_gatedcrossattention_pa_t_kernel(tc, q_scaled, k, key, query, Wv, bv, Wr
         bias_v = const.tile([P, 4], F32, name="bias_v")
 
         def spread_biases():
-            bv_ps = psum.tile([P, P], BF16, tag="big", name="bv_ps", bufs=4)
+            bv_ps = big([P, P], BF16, "bv_ps")
             nc.tensor.transpose(bv_ps[:], bv_rows[:], ident_b[:])
             nc.vector.tensor_copy(out=bias_v[:], in_=bv_ps[:, 0:4])
-            br_ps = psum.tile([P, E], F32, tag="big", name="br_ps", bufs=4)
+            br_ps = big([P, E], F32, "br_ps")
             nc.tensor.matmul(br_ps[:], lhsT=ones[:], rhs=bias_rows[:], start=True, stop=True)
             nc.vector.tensor_copy(out=bias_r[:], in_=br_ps[:])
 
@@ -92,7 +106,10 @@ def tile_gatedcrossattention_pa_t_kernel(tc, q_scaled, k, key, query, Wv, bv, Wr
                 src = (key if kind == "k" else query)[512 * c : 512 * c + 512, a, :].rearrange(
                     "(p j) e -> p j e", j=4
                 )
-            nc.sync.dma_start(out=xin[:], in_=src)
+            pieces = 4 if u == 0 else 2 if u == 1 else 1
+            n = 4 // pieces
+            for i in range(pieces):
+                nc.sync.dma_start(out=xin[:, i * n : (i + 1) * n, :], in_=src[:, i * n : (i + 1) * n, :])
             st[u]["xin"] = xin
 
         def is_kind(u, kind):
@@ -104,7 +121,7 @@ def tile_gatedcrossattention_pa_t_kernel(tc, q_scaled, k, key, query, Wv, bv, Wr
             xin = st[u]["xin"]
             st[u]["tps"] = []
             for half in range(2):
-                tp = psum.tile([P, 2, 2, P], F32, tag="aux", name="tp", bufs=4)
+                tp = aux([P, 2, 2, P], F32, "tp")
                 for r in range(2):
                     words = xin[:, 2 * half + r, :].bitcast(F32)
                     for w in range(2):
@@ -140,7 +157,7 @@ def tile_gatedcrossattention_pa_t_kernel(tc, q_scaled, k, key, query, Wv, bv, Wr
         def project(u, j):
             if not (is_kind(u, "k") or is_kind(u, "q")):
                 return
-            pj = psum.tile([P, E], F32, tag="big", name="pj", bufs=4)
+            pj = big([P, E], F32, "pj")
             cols = slice(j * P, (j + 1) * P)
             x = (st[u]["codes"], st[u]["scales"])
             w = (w_codes[0], w_scales[0]) if units[u][0] == "k" else (w_codes[1], w_scales[1])
@@ -169,7 +186,7 @@ def tile_gatedcrossattention_pa_t_kernel(tc, q_scaled, k, key, query, Wv, bv, Wr
                 return
             st[u]["vps"] = []
             for half in range(2):
-                vp = psum.tile([P, 2, 2, P], F32, tag="aux", name="vp", bufs=4)
+                vp = aux([P, 2, 2, P], F32, "vp")
                 for jj in range(2):
                     words = st[u]["yT"][:, 2 * half + jj, :].bitcast(F32)
                     for w in range(2):
@@ -221,7 +238,7 @@ def tile_gatedcrossattention_pa_t_kernel(tc, q_scaled, k, key, query, Wv, bv, Wr
                 return
             w, b = qk_items[m]
             src = (q_sb, k_sb)[w]
-            tq = psum.tile([P, 8, P], BF16, tag="aux", name="tq", bufs=4)
+            tq = aux([P, 8, P], BF16, "tq")
             for h in range(2):
                 for i in range(4):
                     nc.tensor.transpose(tq[:, 4 * h + i, :], src[:, h, i, b * Z : (b + 1) * Z], ident_b[:])
@@ -247,16 +264,16 @@ def tile_gatedcrossattention_pa_t_kernel(tc, q_scaled, k, key, query, Wv, bv, Wr
                 nc.sync.dma_start(out=k_sb[:], in_=k.rearrange("(h p i) b z -> p h i (b z)", p=P, i=4))
                 nc.sync.dma_start(out=q_sb[:], in_=q_scaled.rearrange("(h p i) b z -> p h i (b z)", p=P, i=4))
 
-        qk_at = {6: 0, 8: 1, 10: 2, 12: 3, 14: 4, 16: 5, 18: 6, 19: 7}
-        for step in range(-2, n_units + 2):
+        qk_at = {6: [0], 8: [1], 10: [2], 12: [3], 14: [4], 16: [5, 6], 17: [7]}
+        for step in range(-2, n_units):
             x_transpose(step + 2)
             load(step + 2 + XIN_BUFS)
-            if step == -1:
-                spread_biases()
             x_quant(step + 1)
-            m = qk_at.get(step, -1)
-            qk_transpose(m)
+            if step == 0:
+                spread_biases()
             if is_kind(step, "k"):
+                for m in qk_at.get(step, []):
+                    qk_transpose(m)
                 for j in range(4):
                     key_silu(step, j)
                     project(step + 1, j)
@@ -264,12 +281,15 @@ def tile_gatedcrossattention_pa_t_kernel(tc, q_scaled, k, key, query, Wv, bv, Wr
                 x_evac(step + 2, 1, "v")
                 v_quant(step - 2)
                 query_silu(step - 1, 1)
-                qk_evac(m)
+                for m in qk_at.get(step, []):
+                    qk_evac(m)
             elif is_kind(step, "q"):
                 v_transpose(step - 1)
                 x_evac(step + 2, 0, "s")
                 x_evac(step + 2, 1, "s")
                 v_evac(step - 1, 0, "s")
+                for m in qk_at.get(step, []):
+                    qk_transpose(m)
                 for j in range(4):
                     if j == 2:
                         v_evac(step - 1, 1, "v")
@@ -277,6 +297,8 @@ def tile_gatedcrossattention_pa_t_kernel(tc, q_scaled, k, key, query, Wv, bv, Wr
                     project(step + 1, j)
                 v_quant(step - 2)
                 query_silu(step, 0)
+                for m in qk_at.get(step, []):
+                    qk_evac(m)
             else:
                 v_transpose(step - 1)
                 x_evac(step + 2, 0, "s")
@@ -285,11 +307,11 @@ def tile_gatedcrossattention_pa_t_kernel(tc, q_scaled, k, key, query, Wv, bv, Wr
                 v_evac(step - 1, 1, "v")
                 for j in range(4):
                     project(step + 1, j)
-                v_quant(step - 2)
-                query_silu(step - 1, 1)
-                qk_evac(m)
 
         n_tiles = 8 * B
+        sc_ring = ring([0, 1, 2, 3, 4, 5])
+        et_ring = ring([6])
+        h_ring = ring([7])
         at = [dict() for i in range(n_tiles)]
 
         def ok(i):
@@ -299,7 +321,7 @@ def tile_gatedcrossattention_pa_t_kernel(tc, q_scaled, k, key, query, Wv, bv, Wr
             b, n = i // 8, i % 8
             at[i]["sc"] = []
             for g in range(2):
-                sc = psum.tile([P, 512], F32, tag="big", name="sc", bufs=4)
+                sc = sc_ring([P, 512], F32, "sc")
                 nc.tensor.matmul(
                     sc[:],
                     lhsT=qT[b][:, n * P : (n + 1) * P],
@@ -333,56 +355,39 @@ def tile_gatedcrossattention_pa_t_kernel(tc, q_scaled, k, key, query, Wv, bv, Wr
             at[i]["e_sb"] = e_sb
 
         def e_transpose(i):
-            et = psum.tile([P, 2, 2, P], F32, tag="aux", name="et", bufs=4)
+            et = et_ring([P, 2, 2, P], F32, "et")
             for g in range(2):
                 words = at[i]["e_sb"][:, g, :].bitcast(F32)
                 for u in range(2):
                     nc.tensor.transpose(et[:, g, u, :], words[:, u * P : (u + 1) * P], ident_f[:])
             at[i]["et"] = et
 
-        pairs = [dict() for a in range(n_tiles // 2)]
-
         def e_evac(i):
-            if i % 2 == 0:
-                eg = work.tile([P, 2, 2, P, 4], BF16, tag="eg", name="eg", bufs=2, align_bytes=64)
-                pairs[i // 2]["eg"] = eg
-            dst = pairs[i // 2]["eg"][:, i % 2].rearrange("p g t j -> p (g t j)").bitcast(F32)
+            eg = work.tile([P, 2, P, 4], BF16, tag="eg", name="eg", bufs=3, align_bytes=64)
+            at[i]["eg"] = eg
+            dst = eg[:].rearrange("p g t j -> p (g t j)").bitcast(F32)
             copy_on("s", dst.rearrange("p (g t u) -> p g t u", g=2, u=2), at[i]["et"][:].rearrange("p g u t -> p g t u"))
 
-        def new_codes(a):
-            e_codes = work.tile([P, 4 * P], U32, tag="e_codes", name="e_codes", bufs=2, align_bytes=64)
-            e_scales = work.tile([P, 4 * P], U8, tag="e_scales", name="e_scales", bufs=2, align_bytes=64)
-            pairs[a]["e_codes"] = e_codes
-            pairs[a]["e_scales"] = e_scales
-
-        def e_quant(a):
-            new_codes(a)
+        def e_quant(i):
+            e_codes = work.tile([P, 2 * P], U32, tag="e_codes", name="e_codes", bufs=3, align_bytes=64)
+            e_scales = work.tile([P, 2 * P], U8, tag="e_scales", name="e_scales", bufs=3, align_bytes=64)
             nc.vector.quantize_mx(
-                out=pairs[a]["e_codes"][:].bitcast(FP8X4),
-                scales=pairs[a]["e_scales"][:],
-                in_=pairs[a]["eg"][:].rearrange("p a g t j -> p (a g t j)"),
+                out=e_codes[:].bitcast(FP8X4),
+                scales=e_scales[:],
+                in_=at[i]["eg"][:].rearrange("p g t j -> p (g t j)"),
             )
-
-        def e_quant_one(i):
-            a = i // 2
-            if i % 2 == 0:
-                new_codes(a)
-            cols = slice((i % 2) * 2 * P, (i % 2 + 1) * 2 * P)
-            nc.vector.quantize_mx(
-                out=pairs[a]["e_codes"][:, cols].bitcast(FP8X4),
-                scales=pairs[a]["e_scales"][:, cols],
-                in_=pairs[a]["eg"][:, i % 2].rearrange("p g t j -> p (g t j)"),
-            )
+            at[i]["e_codes"] = e_codes
+            at[i]["e_scales"] = e_scales
 
         def e_times_v(i):
             b = i // 8
-            h_ps = psum.tile([P, E], F32, tag="aux", name="h_ps", bufs=4)
+            h_ps = h_ring([P, E], F32, "h_ps")
             for g in range(2):
-                cols = slice((2 * (i % 2) + g) * P, (2 * (i % 2) + g + 1) * P)
+                cols = slice(g * P, (g + 1) * P)
                 nc.tensor.matmul_mx(
                     out=h_ps[:],
-                    lhsT=pairs[i // 2]["e_codes"][:, cols].bitcast(FP8X4),
-                    lhsT_scale=pairs[i // 2]["e_scales"][:, cols],
+                    lhsT=at[i]["e_codes"][:, cols].bitcast(FP8X4),
+                    lhsT_scale=at[i]["e_scales"][:, cols],
                     rhs=v_codes[:, 2 * b + g, :].bitcast(FP8X4),
                     rhs_scale=v_scales[:, 2 * b + g, :],
                     start=(g == 0),
@@ -391,9 +396,11 @@ def tile_gatedcrossattention_pa_t_kernel(tc, q_scaled, k, key, query, Wv, bv, Wr
             at[i]["h_ps"] = h_ps
 
         def row_sums(i0):
-            rsum = work.tile([P, 4], F32, tag="rsum", name="rsum", bufs=2)
-            nc.vector.tensor_reduce(out=rsum[:], in_=rs_all[:, i0 : i0 + 4, :], axis=AX.X, op=ALU.add)
-            nc.vector.reciprocal(out=rinv_all[:, i0 : i0 + 4], in_=rsum[:])
+            rsum = work.tile([P, 2], F32, tag="rsum", name="rsum", bufs=2)
+            nc.gpsimd.tensor_tensor(
+                out=rsum[:], in0=rs_all[:, i0 : i0 + 2, 0], in1=rs_all[:, i0 : i0 + 2, 1], op=ALU.add
+            )
+            nc.vector.reciprocal(out=rinv_all[:, i0 : i0 + 2], in_=rsum[:])
 
         def finish(i):
             b, h, ii = i // 8, (i % 8) // 4, i % 4
@@ -404,37 +411,29 @@ def tile_gatedcrossattention_pa_t_kernel(tc, q_scaled, k, key, query, Wv, bv, Wr
             dst = out[512 * h : 512 * h + 512, b, :].rearrange("(p i) e -> p i e", i=4)
             nc.sync.dma_start(out=dst[:, ii, :], in_=o_sb[:])
 
-        for step in range(-2, n_tiles):
-            if ok(step - 5):
-                finish(step - 5)
-            if step % 2 == 0 and ok(step - 4):
-                e_times_v(step - 4)
+        for i in range(3):
+            scores(i)
+        rowmax(0)
+        query_silu(n_units - 1, 1)
+        nc.scalar.activation(out=warm[:], in_=ones[:, 0:1], func=ACT.Exp)
+        v_quant(n_units - 2)
+
+        for step in range(n_tiles + 3):
+            if ok(step - 3):
                 e_times_v(step - 3)
             if ok(step + 1):
                 rowmax(step + 1)
             if ok(step):
                 exps(step)
-            if ok(step + 2):
-                scores(step + 2)
             if ok(step - 1):
                 e_evac(step - 1)
             if ok(step):
                 e_transpose(step)
-            if step % 2 == 1 and ok(step - 3):
-                e_quant((step - 3) // 2)
-            if ok(step) and step % 4 == 3:
-                row_sums(step - 3)
-
-        n = n_tiles
-        finish(n - 5)
-        e_times_v(n - 4)
-        e_times_v(n - 3)
-        e_quant_one(n - 2)
-        e_evac(n - 1)
-        e_times_v(n - 2)
-        finish(n - 4)
-        e_quant_one(n - 1)
-        e_times_v(n - 1)
-        finish(n - 3)
-        finish(n - 2)
-        finish(n - 1)
+            if ok(step + 3):
+                scores(step + 3)
+            if ok(step - 3):
+                finish(step - 3)
+            if ok(step - 2):
+                e_quant(step - 2)
+            if ok(step - 1) and step % 2 == 0:
+                row_sums(step - 2)

@@ -17,6 +17,28 @@ T, S, B, E, Z = 1024, 1024, 4, 512, 128
 FLOPS = 2 * (2 * S * B * E * E + B * T * S * Z + B * T * S * E)
 
 MANUAL = True
+XT = 3
+QK_AT = {6: [0], 8: [1], 10: [2], 12: [3], 14: [4], 16: [5, 6], 17: [7]}
+HEADS = {-2: "xe0s xe1v xt0 xt1", -1: "xq xe0s xe1v xt0 xt1", 0: "xq bi xe0s xe1v pj0 pj1 xt0 pj2 pj3 xt1", 2: "vt0 vt1 xq xe0s xe1v ve0s ve1v pj0 pj1 pj2 pj3 xt0 xt1"}
+KSTEP = "xq kt si0 pj0 si1 pj1 xe0v xe1v xt0 si2 pj2 si3 pj3 xt1 vq2 qs11 ke"
+QSTEP = "vt0 vt1 xq xe0s xe1s ve0s kt ad0 pj0 ad1 pj1 xt0 ve1v ad2 pj2 ad3 pj3 xt1 vq2 qs0 ke"
+QSTEP2 = "vt0 vt1 xq xe0s xe1s kt ad0 pj0 ve0v ad1 pj1 xt0 ve1v ad2 pj2 ad3 pj3 xt1 vq2 qs0 ke"
+Q2 = 9
+SC = [0, 1, 2, 3]
+ETR = [4, 5]
+HR = [6, 7]
+LEAD = 2
+NQ1 = 8
+KQ2 = {}
+QKE = "v"
+MISC = None
+LAGS = dict(ev=1, quant=3, mx=4, fin=5)
+PE = ["mx", "sc", "et"]
+VO = ["fin", "rm", "quant"]
+NEG = "g"
+ORDER = ["rs", "mx", "rm", "exp", "sc", "ev", "et", "kt", "ke", "quant", "fin"]
+RS = 4
+RSL = 5
 XIN_BUFS = 10
 QK_LOAD_AFTER = 5
 
@@ -115,27 +137,27 @@ def tile_gatedcrossattention_pa_t_kernel(tc, q_scaled, k, key, query, Wv, bv, Wr
         def is_kind(u, kind):
             return 0 <= u < n_units and units[u][0] == kind
 
-        def x_transpose(u):
-            if u >= n_units:
+        def x_transpose(u, half):
+            if u < 0 or u >= n_units:
                 return
             xin = st[u]["xin"]
-            st[u]["tps"] = []
-            for half in range(2):
-                tp = aux([P, 2, 2, P], F32, "tp")
-                for r in range(2):
-                    words = xin[:, 2 * half + r, :].bitcast(F32)
-                    for w in range(2):
-                        nc.tensor.transpose(tp[:, r, w, :], words[:, w * P : (w + 1) * P], ident_f[:])
-                st[u]["tps"].append(tp)
+            tp = aux([P, 2, 2, P], F32, "tp")
+            for r in range(2):
+                words = xin[:, 2 * half + r, :].bitcast(F32)
+                for w in range(2):
+                    nc.tensor.transpose(tp[:, r, w, :], words[:, w * P : (w + 1) * P], ident_f[:])
+            st[u]["tp%d" % half] = tp
+            if half == 1:
+                load(u + XIN_BUFS)
 
         def x_evac(u, half, eng):
-            if u >= n_units:
+            if u < 0 or u >= n_units:
                 return
             if half == 0:
                 grouped = work.tile([P, 4 * E], BF16, tag="grouped", name="grouped", bufs=3, align_bytes=64)
                 st[u]["grouped"] = grouped
             words = st[u]["grouped"][:].bitcast(F32)[:, half * E : (half + 1) * E]
-            tp = st[u]["tps"][half]
+            tp = st[u]["tp%d" % half]
             if units[u][0] == "k":
                 copy_on(eng, words.rearrange("p (c r w) -> p c r w", r=2, w=2), tp[:].rearrange("p r w c -> p c r w"))
             else:
@@ -174,6 +196,8 @@ def tile_gatedcrossattention_pa_t_kernel(tc, q_scaled, k, key, query, Wv, bv, Wr
             st[u]["pj%d" % j] = pj
 
         def key_silu(u, j):
+            if not is_kind(u, "k"):
+                return
             if j == 0:
                 yT = work.tile([P, 4, E], BF16, tag="yT", name="yT", bufs=2)
                 st[u]["yT"] = yT
@@ -181,17 +205,15 @@ def tile_gatedcrossattention_pa_t_kernel(tc, q_scaled, k, key, query, Wv, bv, Wr
                 out=st[u]["yT"][:, j, :], in_=st[u]["pj%d" % j][:], func=ACT.Silu, bias=bias_v[:, j : j + 1], scale=1.0
             )
 
-        def v_transpose(u):
+        def v_transpose(u, half):
             if not is_kind(u, "k"):
                 return
-            st[u]["vps"] = []
-            for half in range(2):
-                vp = aux([P, 2, 2, P], F32, "vp")
-                for jj in range(2):
-                    words = st[u]["yT"][:, 2 * half + jj, :].bitcast(F32)
-                    for w in range(2):
-                        nc.tensor.transpose(vp[:, jj, w, :], words[:, w * P : (w + 1) * P], ident_f[:])
-                st[u]["vps"].append(vp)
+            vp = aux([P, 2, 2, P], F32, "vp")
+            for jj in range(2):
+                words = st[u]["yT"][:, 2 * half + jj, :].bitcast(F32)
+                for w in range(2):
+                    nc.tensor.transpose(vp[:, jj, w, :], words[:, w * P : (w + 1) * P], ident_f[:])
+            st[u]["vp%d" % half] = vp
 
         def v_evac(u, half, eng):
             if not is_kind(u, "k"):
@@ -203,7 +225,7 @@ def tile_gatedcrossattention_pa_t_kernel(tc, q_scaled, k, key, query, Wv, bv, Wr
             copy_on(
                 eng,
                 words.rearrange("p (j c w) -> p j c w", j=2, w=2),
-                st[u]["vps"][half][:].rearrange("p j w c -> p j c w"),
+                st[u]["vp%d" % half][:].rearrange("p j w c -> p j c w"),
             )
 
         def v_quant(u):
@@ -217,6 +239,8 @@ def tile_gatedcrossattention_pa_t_kernel(tc, q_scaled, k, key, query, Wv, bv, Wr
             )
 
         def query_add(u, j):
+            if not is_kind(u, "q"):
+                return
             kind, a, c = units[u]
             nc.vector.tensor_tensor(
                 out=r_sb[:, 4 * (2 * a + c) + j, :], in0=st[u]["pj%d" % j][:], in1=bias_r[:], op=ALU.add
@@ -238,7 +262,7 @@ def tile_gatedcrossattention_pa_t_kernel(tc, q_scaled, k, key, query, Wv, bv, Wr
                 return
             w, b = qk_items[m]
             src = (q_sb, k_sb)[w]
-            tq = aux([P, 8, P], BF16, "tq")
+            tq = (aux if m < NQ1 else misc)([P, 8, P], BF16, "tq")
             for h in range(2):
                 for i in range(4):
                     nc.tensor.transpose(tq[:, 4 * h + i, :], src[:, h, i, b * Z : (b + 1) * Z], ident_b[:])
@@ -250,10 +274,10 @@ def tile_gatedcrossattention_pa_t_kernel(tc, q_scaled, k, key, query, Wv, bv, Wr
             w, b = qk_items[m]
             dst = (qT, kT)[w][b]
             if w == 0:
-                copy_on("v", dst[:], qk_ps[m][:].rearrange("p n c -> p (n c)"))
+                copy_on(QKE if m < NQ1 else "s", dst[:], qk_ps[m][:].rearrange("p n c -> p (n c)"))
             else:
                 copy_on(
-                    "v",
+                    QKE if m < NQ1 else "s",
                     dst[:].rearrange("z (x p e) -> z x p e", x=4, e=2),
                     qk_ps[m][:].rearrange("z (x e) p -> z x p e", e=2),
                 )
@@ -264,54 +288,37 @@ def tile_gatedcrossattention_pa_t_kernel(tc, q_scaled, k, key, query, Wv, bv, Wr
                 nc.sync.dma_start(out=k_sb[:], in_=k.rearrange("(h p i) b z -> p h i (b z)", p=P, i=4))
                 nc.sync.dma_start(out=q_sb[:], in_=q_scaled.rearrange("(h p i) b z -> p h i (b z)", p=P, i=4))
 
-        qk_at = {6: [0], 8: [1], 10: [2], 12: [3], 14: [4], 16: [5, 6], 17: [7]}
-        for step in range(-2, n_units):
-            x_transpose(step + 2)
-            load(step + 2 + XIN_BUFS)
-            x_quant(step + 1)
-            if step == 0:
-                spread_biases()
-            if is_kind(step, "k"):
-                for m in qk_at.get(step, []):
-                    qk_transpose(m)
-                for j in range(4):
-                    key_silu(step, j)
-                    project(step + 1, j)
-                x_evac(step + 2, 0, "v")
-                x_evac(step + 2, 1, "v")
-                v_quant(step - 2)
-                query_silu(step - 1, 1)
-                for m in qk_at.get(step, []):
-                    qk_evac(m)
-            elif is_kind(step, "q"):
-                v_transpose(step - 1)
-                x_evac(step + 2, 0, "s")
-                x_evac(step + 2, 1, "s")
-                v_evac(step - 1, 0, "s")
-                for m in qk_at.get(step, []):
-                    qk_transpose(m)
-                for j in range(4):
-                    if j == 2:
-                        v_evac(step - 1, 1, "v")
-                    query_add(step, j)
-                    project(step + 1, j)
-                v_quant(step - 2)
-                query_silu(step, 0)
-                for m in qk_at.get(step, []):
-                    qk_evac(m)
-            else:
-                v_transpose(step - 1)
-                x_evac(step + 2, 0, "s")
-                x_evac(step + 2, 1, "v")
-                v_evac(step - 1, 0, "s")
-                v_evac(step - 1, 1, "v")
-                for j in range(4):
-                    project(step + 1, j)
+        def run(t, tokens):
+            for tok in tokens.split():
+                n, rest = tok[:2], tok[2:]
+                if n == "xq": x_quant(t + 1)
+                elif n == "xt": x_transpose(t + XT, int(rest))
+                elif n == "xe": x_evac(t + 2, int(rest[0]), rest[1])
+                elif n == "si": key_silu(t, int(rest))
+                elif n == "ad": query_add(t, int(rest))
+                elif n == "pj": project(t + 1, int(rest))
+                elif n == "vt": v_transpose(t - 1 - int(rest[1:] or "0"), int(rest[0]))
+                elif n == "ve": v_evac(t - 1 - int(rest[2:] or "0"), int(rest[0]), rest[1])
+                elif n == "vq": v_quant(t - int(rest))
+                elif n == "qs": query_silu(t - int(rest[1:] or "0"), int(rest[0]))
+                elif n == "bi": spread_biases()
+                elif n == "kt":
+                    for m in qk_at.get(t, []): qk_transpose(m)
+                elif n == "ke":
+                    for m in qk_at.get(t, []): qk_evac(m)
+
+        qk_at = QK_AT
+        for u in range(XT - 2):
+            x_transpose(u, 0)
+            x_transpose(u, 1)
+        for t in range(-2, n_units):
+            run(t, HEADS[t] if t in HEADS else KSTEP if is_kind(t, "k") else QSTEP2 if t % 4 == Q2 else QSTEP)
 
         n_tiles = 8 * B
-        sc_ring = ring([0, 1, 2, 3, 4, 5])
-        et_ring = ring([6])
-        h_ring = ring([7])
+        sc_ring = ring(SC)
+        et_ring = ring(ETR)
+        h_ring = et_ring if HR is None else ring(HR)
+        misc = et_ring if MISC is None else ring(MISC)
         at = [dict() for i in range(n_tiles)]
 
         def ok(i):
@@ -332,6 +339,13 @@ def tile_gatedcrossattention_pa_t_kernel(tc, q_scaled, k, key, query, Wv, bv, Wr
                 at[i]["sc"].append(sc)
 
         def rowmax(i):
+            if NEG == "v":
+                m0 = work.tile([P, 2], F32, tag="m2", name="m2", bufs=4)
+                junk = work.tile([P, 512], BF16, tag="junk", name="junk", bufs=2)
+                nc.vector.tensor_reduce(out=m0[:, 0:1], in_=at[i]["sc"][0][:], axis=AX.X, op=ALU.min)
+                nc.vector.tensor_scalar(out=junk[:], in0=at[i]["sc"][1][:], scalar1=1.0, scalar2=m0[:, 0:1], op0=ALU.mult, op1=ALU.min, accum_out=m0[:, 1:2])
+                at[i]["negm"] = m0[:, 1:2]
+                return
             m2 = work.tile([P, 2], F32, tag="m2", name="m2", bufs=4)
             for g in range(2):
                 nc.vector.tensor_reduce(out=m2[:, g : g + 1], in_=at[i]["sc"][g][:], axis=AX.X, op=ALU.max)
@@ -348,7 +362,7 @@ def tile_gatedcrossattention_pa_t_kernel(tc, q_scaled, k, key, query, Wv, bv, Wr
                     out=e_sb[:, g, :],
                     in_=at[i]["sc"][g][:],
                     func=ACT.Exp,
-                    bias=at[i]["negm"][:],
+                    bias=at[i]["negm"] if NEG == "v" else at[i]["negm"][:],
                     scale=1.0,
                     accum_out=rs_all[:, i, g : g + 1],
                 )
@@ -396,11 +410,11 @@ def tile_gatedcrossattention_pa_t_kernel(tc, q_scaled, k, key, query, Wv, bv, Wr
             at[i]["h_ps"] = h_ps
 
         def row_sums(i0):
-            rsum = work.tile([P, 2], F32, tag="rsum", name="rsum", bufs=2)
+            rsum = work.tile([P, RS], F32, tag="rsum", name="rsum", bufs=2)
             nc.gpsimd.tensor_tensor(
-                out=rsum[:], in0=rs_all[:, i0 : i0 + 2, 0], in1=rs_all[:, i0 : i0 + 2, 1], op=ALU.add
+                out=rsum[:], in0=rs_all[:, i0 : i0 + RS, 0], in1=rs_all[:, i0 : i0 + RS, 1], op=ALU.add
             )
-            nc.vector.reciprocal(out=rinv_all[:, i0 : i0 + 2], in_=rsum[:])
+            nc.vector.reciprocal(out=rinv_all[:, i0 : i0 + RS], in_=rsum[:])
 
         def finish(i):
             b, h, ii = i // 8, (i % 8) // 4, i % 4
@@ -411,29 +425,27 @@ def tile_gatedcrossattention_pa_t_kernel(tc, q_scaled, k, key, query, Wv, bv, Wr
             dst = out[512 * h : 512 * h + 512, b, :].rearrange("(p i) e -> p i e", i=4)
             nc.sync.dma_start(out=dst[:, ii, :], in_=o_sb[:])
 
-        for i in range(3):
+        for i in range(LEAD):
             scores(i)
         rowmax(0)
         query_silu(n_units - 1, 1)
         nc.scalar.activation(out=warm[:], in_=ones[:, 0:1], func=ACT.Exp)
         v_quant(n_units - 2)
-
-        for step in range(n_tiles + 3):
-            if ok(step - 3):
-                e_times_v(step - 3)
-            if ok(step + 1):
-                rowmax(step + 1)
-            if ok(step):
-                exps(step)
-            if ok(step - 1):
-                e_evac(step - 1)
-            if ok(step):
-                e_transpose(step)
-            if ok(step + 3):
-                scores(step + 3)
-            if ok(step - 3):
-                finish(step - 3)
-            if ok(step - 2):
-                e_quant(step - 2)
-            if ok(step - 1) and step % 2 == 0:
-                row_sums(step - 2)
+        fns = dict(fin=finish, mx=e_times_v, exp=exps, sc=scores, ev=e_evac, et=e_transpose, quant=e_quant, rm=rowmax)
+        lag = dict(LAGS, exp=0, et=0, rm=-1, sc=-LEAD)
+        for step in range(n_tiles + 8):
+            for o in ORDER:
+                if o == "rs":
+                    if (step - RSL) % RS == 0 and ok(step - RSL): row_sums(step - RSL)
+                    continue
+                if o == "kt":
+                    if step in KQ2: qk_transpose(KQ2[step])
+                    continue
+                if o == "ke":
+                    if step - 1 in KQ2: qk_evac(KQ2[step - 1])
+                    continue
+                i = step - lag[o]
+                if ok(i):
+                    if o == "rm" and i == 0: continue
+                    if o == "sc" and i < LEAD: continue
+                    fns[o](i)

@@ -18,17 +18,20 @@ FLOPS = 2 * (2 * S * B * E * E + B * T * S * Z + B * T * S * E)
 
 MANUAL = True
 XT = 3
-QK_AT = {6: [0], 8: [1], 10: [2], 12: [3], 14: [4], 16: [5, 6], 17: [7]}
-HEADS = {-2: "xe0s xe1v xt0 xt1", -1: "xq xe0s xe1v xt0 xt1", 0: "xq bi xe0s xe1v pj0 pj1 xt0 pj2 pj3 xt1", 2: "vt0 vt1 xq xe0s xe1v ve0s ve1v pj0 pj1 pj2 pj3 xt0 xt1"}
-KSTEP = "xq kt si0 pj0 si1 pj1 xe0v xe1v xt0 si2 pj2 si3 pj3 xt1 vq2 qs11 ke"
-QSTEP = "vt0 vt1 xq xe0s xe1s ve0s kt ad0 pj0 ad1 pj1 xt0 ve1v ad2 pj2 ad3 pj3 xt1 vq2 qs0 ke"
-QSTEP2 = "vt0 vt1 xq xe0s xe1s kt ad0 pj0 ve0v ad1 pj1 xt0 ve1v ad2 pj2 ad3 pj3 xt1 vq2 qs0 ke"
-Q2 = 9
+QK_AT = {6: [0], 8: [1], 10: [2], 12: [3], 14: [4]}
+T0 = 4
+HEAD = "xt0.0 xt0.1 xe0.0s xe0.1v xt1.0 xt1.1 bv xq0 xe1.0s xe1.1v br xt2.0 xt2.1 xq1 xe2.0s xe2.1v xt3.0 xt3.1 pj1.0 pj1.1 pj1.2 pj1.3 xq2 si1.0 si1.1 xe3.0v xe3.1v si1.2 si1.3 xt4.0 xt4.1 xq3 pj3.0 pj3.1 pj3.2 pj3.3 xe4.0s xe4.1s vt1.0 xt5.0 xt5.1 vt1.1 ad3.0 ad3.1 xq4 pj4.0 pj4.1 ad3.2 ad3.3 pj4.2 pj4.3 ve1.0s xe5.0s xe5.1v ve1.1v xt6.0 xt6.1 qs3.0 vq1"
+KSTEP = "xq kt si0 pj0 si1 pj1 xe0v xe1v xt0 xt1 si2 pj2 si3 pj3 vq2 qs11 ke"
+QSTEP = "vt0 vt1 xq xe0s xe1s ve0s kt ad0 pj0 ad1 pj1 xt0 xt1 ad2 pj2 ad3 pj3 ve1v vq2 qs0 ke"
+QSTEP2 = "vt0 vt1 xq xe0s xe1s kt ad0 pj0 ad1 pj1 xt0 xt1 ad2 pj2 ad3 pj3 ve0v ve1v vq2 qs0 ke"
+Q2 = 1
+PRO = "sc0 sc1 kt5 kt6 rm0 qs ex rm1 sc2 ke5 ke6 kt7 vq rm2 ke7"
+HT = 2
 SC = [0, 1, 2, 3]
 ETR = [4, 5]
 HR = [6, 7]
 LEAD = 2
-NQ1 = 8
+NQ1 = 5
 KQ2 = {}
 QKE = "v"
 MISC = None
@@ -89,13 +92,14 @@ def tile_gatedcrossattention_pa_t_kernel(tc, q_scaled, k, key, query, Wv, bv, Wr
         bias_r = const.tile([P, E], F32, name="bias_r")
         bias_v = const.tile([P, 4], F32, name="bias_v")
 
-        def spread_biases():
+        def spread_bv():
             bv_ps = big([P, P], BF16, "bv_ps")
             nc.tensor.transpose(bv_ps[:], bv_rows[:], ident_b[:])
             nc.vector.tensor_copy(out=bias_v[:], in_=bv_ps[:, 0:4])
+        def spread_br():
             br_ps = big([P, E], F32, "br_ps")
             nc.tensor.matmul(br_ps[:], lhsT=ones[:], rhs=bias_rows[:], start=True, stop=True)
-            nc.vector.tensor_copy(out=bias_r[:], in_=br_ps[:])
+            nc.scalar.copy(out=bias_r[:], in_=br_ps[:])
 
         q_sb = const.tile([P, 2, 4, B * Z], BF16, name="q_sb")
         k_sb = const.tile([P, 2, 4, B * Z], BF16, name="k_sb")
@@ -274,10 +278,10 @@ def tile_gatedcrossattention_pa_t_kernel(tc, q_scaled, k, key, query, Wv, bv, Wr
             w, b = qk_items[m]
             dst = (qT, kT)[w][b]
             if w == 0:
-                copy_on(QKE if m < NQ1 else "s", dst[:], qk_ps[m][:].rearrange("p n c -> p (n c)"))
+                copy_on(QKE, dst[:], qk_ps[m][:].rearrange("p n c -> p (n c)"))
             else:
                 copy_on(
-                    QKE if m < NQ1 else "s",
+                    QKE,
                     dst[:].rearrange("z (x p e) -> z x p e", x=4, e=2),
                     qk_ps[m][:].rearrange("z (x e) p -> z x p e", e=2),
                 )
@@ -301,18 +305,33 @@ def tile_gatedcrossattention_pa_t_kernel(tc, q_scaled, k, key, query, Wv, bv, Wr
                 elif n == "ve": v_evac(t - 1 - int(rest[2:] or "0"), int(rest[0]), rest[1])
                 elif n == "vq": v_quant(t - int(rest))
                 elif n == "qs": query_silu(t - int(rest[1:] or "0"), int(rest[0]))
-                elif n == "bi": spread_biases()
                 elif n == "kt":
                     for m in qk_at.get(t, []): qk_transpose(m)
                 elif n == "ke":
                     for m in qk_at.get(t, []): qk_evac(m)
 
         qk_at = QK_AT
-        for u in range(XT - 2):
-            x_transpose(u, 0)
-            x_transpose(u, 1)
-        for t in range(-2, n_units):
-            run(t, HEADS[t] if t in HEADS else KSTEP if is_kind(t, "k") else QSTEP2 if t % 4 == Q2 else QSTEP)
+        for tok in HEAD.split():
+            n, rest = tok[:2], tok[2:].split(".")
+            u = int(rest[0] or "0")
+            h = int(rest[1][0]) if len(rest) > 1 else 0
+            e = rest[1][1:] if len(rest) > 1 else ""
+            if n == "xt": x_transpose(u, h)
+            elif n == "xe": x_evac(u, h, e)
+            elif n == "xq": x_quant(u)
+            elif n == "pj": project(u, h)
+            elif n == "si": key_silu(u, h)
+            elif n == "ad": query_add(u, h)
+            elif n == "vt": v_transpose(u, h)
+            elif n == "ve": v_evac(u, h, e)
+            elif n == "vq": v_quant(u)
+            elif n == "qs": query_silu(u, h)
+            elif n == "bv": spread_bv()
+            elif n == "br": spread_br()
+            elif n == "kt": qk_transpose(u)
+            elif n == "ke": qk_evac(u)
+        for t in range(T0, n_units):
+            run(t, KSTEP if is_kind(t, "k") else QSTEP2 if t % 4 == Q2 else QSTEP)
 
         n_tiles = 8 * B
         sc_ring = ring(SC)
@@ -328,7 +347,7 @@ def tile_gatedcrossattention_pa_t_kernel(tc, q_scaled, k, key, query, Wv, bv, Wr
             b, n = i // 8, i % 8
             at[i]["sc"] = []
             for g in range(2):
-                sc = sc_ring([P, 512], F32, "sc")
+                sc = (h_ring if i == HT else sc_ring)([P, 512], F32, "sc")
                 nc.tensor.matmul(
                     sc[:],
                     lhsT=qT[b][:, n * P : (n + 1) * P],
@@ -425,12 +444,18 @@ def tile_gatedcrossattention_pa_t_kernel(tc, q_scaled, k, key, query, Wv, bv, Wr
             dst = out[512 * h : 512 * h + 512, b, :].rearrange("(p i) e -> p i e", i=4)
             nc.sync.dma_start(out=dst[:, ii, :], in_=o_sb[:])
 
-        for i in range(LEAD):
-            scores(i)
-        rowmax(0)
-        query_silu(n_units - 1, 1)
-        nc.scalar.activation(out=warm[:], in_=ones[:, 0:1], func=ACT.Exp)
-        v_quant(n_units - 2)
+        done = set()
+        for tok in PRO.split():
+            n, m = tok[:2], int(tok[2:] or "0")
+            if n == "sc": scores(m); done.add(("sc", m))
+            elif n == "rm": rowmax(m); done.add(("rm", m))
+            elif n == "qs": query_silu(n_units - 1, 1)
+            elif n == "ex": nc.scalar.activation(out=warm[:], in_=ones[:, 0:1], func=ACT.Exp)
+            elif n == "vq": v_quant(n_units - 2)
+            elif n == "kt": qk_transpose(m)
+            elif n == "ke": qk_evac(m)
+            elif n == "vt": v_transpose(n_units - 2, m)
+            elif n == "ve": v_evac(n_units - 2, m, "v")
         fns = dict(fin=finish, mx=e_times_v, exp=exps, sc=scores, ev=e_evac, et=e_transpose, quant=e_quant, rm=rowmax)
         lag = dict(LAGS, exp=0, et=0, rm=-1, sc=-LEAD)
         for step in range(n_tiles + 8):
@@ -446,6 +471,5 @@ def tile_gatedcrossattention_pa_t_kernel(tc, q_scaled, k, key, query, Wv, bv, Wr
                     continue
                 i = step - lag[o]
                 if ok(i):
-                    if o == "rm" and i == 0: continue
-                    if o == "sc" and i < LEAD: continue
+                    if (o, i) in done: continue
                     fns[o](i)

@@ -19,12 +19,13 @@ FLOPS = 2 * (2 * S * B * E * E + B * T * S * Z + B * T * S * E)
 MANUAL = True
 XT = 3
 QK_AT = {6: [0], 8: [1], 10: [2], 12: [3], 14: [4]}
+K2ND = False
 T0 = 4
 HEAD = "xt0.0 xt0.1 xe0.0s xe0.1v xt1.0 xt1.1 bv xq0 xe1.0s xe1.1v br xt2.0 xt2.1 xq1 xe2.0s xe2.1v xt3.0 xt3.1 pj1.0 pj1.1 pj1.2 pj1.3 xq2 si1.0 si1.1 xe3.0v xe3.1v si1.2 si1.3 xt4.0 xt4.1 xq3 pj3.0 pj3.1 pj3.2 pj3.3 xe4.0s xe4.1s vt1.0 xt5.0 xt5.1 vt1.1 ad3.0 ad3.1 xq4 pj4.0 pj4.1 ad3.2 ad3.3 pj4.2 pj4.3 ve1.0s xe5.0s xe5.1v ve1.1v xt6.0 xt6.1 qs3.0 vq1"
 KSTEP = "xq kt si0 pj0 si1 pj1 xe0v xe1v xt0 xt1 si2 pj2 si3 pj3 vq2 qs11 ke"
 QSTEP = "vt0 vt1 xq xe0s xe1s ve0s kt ad0 pj0 ad1 pj1 xt0 xt1 ad2 pj2 ad3 pj3 ve1v vq2 qs0 ke"
 QSTEP2 = "vt0 vt1 xq xe0s xe1s kt ad0 pj0 ad1 pj1 xt0 xt1 ad2 pj2 ad3 pj3 ve0v ve1v vq2 qs0 ke"
-Q2 = 1
+Q2 = 9
 PRO = "sc0 sc1 kt5 kt6 rm0 qs ex rm1 sc2 ke5 ke6 kt7 vq rm2 ke7"
 HT = 2
 SC = [0, 1, 2, 3]
@@ -33,13 +34,21 @@ HR = [6, 7]
 LEAD = 2
 NQ1 = 5
 KQ2 = {}
+V2 = {}
+VDEF = []
+V2E = "s"
 QKE = "v"
+QKL = "v"
 MISC = None
-LAGS = dict(ev=1, quant=3, mx=4, fin=5)
+LAGS = dict(ev=1, quant=2, mx=4, fin=5)
 PE = ["mx", "sc", "et"]
 VO = ["fin", "rm", "quant"]
 NEG = "g"
-ORDER = ["rs", "mx", "rm", "exp", "sc", "ev", "et", "kt", "ke", "quant", "fin"]
+ORDER = ["rs", "mx", "rm", "exp", "sc", "ev", "et", "kt", "ke", "fin", "quant"]
+PAIRQ = True
+EVE = "s"
+GF = 6
+GFR = [4]
 RS = 4
 RSL = 5
 XIN_BUFS = 10
@@ -115,11 +124,13 @@ def tile_gatedcrossattention_pa_t_kernel(tc, q_scaled, k, key, query, Wv, bv, Wr
 
         k_units = [("k", b, g) for b in range(B) for g in range(2)]
         q_units = [("q", b, h) for b in range(B) for h in range(2)]
-        units = [("w", 0, 0), k_units[0], ("w", 1, 0)]
-        for i in range(2 * B):
-            units += ([k_units[i]] if i > 0 else []) + [q_units[i]]
+        units = [("w", 0, 0), k_units[0], k_units[1], ("w", 1, 0), q_units[0]] if K2ND else [("w", 0, 0), k_units[0], ("w", 1, 0), q_units[0]]
+        for i in range(2 if K2ND else 1, 2 * B):
+            units += [k_units[i], q_units[i - 1 if K2ND else i]]
+        if K2ND: units += [q_units[2 * B - 1]]
         n_units = len(units)
         st = [dict() for u in range(n_units)]
+        KLAST = max(u for u in range(n_units) if units[u][0] == "k")
 
         def load(u):
             if u < 0 or u >= n_units:
@@ -203,7 +214,7 @@ def tile_gatedcrossattention_pa_t_kernel(tc, q_scaled, k, key, query, Wv, bv, Wr
             if not is_kind(u, "k"):
                 return
             if j == 0:
-                yT = work.tile([P, 4, E], BF16, tag="yT", name="yT", bufs=2)
+                yT = work.tile([P, 4, E], BF16, tag="yT", name="yT", bufs=2 + len(VDEF))
                 st[u]["yT"] = yT
             nc.scalar.activation(
                 out=st[u]["yT"][:, j, :], in_=st[u]["pj%d" % j][:], func=ACT.Silu, bias=bias_v[:, j : j + 1], scale=1.0
@@ -212,7 +223,7 @@ def tile_gatedcrossattention_pa_t_kernel(tc, q_scaled, k, key, query, Wv, bv, Wr
         def v_transpose(u, half):
             if not is_kind(u, "k"):
                 return
-            vp = aux([P, 2, 2, P], F32, "vp")
+            vp = (misc if u in VDEF else aux)([P, 2, 2, P], F32, "vp")
             for jj in range(2):
                 words = st[u]["yT"][:, 2 * half + jj, :].bitcast(F32)
                 for w in range(2):
@@ -278,10 +289,14 @@ def tile_gatedcrossattention_pa_t_kernel(tc, q_scaled, k, key, query, Wv, bv, Wr
             w, b = qk_items[m]
             dst = (qT, kT)[w][b]
             if w == 0:
-                copy_on(QKE, dst[:], qk_ps[m][:].rearrange("p n c -> p (n c)"))
+                src = qk_ps[m][:].rearrange("p n c -> p (n c)")
+                if NEG == "acc":
+                    nc.vector.tensor_scalar(out=dst[:], in0=src, scalar1=-1.0, scalar2=0.0, op0=ALU.mult, op1=ALU.add)
+                else:
+                    copy_on(QKE if m < NQ1 else QKL, dst[:], src)
             else:
                 copy_on(
-                    QKE,
+                    QKE if m < NQ1 else QKL,
                     dst[:].rearrange("z (x p e) -> z x p e", x=4, e=2),
                     qk_ps[m][:].rearrange("z (x e) p -> z x p e", e=2),
                 )
@@ -301,9 +316,12 @@ def tile_gatedcrossattention_pa_t_kernel(tc, q_scaled, k, key, query, Wv, bv, Wr
                 elif n == "si": key_silu(t, int(rest))
                 elif n == "ad": query_add(t, int(rest))
                 elif n == "pj": project(t + 1, int(rest))
-                elif n == "vt": v_transpose(t - 1 - int(rest[1:] or "0"), int(rest[0]))
-                elif n == "ve": v_evac(t - 1 - int(rest[2:] or "0"), int(rest[0]), rest[1])
-                elif n == "vq": v_quant(t - int(rest))
+                elif n == "vt":
+                    if t - 1 - int(rest[1:] or "0") not in VDEF: v_transpose(t - 1 - int(rest[1:] or "0"), int(rest[0]))
+                elif n == "ve":
+                    if t - 1 - int(rest[2:] or "0") not in VDEF: v_evac(t - 1 - int(rest[2:] or "0"), int(rest[0]), rest[1])
+                elif n == "vq":
+                    if t - int(rest) not in VDEF: v_quant(t - int(rest))
                 elif n == "qs": query_silu(t - int(rest[1:] or "0"), int(rest[0]))
                 elif n == "kt":
                     for m in qk_at.get(t, []): qk_transpose(m)
@@ -358,20 +376,30 @@ def tile_gatedcrossattention_pa_t_kernel(tc, q_scaled, k, key, query, Wv, bv, Wr
                 at[i]["sc"].append(sc)
 
         def rowmax(i):
-            if NEG == "v":
-                m0 = work.tile([P, 2], F32, tag="m2", name="m2", bufs=4)
-                junk = work.tile([P, 512], BF16, tag="junk", name="junk", bufs=2)
-                nc.vector.tensor_reduce(out=m0[:, 0:1], in_=at[i]["sc"][0][:], axis=AX.X, op=ALU.min)
-                nc.vector.tensor_scalar(out=junk[:], in0=at[i]["sc"][1][:], scalar1=1.0, scalar2=m0[:, 0:1], op0=ALU.mult, op1=ALU.min, accum_out=m0[:, 1:2])
-                at[i]["negm"] = m0[:, 1:2]
-                return
+            rmax_a(i)
+            rmax_b(i)
+            if NEG != "acc": rmax_c(i)
+
+        def rmax_a(i):
             m2 = work.tile([P, 2], F32, tag="m2", name="m2", bufs=4)
-            for g in range(2):
-                nc.vector.tensor_reduce(out=m2[:, g : g + 1], in_=at[i]["sc"][g][:], axis=AX.X, op=ALU.max)
+            at[i]["m2"] = m2
+            nc.vector.tensor_reduce(out=m2[:, 0:1], in_=at[i]["sc"][0][:], axis=AX.X, op=ALU.min if NEG == "acc" else ALU.max)
+
+        def rmax_b(i):
+            m2 = at[i]["m2"]
+            if NEG == "acc":
+                junk = work.tile([P, 512], BF16, tag="junk", name="junk", bufs=1)
+                negm = work.tile([P, 1], F32, tag="negm", name="negm", bufs=4)
+                nc.vector.tensor_scalar(out=junk[:], in0=at[i]["sc"][1][:], scalar1=1.0, scalar2=m2[:, 0:1], op0=ALU.mult, op1=ALU.min, accum_out=negm[:])
+                at[i]["negm"] = negm
+            else:
+                nc.vector.tensor_reduce(out=m2[:, 1:2], in_=at[i]["sc"][1][:], axis=AX.X, op=ALU.max)
+
+        def rmax_c(i):
+            m2 = at[i]["m2"]
             negm = work.tile([P, 1], F32, tag="negm", name="negm", bufs=4)
-            nc.gpsimd.tensor_scalar(
-                out=negm[:], in0=m2[:, 0:1], scalar1=m2[:, 1:2], scalar2=-1.0, op0=ALU.max, op1=ALU.mult
-            )
+            eng = nc.gpsimd if NEG == "g" else nc.vector
+            eng.tensor_scalar(out=negm[:], in0=m2[:, 0:1], scalar1=m2[:, 1:2], scalar2=-1.0, op0=ALU.max, op1=ALU.mult)
             at[i]["negm"] = negm
 
         def exps(i):
@@ -381,8 +409,8 @@ def tile_gatedcrossattention_pa_t_kernel(tc, q_scaled, k, key, query, Wv, bv, Wr
                     out=e_sb[:, g, :],
                     in_=at[i]["sc"][g][:],
                     func=ACT.Exp,
-                    bias=at[i]["negm"] if NEG == "v" else at[i]["negm"][:],
-                    scale=1.0,
+                    bias=at[i]["negm"][:],
+                    scale=-1.0 if NEG == "acc" else 1.0,
                     accum_out=rs_all[:, i, g : g + 1],
                 )
             at[i]["e_sb"] = e_sb
@@ -396,12 +424,28 @@ def tile_gatedcrossattention_pa_t_kernel(tc, q_scaled, k, key, query, Wv, bv, Wr
             at[i]["et"] = et
 
         def e_evac(i):
-            eg = work.tile([P, 2, P, 4], BF16, tag="eg", name="eg", bufs=3, align_bytes=64)
-            at[i]["eg"] = eg
-            dst = eg[:].rearrange("p g t j -> p (g t j)").bitcast(F32)
-            copy_on("s", dst.rearrange("p (g t u) -> p g t u", g=2, u=2), at[i]["et"][:].rearrange("p g u t -> p g t u"))
+            if PAIRQ:
+                if i % 2 == 0:
+                    eg = work.tile([P, 2, 2, P, 4], BF16, tag="eg", name="eg", bufs=2, align_bytes=64)
+                    at[i]["egp"] = eg
+                at[i]["egp"] = at[i - i % 2]["egp"]
+                dst = at[i]["egp"][:, i % 2].rearrange("p g t j -> p (g t j)").bitcast(F32)
+            else:
+                eg = work.tile([P, 2, P, 4], BF16, tag="eg", name="eg", bufs=3, align_bytes=64)
+                at[i]["eg"] = eg
+                dst = eg[:].rearrange("p g t j -> p (g t j)").bitcast(F32)
+            copy_on(EVE[i % len(EVE)], dst.rearrange("p (g t u) -> p g t u", g=2, u=2), at[i]["et"][:].rearrange("p g u t -> p g t u"))
 
         def e_quant(i):
+            if PAIRQ:
+                if i % 2 == 0: return
+                e_codes = work.tile([P, 4 * P], U32, tag="e_codes", name="e_codes", bufs=2, align_bytes=64)
+                e_scales = work.tile([P, 4 * P], U8, tag="e_scales", name="e_scales", bufs=2, align_bytes=64)
+                nc.vector.quantize_mx(out=e_codes[:].bitcast(FP8X4), scales=e_scales[:], in_=at[i]["egp"][:].rearrange("p a g t j -> p (a g t j)"))
+                for d in range(2):
+                    at[i - 1 + d]["e_codes"] = e_codes[:, 2 * P * d : 2 * P * d + 2 * P]
+                    at[i - 1 + d]["e_scales"] = e_scales[:, 2 * P * d : 2 * P * d + 2 * P]
+                return
             e_codes = work.tile([P, 2 * P], U32, tag="e_codes", name="e_codes", bufs=3, align_bytes=64)
             e_scales = work.tile([P, 2 * P], U8, tag="e_scales", name="e_scales", bufs=3, align_bytes=64)
             nc.vector.quantize_mx(
@@ -430,17 +474,23 @@ def tile_gatedcrossattention_pa_t_kernel(tc, q_scaled, k, key, query, Wv, bv, Wr
 
         def row_sums(i0):
             rsum = work.tile([P, RS], F32, tag="rsum", name="rsum", bufs=2)
-            nc.gpsimd.tensor_tensor(
-                out=rsum[:], in0=rs_all[:, i0 : i0 + RS, 0], in1=rs_all[:, i0 : i0 + RS, 1], op=ALU.add
-            )
+            if NEG == "g":
+                nc.gpsimd.tensor_tensor(out=rsum[:], in0=rs_all[:, i0 : i0 + RS, 0], in1=rs_all[:, i0 : i0 + RS, 1], op=ALU.add)
+            else:
+                nc.vector.tensor_reduce(out=rsum[:], in_=rs_all[:, i0 : i0 + RS, :], axis=AX.X, op=ALU.add)
             nc.vector.reciprocal(out=rinv_all[:, i0 : i0 + RS], in_=rsum[:])
 
         def finish(i):
             b, h, ii = i // 8, (i % 8) // 4, i % 4
             o_sb = work.tile([P, E], F32, tag="o_sb", name="o_sb", bufs=4)
-            nc.vector.scalar_tensor_tensor(
-                out=o_sb[:], in0=at[i]["h_ps"][:], scalar=rinv_all[:, i : i + 1], in1=r_sb[:, i, :], op0=ALU.mult, op1=ALU.mult
-            )
+            if i % GF in GFR and i < n_tiles - 4:
+                hs = work.tile([P, E], F32, tag="hs", name="hs", bufs=2)
+                nc.scalar.activation(out=hs[:], in_=at[i]["h_ps"][:], func=ACT.Copy, scale=rinv_all[:, i : i + 1])
+                nc.gpsimd.tensor_tensor(out=o_sb[:], in0=hs[:], in1=r_sb[:, i, :], op=ALU.mult)
+            else:
+                nc.vector.scalar_tensor_tensor(
+                    out=o_sb[:], in0=at[i]["h_ps"][:], scalar=rinv_all[:, i : i + 1], in1=r_sb[:, i, :], op0=ALU.mult, op1=ALU.mult
+                )
             dst = out[512 * h : 512 * h + 512, b, :].rearrange("(p i) e -> p i e", i=4)
             nc.sync.dma_start(out=dst[:, ii, :], in_=o_sb[:])
 
@@ -451,13 +501,13 @@ def tile_gatedcrossattention_pa_t_kernel(tc, q_scaled, k, key, query, Wv, bv, Wr
             elif n == "rm": rowmax(m); done.add(("rm", m))
             elif n == "qs": query_silu(n_units - 1, 1)
             elif n == "ex": nc.scalar.activation(out=warm[:], in_=ones[:, 0:1], func=ACT.Exp)
-            elif n == "vq": v_quant(n_units - 2)
+            elif n == "vq": v_quant(KLAST)
             elif n == "kt": qk_transpose(m)
             elif n == "ke": qk_evac(m)
-            elif n == "vt": v_transpose(n_units - 2, m)
-            elif n == "ve": v_evac(n_units - 2, m, "v")
-        fns = dict(fin=finish, mx=e_times_v, exp=exps, sc=scores, ev=e_evac, et=e_transpose, quant=e_quant, rm=rowmax)
-        lag = dict(LAGS, exp=0, et=0, rm=-1, sc=-LEAD)
+            elif n == "vt": v_transpose(KLAST, m)
+            elif n == "ve": v_evac(KLAST, m, "v")
+        fns = dict(fin=finish, mx=e_times_v, exp=exps, sc=scores, ev=e_evac, et=e_transpose, quant=e_quant, rm=rowmax, ra=rmax_a, rb=rmax_b, rc=rmax_c)
+        lag = dict(LAGS, exp=0, et=0, rm=-1, ra=-1, rb=-1, rc=-1, sc=-LEAD)
         for step in range(n_tiles + 8):
             for o in ORDER:
                 if o == "rs":
@@ -465,11 +515,16 @@ def tile_gatedcrossattention_pa_t_kernel(tc, q_scaled, k, key, query, Wv, bv, Wr
                     continue
                 if o == "kt":
                     if step in KQ2: qk_transpose(KQ2[step])
+                    if step in V2: v_transpose(*V2[step])
                     continue
                 if o == "ke":
                     if step - 1 in KQ2: qk_evac(KQ2[step - 1])
+                    if step - 1 in V2:
+                        v_evac(*V2[step - 1], V2E)
+                    if step - 2 in V2 and V2[step - 2][1] == 1:
+                        v_quant(V2[step - 2][0])
                     continue
                 i = step - lag[o]
                 if ok(i):
-                    if (o, i) in done: continue
+                    if (o, i) in done or (o in ("ra", "rb", "rc") and ("rm", i) in done): continue
                     fns[o](i)

@@ -18,16 +18,18 @@ FLOPS = 2 * (2 * S * B * E * E + B * T * S * Z + B * T * S * E)
 
 MANUAL = True
 XT = 3
-QK_AT = {6: [0], 8: [1], 10: [2], 12: [3], 14: [4]}
+QK_AT = {8: [1], 10: [2], 12: [3], 14: [4]}
 K2ND = False
 T0 = 4
-HEAD = "xt0.0 xt0.1 xe0.0s xe0.1v xt1.0 xt1.1 bv xq0 xe1.0s xe1.1v br xt2.0 xt2.1 xq1 xe2.0s xe2.1v xt3.0 xt3.1 pj1.0 pj1.1 pj1.2 pj1.3 xq2 si1.0 si1.1 xe3.0v xe3.1v si1.2 si1.3 xt4.0 xt4.1 xq3 pj3.0 pj3.1 pj3.2 pj3.3 xe4.0s xe4.1s vt1.0 xt5.0 xt5.1 vt1.1 ad3.0 ad3.1 xq4 pj4.0 pj4.1 ad3.2 ad3.3 pj4.2 pj4.3 ve1.0s xe5.0s xe5.1v ve1.1v xt6.0 xt6.1 qs3.0 vq1"
+HEAD = "xt0.0 xt0.1 xe0.0s xe0.1v xt1.0 xt1.1 bv wu1 xq0 xe1.0s xe1.1v br xt2.0 xt2.1 xq1 xe2.0s xe2.1v xt3.0 xt3.1 pj1.0 pj1.1 pj1.2 pj1.3 xq2 si1.0 si1.1 xe3.0v xe3.1v kt0 si1.2 si1.3 xt4.0 xt4.1 xq3 pj3.0 pj3.1 pj3.2 pj3.3 ke0 xe4.0s xe4.1s vt1.0 xt5.0 xt5.1 vt1.1 ad3.0 ad3.1 xq4 pj4.0 pj4.1 ad3.2 ad3.3 pj4.2 pj4.3 ve1.0s xe5.0s xe5.1v ve1.1v xt6.0 xt6.1 qs3.0 vq1"
 KSTEP = "xq kt si0 pj0 si1 pj1 xe0v xe1v xt0 xt1 si2 pj2 si3 pj3 vq2 qs11 ke"
 QSTEP = "vt0 vt1 xq xe0s xe1s ve0s kt ad0 pj0 ad1 pj1 xt0 xt1 ad2 pj2 ad3 pj3 ve1v vq2 qs0 ke"
 QSTEP2 = "vt0 vt1 xq xe0s xe1s kt ad0 pj0 ad1 pj1 xt0 xt1 ad2 pj2 ad3 pj3 ve0v ve1v vq2 qs0 ke"
 Q2 = 9
+NWARM = 5
 PRO = "sc0 sc1 kt5 kt6 rm0 qs ex rm1 sc2 ke5 ke6 kt7 vq rm2 ke7"
 HT = 2
+ASG = {}
 SC = [0, 1, 2, 3]
 ETR = [4, 5]
 HR = [6, 7]
@@ -37,22 +39,26 @@ KQ2 = {}
 V2 = {}
 VDEF = []
 V2E = "s"
-QKE = "v"
-QKL = "v"
+QKS = "svvvvvvv"
 MISC = None
-LAGS = dict(ev=1, quant=2, mx=4, fin=5)
+TAIL = False
+TAILSEQ = "mx28 qu29 fi27 mx29 qu30 ms30 su28 fi28 ev0v ev1s qg0 qg1 ms31 fi29 su30 fi30 fh0 fh1"
+LAGS = dict(ev=1, quant=3, mx=4, fin=5)
 PE = ["mx", "sc", "et"]
 VO = ["fin", "rm", "quant"]
 NEG = "g"
-ORDER = ["rs", "mx", "rm", "exp", "sc", "ev", "et", "kt", "ke", "fin", "quant"]
-PAIRQ = True
+ORDER = ["rs", "mx", "rm", "exp", "sc", "ev", "et", "kt", "ke", "quant", "fin"]
+PAIRQ = False
 EVE = "s"
-GF = 6
-GFR = [4]
+GF = 999
+GFR = [998]
+GFT = []
 RS = 4
 RSL = 5
+RGL = 5
 XIN_BUFS = 10
-QK_LOAD_AFTER = 5
+K_AFTER = 3
+Q_AFTER = 6
 
 
 def tile_gatedcrossattention_pa_t_kernel(tc, q_scaled, k, key, query, Wv, bv, Wr, br, out):
@@ -92,10 +98,15 @@ def tile_gatedcrossattention_pa_t_kernel(tc, q_scaled, k, key, query, Wv, bv, Wr
         bias_rows = const.tile([P, E], BF16, name="bias_rows")
         bv_rows = const.tile([P, P], BF16, name="bv_rows")
         nc.vector.memset(ones[:], 1.0)
+        wrow = const.tile([P, E], BF16, name="wrow")
+        nc.vector.memset(wrow[:], 0.0)
         nc.vector.memset(bias_rows[:], 0.0)
         nc.vector.memset(bv_rows[:], 0.0)
         nc.scalar.dma_start(out=bv_rows[0:4, :], in_=bv.rearrange("(j p) -> j p", p=P))
         nc.scalar.dma_start(out=bias_rows[0:1, :], in_=br.unsqueeze(0))
+        for i in range(NWARM):
+            warm_ps = big([P, E], F32, "warm_ps")
+            nc.tensor.matmul(warm_ps[:], lhsT=ones[:], rhs=wrow[:], start=True, stop=True)
         warm = const.tile([P, 1], F32, name="warm")
         nc.scalar.activation(out=warm[:], in_=ones[:, 0:1], func=ACT.Silu)
         bias_r = const.tile([P, E], F32, name="bias_r")
@@ -293,18 +304,19 @@ def tile_gatedcrossattention_pa_t_kernel(tc, q_scaled, k, key, query, Wv, bv, Wr
                 if NEG == "acc":
                     nc.vector.tensor_scalar(out=dst[:], in0=src, scalar1=-1.0, scalar2=0.0, op0=ALU.mult, op1=ALU.add)
                 else:
-                    copy_on(QKE if m < NQ1 else QKL, dst[:], src)
+                    copy_on(QKS[m], dst[:], src)
             else:
                 copy_on(
-                    QKE if m < NQ1 else QKL,
+                    QKS[m],
                     dst[:].rearrange("z (x p e) -> z x p e", x=4, e=2),
                     qk_ps[m][:].rearrange("z (x e) p -> z x p e", e=2),
                 )
 
         for u in range(XIN_BUFS):
             load(u)
-            if u == QK_LOAD_AFTER:
+            if u == K_AFTER:
                 nc.sync.dma_start(out=k_sb[:], in_=k.rearrange("(h p i) b z -> p h i (b z)", p=P, i=4))
+            if u == Q_AFTER:
                 nc.sync.dma_start(out=q_sb[:], in_=q_scaled.rearrange("(h p i) b z -> p h i (b z)", p=P, i=4))
 
         def run(t, tokens):
@@ -312,17 +324,21 @@ def tile_gatedcrossattention_pa_t_kernel(tc, q_scaled, k, key, query, Wv, bv, Wr
                 n, rest = tok[:2], tok[2:]
                 if n == "xq": x_quant(t + 1)
                 elif n == "xt": x_transpose(t + XT, int(rest))
-                elif n == "xe": x_evac(t + 2, int(rest[0]), rest[1])
+                elif n == "xe": x_evac(t + 2, int(rest[0]), ASG[t][int(rest[0])] if t in ASG else rest[1])
                 elif n == "si": key_silu(t, int(rest))
                 elif n == "ad": query_add(t, int(rest))
                 elif n == "pj": project(t + 1, int(rest))
                 elif n == "vt":
                     if t - 1 - int(rest[1:] or "0") not in VDEF: v_transpose(t - 1 - int(rest[1:] or "0"), int(rest[0]))
                 elif n == "ve":
-                    if t - 1 - int(rest[2:] or "0") not in VDEF: v_evac(t - 1 - int(rest[2:] or "0"), int(rest[0]), rest[1])
+                    if t - 1 - int(rest[2:] or "0") not in VDEF: v_evac(t - 1 - int(rest[2:] or "0"), int(rest[0]), ASG[t][2 + int(rest[0])] if t in ASG else rest[1])
                 elif n == "vq":
                     if t - int(rest) not in VDEF: v_quant(t - int(rest))
                 elif n == "qs": query_silu(t - int(rest[1:] or "0"), int(rest[0]))
+                elif n == "wu":
+                    for i in range(int(rest)):
+                        warm_ps = big([P, E], F32, "warm_ps")
+                        nc.tensor.matmul(warm_ps[:], lhsT=ones[:], rhs=wrow[:], start=True, stop=True)
                 elif n == "kt":
                     for m in qk_at.get(t, []): qk_transpose(m)
                 elif n == "ke":
@@ -348,6 +364,10 @@ def tile_gatedcrossattention_pa_t_kernel(tc, q_scaled, k, key, query, Wv, bv, Wr
             elif n == "br": spread_br()
             elif n == "kt": qk_transpose(u)
             elif n == "ke": qk_evac(u)
+            elif n == "wu":
+                for i in range(u):
+                    warm_ps = big([P, E], F32, "warm_ps")
+                    nc.tensor.matmul(warm_ps[:], lhsT=ones[:], rhs=wrow[:], start=True, stop=True)
         for t in range(T0, n_units):
             run(t, KSTEP if is_kind(t, "k") else QSTEP2 if t % 4 == Q2 else QSTEP)
 
@@ -472,18 +492,22 @@ def tile_gatedcrossattention_pa_t_kernel(tc, q_scaled, k, key, query, Wv, bv, Wr
                 )
             at[i]["h_ps"] = h_ps
 
-        def row_sums(i0):
+        def row_adds(i0):
             rsum = work.tile([P, RS], F32, tag="rsum", name="rsum", bufs=2)
             if NEG == "g":
                 nc.gpsimd.tensor_tensor(out=rsum[:], in0=rs_all[:, i0 : i0 + RS, 0], in1=rs_all[:, i0 : i0 + RS, 1], op=ALU.add)
             else:
                 nc.vector.tensor_reduce(out=rsum[:], in_=rs_all[:, i0 : i0 + RS, :], axis=AX.X, op=ALU.add)
-            nc.vector.reciprocal(out=rinv_all[:, i0 : i0 + RS], in_=rsum[:])
+            at[i0]["rsum"] = rsum
+
+        def row_sums(i0):
+            if "rsum" not in at[i0]: row_adds(i0)
+            nc.vector.reciprocal(out=rinv_all[:, i0 : i0 + RS], in_=at[i0]["rsum"][:])
 
         def finish(i):
             b, h, ii = i // 8, (i % 8) // 4, i % 4
-            o_sb = work.tile([P, E], F32, tag="o_sb", name="o_sb", bufs=4)
-            if i % GF in GFR and i < n_tiles - 4:
+            o_sb = work.tile([P, E], F32, tag="o_sb", name="o_sb", bufs=6)
+            if i in GFT or (i % GF in GFR and i < n_tiles - 4):
                 hs = work.tile([P, E], F32, tag="hs", name="hs", bufs=2)
                 nc.scalar.activation(out=hs[:], in_=at[i]["h_ps"][:], func=ACT.Copy, scale=rinv_all[:, i : i + 1])
                 nc.gpsimd.tensor_tensor(out=o_sb[:], in0=hs[:], in1=r_sb[:, i, :], op=ALU.mult)
@@ -508,10 +532,13 @@ def tile_gatedcrossattention_pa_t_kernel(tc, q_scaled, k, key, query, Wv, bv, Wr
             elif n == "ve": v_evac(KLAST, m, "v")
         fns = dict(fin=finish, mx=e_times_v, exp=exps, sc=scores, ev=e_evac, et=e_transpose, quant=e_quant, rm=rowmax, ra=rmax_a, rb=rmax_b, rc=rmax_c)
         lag = dict(LAGS, exp=0, et=0, rm=-1, ra=-1, rb=-1, rc=-1, sc=-LEAD)
-        for step in range(n_tiles + 8):
+        for step in range(n_tiles if TAIL else n_tiles + 8):
             for o in ORDER:
                 if o == "rs":
                     if (step - RSL) % RS == 0 and ok(step - RSL): row_sums(step - RSL)
+                    continue
+                if o == "rg":
+                    if (step - RGL) % RS == 0 and ok(step - RGL): row_adds(step - RGL)
                     continue
                 if o == "kt":
                     if step in KQ2: qk_transpose(KQ2[step])
@@ -527,4 +554,62 @@ def tile_gatedcrossattention_pa_t_kernel(tc, q_scaled, k, key, query, Wv, bv, Wr
                 i = step - lag[o]
                 if ok(i):
                     if (o, i) in done or (o in ("ra", "rb", "rc") and ("rm", i) in done): continue
+                    if TAIL and i == n_tiles - 1 and o in ("exp", "et", "ev"): continue
                     fns[o](i)
+
+        if TAIL:
+            n = n_tiles - 1
+            e_sb = work.tile([P, 2, 512], BF16, tag="e_sb", name="e_sb", bufs=3)
+            at[n]["e_sb"] = e_sb
+            et = et_ring([P, 2, 2, P], F32, "et")
+            eg = work.tile([P, 2, P, 4], BF16, tag="eg", name="eg", bufs=3, align_bytes=64)
+            at[n]["eg"] = eg
+            e_codes = work.tile([P, 2 * P], U32, tag="e_codes", name="e_codes", bufs=3, align_bytes=64)
+            e_scales = work.tile([P, 2 * P], U8, tag="e_scales", name="e_scales", bufs=3, align_bytes=64)
+            at[n]["e_codes"] = e_codes
+            at[n]["e_scales"] = e_scales
+
+            def exp_g(g):
+                nc.scalar.activation(out=e_sb[:, g, :], in_=at[n]["sc"][g][:], func=ACT.Exp, bias=at[n]["negm"][:], scale=1.0, accum_out=rs_all[:, n, g : g + 1])
+                words = e_sb[:, g, :].bitcast(F32)
+                for u in range(2):
+                    nc.tensor.transpose(et[:, g, u, :], words[:, u * P : (u + 1) * P], ident_f[:])
+
+            def ev_g(g, eng):
+                dst = eg[:, g].rearrange("p t j -> p (t j)").bitcast(F32)
+                copy_on(eng, dst.rearrange("p (t u) -> p t u", u=2), et[:, g].rearrange("p u t -> p t u"))
+
+            def quant_g(g):
+                nc.vector.quantize_mx(out=e_codes[:, g * P : (g + 1) * P].bitcast(FP8X4), scales=e_scales[:, g * P : (g + 1) * P], in_=eg[:, g].rearrange("p t j -> p (t j)"))
+
+            def sums(i0):
+                rsum = work.tile([P, 2], F32, tag="rsum2", name="rsum2", bufs=2)
+                nc.gpsimd.tensor_tensor(out=rsum[:], in0=rs_all[:, i0 : i0 + 2, 0], in1=rs_all[:, i0 : i0 + 2, 1], op=ALU.add)
+                nc.vector.reciprocal(out=rinv_all[:, i0 : i0 + 2], in_=rsum[:])
+
+            def mx(i, r):
+                h_ps = r([P, E], F32, "h_ps")
+                for g in range(2):
+                    cols = slice(g * P, (g + 1) * P)
+                    nc.tensor.matmul_mx(out=h_ps[:], lhsT=at[i]["e_codes"][:, cols].bitcast(FP8X4), lhsT_scale=at[i]["e_scales"][:, cols], rhs=v_codes[:, 2 * 3 + g, :].bitcast(FP8X4), rhs_scale=v_scales[:, 2 * 3 + g, :], start=(g == 0), stop=(g == 1))
+                at[i]["h_ps"] = h_ps
+
+            def fin_half(i, c):
+                o_half = work.tile([P, 256], F32, tag="o_half", name="o_half", bufs=2)
+                cs = slice(256 * c, 256 * c + 256)
+                nc.vector.scalar_tensor_tensor(out=o_half[:], in0=at[i]["h_ps"][:, cs], scalar=rinv_all[:, i : i + 1], in1=r_sb[:, i, cs], op0=ALU.mult, op1=ALU.mult)
+                dst = out[512:1024, 3, :].rearrange("(p i) e -> p i e", i=4)
+                nc.sync.dma_start(out=dst[:, 3, cs], in_=o_half[:])
+
+            exp_g(0)
+            exp_g(1)
+            for tok in TAILSEQ.split():
+                a, m = tok[:2], tok[2:]
+                if a == "qu": e_quant(int(m))
+                elif a == "mx": mx(int(m), h_ring)
+                elif a == "ms": mx(int(m), sc_ring)
+                elif a == "fi": finish(int(m))
+                elif a == "su": sums(int(m))
+                elif a == "ev": ev_g(int(m[0]), m[1])
+                elif a == "qg": quant_g(int(m))
+                elif a == "fh": fin_half(n, int(m))

@@ -24,12 +24,18 @@ T0 = 4
 HEAD = "xt0.0 xt0.1 xe0.0s xe0.1v xt1.0 xt1.1 bv wu1 xq0 xe1.0s xe1.1v br xt2.0 xt2.1 xq1 xe2.0s xe2.1v xt3.0 xt3.1 pj1.0 pj1.1 pj1.2 pj1.3 xq2 si1.0 si1.1 xe3.0v xe3.1v kt0 si1.2 si1.3 xt4.0 xt4.1 xq3 pj3.0 pj3.1 pj3.2 pj3.3 ke0 xe4.0s xe4.1s vt1.0 xt5.0 xt5.1 vt1.1 ad3.0 ad3.1 xq4 pj4.0 pj4.1 ad3.2 ad3.3 pj4.2 pj4.3 ve1.0s xe5.0s xe5.1v ve1.1v xt6.0 xt6.1 qs3.0 vq1"
 KSTEP = "xq kt si0 pj0 si1 pj1 xe0v xe1v xt0 xt1 si2 pj2 si3 pj3 vq2 qs11 ke"
 QSTEP = "vt0 vt1 xq xe0s xe1s ve0s kt ad0 pj0 ad1 pj1 xt0 xt1 ad2 pj2 ad3 pj3 ve1v vq2 qs0 ke"
-QSTEP2 = "vt0 vt1 xq xe0s xe1s kt ad0 pj0 ad1 pj1 xt0 xt1 ad2 pj2 ad3 pj3 ve0v ve1v vq2 qs0 ke"
-Q2 = 9
+QSTEPT = "vt0 vt1 xq ad0 pj0 ad1 pj1 xe0v xe1s xt0 xt1 ve0s ad2 pj2 ad3 pj3 ve1v vq2 kt qs0 ke"
 NWARM = 5
 PRO = "sc0 sc1 kt5 kt6 rm0 qs ex rm1 sc2 ke5 ke6 kt7 vq rm2 ke7"
 HT = 2
-ASG = {}
+ASG = {15: "vvsv"}
+OB = 8
+ETS = 31
+HS = 30
+VELATE = []
+TU = [3,5,7,9,11,13,15]
+OT = 6
+OE = 7
 SC = [0, 1, 2, 3]
 ETR = [4, 5]
 HR = [6, 7]
@@ -41,14 +47,13 @@ VDEF = []
 V2E = "s"
 QKS = "svvvvvvv"
 MISC = None
-TAIL = False
-TAILSEQ = "mx28 qu29 fi27 mx29 qu30 ms30 su28 fi28 ev0v ev1s qg0 qg1 ms31 fi29 su30 fi30 fh0 fh1"
 LAGS = dict(ev=1, quant=3, mx=4, fin=5)
 PE = ["mx", "sc", "et"]
 VO = ["fin", "rm", "quant"]
 NEG = "g"
-ORDER = ["rs", "mx", "rm", "exp", "sc", "ev", "et", "kt", "ke", "quant", "fin"]
+ORDER = ["rs", "mx", "rm", "exp", "sc", "ev", "oe", "et", "ot", "kt", "ke", "quant", "fin"]
 PAIRQ = False
+PQN = 32
 EVE = "s"
 GF = 999
 GFR = [998]
@@ -56,7 +61,7 @@ GFT = []
 RS = 4
 RSL = 5
 RGL = 5
-XIN_BUFS = 10
+XIN_BUFS = 8
 K_AFTER = 3
 Q_AFTER = 6
 
@@ -103,6 +108,9 @@ def tile_gatedcrossattention_pa_t_kernel(tc, q_scaled, k, key, query, Wv, bv, Wr
         nc.vector.memset(bias_rows[:], 0.0)
         nc.vector.memset(bv_rows[:], 0.0)
         nc.scalar.dma_start(out=bv_rows[0:4, :], in_=bv.rearrange("(j p) -> j p", p=P))
+        br_cols = const.tile([P, P], BF16, name="br_cols")
+        nc.vector.memset(br_cols[:], 0.0)
+        nc.scalar.dma_start(out=br_cols[0:4, :], in_=br.rearrange("(j p) -> j p", p=P))
         nc.scalar.dma_start(out=bias_rows[0:1, :], in_=br.unsqueeze(0))
         for i in range(NWARM):
             warm_ps = big([P, E], F32, "warm_ps")
@@ -110,12 +118,13 @@ def tile_gatedcrossattention_pa_t_kernel(tc, q_scaled, k, key, query, Wv, bv, Wr
         warm = const.tile([P, 1], F32, name="warm")
         nc.scalar.activation(out=warm[:], in_=ones[:, 0:1], func=ACT.Silu)
         bias_r = const.tile([P, E], F32, name="bias_r")
-        bias_v = const.tile([P, 4], F32, name="bias_v")
+        bias_v = const.tile([P, 8], F32, name="bias_v")
 
         def spread_bv():
-            bv_ps = big([P, P], BF16, "bv_ps")
-            nc.tensor.transpose(bv_ps[:], bv_rows[:], ident_b[:])
-            nc.vector.tensor_copy(out=bias_v[:], in_=bv_ps[:, 0:4])
+            bv_ps = big([P, 2, P], BF16, "bv_ps")
+            nc.tensor.transpose(bv_ps[:, 0, :], bv_rows[:], ident_b[:])
+            nc.tensor.transpose(bv_ps[:, 1, :], br_cols[:], ident_b[:])
+            nc.vector.tensor_copy(out=bias_v[:].rearrange("p (w j) -> p w j", w=2), in_=bv_ps[:, :, 0:4])
         def spread_br():
             br_ps = big([P, E], F32, "br_ps")
             nc.tensor.matmul(br_ps[:], lhsT=ones[:], rhs=bias_rows[:], start=True, stop=True)
@@ -210,6 +219,20 @@ def tile_gatedcrossattention_pa_t_kernel(tc, q_scaled, k, key, query, Wv, bv, Wr
             x = (st[u]["codes"], st[u]["scales"])
             w = (w_codes[0], w_scales[0]) if units[u][0] == "k" else (w_codes[1], w_scales[1])
             sta, mov = (w, x) if units[u][0] == "k" else (x, w)
+            if u in TU and j < 2:
+                for k2 in range(2):
+                    c = slice((2 * j + k2) * P, (2 * j + k2 + 1) * P)
+                    nc.tensor.matmul_mx(
+                        out=pj[:, k2 * 256 : k2 * 256 + 256],
+                        lhsT=w[0][:, c].bitcast(FP8X4),
+                        lhsT_scale=w[1][:, c],
+                        rhs=x[0][:, 0:256].bitcast(FP8X4),
+                        rhs_scale=x[1][:, 0:256],
+                        start=True,
+                        stop=True,
+                    )
+                st[u]["pj%d" % j] = pj
+                return
             nc.tensor.matmul_mx(
                 out=pj[:],
                 lhsT=sta[0][:, cols].bitcast(FP8X4),
@@ -268,6 +291,19 @@ def tile_gatedcrossattention_pa_t_kernel(tc, q_scaled, k, key, query, Wv, bv, Wr
             if not is_kind(u, "q"):
                 return
             kind, a, c = units[u]
+            if u in TU and j < 2:
+                i0 = 4 * (2 * a + c)
+                rT = r_sb[:, i0 : i0 + 2, :].rearrange("p x e -> p (x e)")
+                for k2 in range(2):
+                    c2 = 2 * j + k2
+                    nc.scalar.activation(
+                        out=rT[:, c2 * 256 : c2 * 256 + 256],
+                        in_=st[u]["pj%d" % j][:, k2 * 256 : k2 * 256 + 256],
+                        func=ACT.Silu,
+                        bias=bias_v[:, 4 + c2 : 5 + c2],
+                        scale=1.0,
+                    )
+                return
             nc.vector.tensor_tensor(
                 out=r_sb[:, 4 * (2 * a + c) + j, :], in0=st[u]["pj%d" % j][:], in1=bias_r[:], op=ALU.add
             )
@@ -276,6 +312,8 @@ def tile_gatedcrossattention_pa_t_kernel(tc, q_scaled, k, key, query, Wv, bv, Wr
             if not is_kind(u, "q"):
                 return
             kind, a, c = units[u]
+            if u in TU and half == 0:
+                return
             i0 = 4 * (2 * a + c) + 2 * half
             rr = r_sb[:, i0 : i0 + 2, :]
             nc.scalar.activation(out=rr, in_=rr, func=ACT.Silu)
@@ -331,7 +369,7 @@ def tile_gatedcrossattention_pa_t_kernel(tc, q_scaled, k, key, query, Wv, bv, Wr
                 elif n == "vt":
                     if t - 1 - int(rest[1:] or "0") not in VDEF: v_transpose(t - 1 - int(rest[1:] or "0"), int(rest[0]))
                 elif n == "ve":
-                    if t - 1 - int(rest[2:] or "0") not in VDEF: v_evac(t - 1 - int(rest[2:] or "0"), int(rest[0]), ASG[t][2 + int(rest[0])] if t in ASG else rest[1])
+                    if t - 1 - int(rest[2:] or "0") not in VDEF + VELATE: v_evac(t - 1 - int(rest[2:] or "0"), int(rest[0]), ASG[t][2 + int(rest[0])] if t in ASG else rest[1])
                 elif n == "vq":
                     if t - int(rest) not in VDEF: v_quant(t - int(rest))
                 elif n == "qs": query_silu(t - int(rest[1:] or "0"), int(rest[0]))
@@ -369,7 +407,7 @@ def tile_gatedcrossattention_pa_t_kernel(tc, q_scaled, k, key, query, Wv, bv, Wr
                     warm_ps = big([P, E], F32, "warm_ps")
                     nc.tensor.matmul(warm_ps[:], lhsT=ones[:], rhs=wrow[:], start=True, stop=True)
         for t in range(T0, n_units):
-            run(t, KSTEP if is_kind(t, "k") else QSTEP2 if t % 4 == Q2 else QSTEP)
+            run(t, KSTEP if is_kind(t, "k") else QSTEPT if t in TU else QSTEP)
 
         n_tiles = 8 * B
         sc_ring = ring(SC)
@@ -377,12 +415,23 @@ def tile_gatedcrossattention_pa_t_kernel(tc, q_scaled, k, key, query, Wv, bv, Wr
         h_ring = et_ring if HR is None else ring(HR)
         misc = et_ring if MISC is None else ring(MISC)
         at = [dict() for i in range(n_tiles)]
+        u_of = dict(((units[u][1], units[u][2]), u) for u in range(n_units) if units[u][0] == "q")
+        II = [0, 2, 1, 3]
+
+        def where(i):
+            return i // 8, (i % 8) // 4, II[i % 4]
+
+        def is_t(i):
+            b, h, ii = where(i)
+            return u_of[(b, h)] in TU and ii < 2
+
 
         def ok(i):
             return 0 <= i < n_tiles
 
         def scores(i):
-            b, n = i // 8, i % 8
+            b, h, ii = where(i)
+            n = 4 * h + ii
             at[i]["sc"] = []
             for g in range(2):
                 sc = (h_ring if i == HT else sc_ring)([P, 512], F32, "sc")
@@ -436,7 +485,7 @@ def tile_gatedcrossattention_pa_t_kernel(tc, q_scaled, k, key, query, Wv, bv, Wr
             at[i]["e_sb"] = e_sb
 
         def e_transpose(i):
-            et = et_ring([P, 2, 2, P], F32, "et")
+            et = (sc_ring if i >= ETS else et_ring)([P, 2, 2, P], F32, "et")
             for g in range(2):
                 words = at[i]["e_sb"][:, g, :].bitcast(F32)
                 for u in range(2):
@@ -444,20 +493,20 @@ def tile_gatedcrossattention_pa_t_kernel(tc, q_scaled, k, key, query, Wv, bv, Wr
             at[i]["et"] = et
 
         def e_evac(i):
-            if PAIRQ:
+            if PAIRQ and i < PQN:
                 if i % 2 == 0:
                     eg = work.tile([P, 2, 2, P, 4], BF16, tag="eg", name="eg", bufs=2, align_bytes=64)
                     at[i]["egp"] = eg
                 at[i]["egp"] = at[i - i % 2]["egp"]
                 dst = at[i]["egp"][:, i % 2].rearrange("p g t j -> p (g t j)").bitcast(F32)
             else:
-                eg = work.tile([P, 2, P, 4], BF16, tag="eg", name="eg", bufs=3, align_bytes=64)
+                eg = work.tile([P, 2, P, 4], BF16, tag="eg1", name="eg1", bufs=2 if PAIRQ else 3, align_bytes=64)
                 at[i]["eg"] = eg
                 dst = eg[:].rearrange("p g t j -> p (g t j)").bitcast(F32)
             copy_on(EVE[i % len(EVE)], dst.rearrange("p (g t u) -> p g t u", g=2, u=2), at[i]["et"][:].rearrange("p g u t -> p g t u"))
 
         def e_quant(i):
-            if PAIRQ:
+            if PAIRQ and i < PQN:
                 if i % 2 == 0: return
                 e_codes = work.tile([P, 4 * P], U32, tag="e_codes", name="e_codes", bufs=2, align_bytes=64)
                 e_scales = work.tile([P, 4 * P], U8, tag="e_scales", name="e_scales", bufs=2, align_bytes=64)
@@ -466,8 +515,8 @@ def tile_gatedcrossattention_pa_t_kernel(tc, q_scaled, k, key, query, Wv, bv, Wr
                     at[i - 1 + d]["e_codes"] = e_codes[:, 2 * P * d : 2 * P * d + 2 * P]
                     at[i - 1 + d]["e_scales"] = e_scales[:, 2 * P * d : 2 * P * d + 2 * P]
                 return
-            e_codes = work.tile([P, 2 * P], U32, tag="e_codes", name="e_codes", bufs=3, align_bytes=64)
-            e_scales = work.tile([P, 2 * P], U8, tag="e_scales", name="e_scales", bufs=3, align_bytes=64)
+            e_codes = work.tile([P, 2 * P], U32, tag="e_codes1", name="e_codes1", bufs=2 if PAIRQ else 3, align_bytes=64)
+            e_scales = work.tile([P, 2 * P], U8, tag="e_scales1", name="e_scales1", bufs=2 if PAIRQ else 3, align_bytes=64)
             nc.vector.quantize_mx(
                 out=e_codes[:].bitcast(FP8X4),
                 scales=e_scales[:],
@@ -478,19 +527,49 @@ def tile_gatedcrossattention_pa_t_kernel(tc, q_scaled, k, key, query, Wv, bv, Wr
 
         def e_times_v(i):
             b = i // 8
-            h_ps = h_ring([P, E], F32, "h_ps")
-            for g in range(2):
-                cols = slice(g * P, (g + 1) * P)
-                nc.tensor.matmul_mx(
-                    out=h_ps[:],
-                    lhsT=at[i]["e_codes"][:, cols].bitcast(FP8X4),
-                    lhsT_scale=at[i]["e_scales"][:, cols],
-                    rhs=v_codes[:, 2 * b + g, :].bitcast(FP8X4),
-                    rhs_scale=v_scales[:, 2 * b + g, :],
-                    start=(g == 0),
-                    stop=(g == 1),
-                )
+            h_ps = (sc_ring if i >= HS else h_ring)([P, E], F32, "h_ps")
+            if is_t(i):
+                for c in range(4):
+                    cols = slice(c * P, (c + 1) * P)
+                    for g in range(2):
+                        q = slice(g * P, (g + 1) * P)
+                        nc.tensor.matmul_mx(
+                            out=h_ps[:, cols],
+                            lhsT=v_codes[:, 2 * b + g, cols].bitcast(FP8X4),
+                            lhsT_scale=v_scales[:, 2 * b + g, cols],
+                            rhs=at[i]["e_codes"][:, q].bitcast(FP8X4),
+                            rhs_scale=at[i]["e_scales"][:, q],
+                            start=(g == 0),
+                            stop=(g == 1),
+                        )
+            else:
+                for g in range(2):
+                    cols = slice(g * P, (g + 1) * P)
+                    nc.tensor.matmul_mx(
+                        out=h_ps[:],
+                        lhsT=at[i]["e_codes"][:, cols].bitcast(FP8X4),
+                        lhsT_scale=at[i]["e_scales"][:, cols],
+                        rhs=v_codes[:, 2 * b + g, :].bitcast(FP8X4),
+                        rhs_scale=v_scales[:, 2 * b + g, :],
+                        start=(g == 0),
+                        stop=(g == 1),
+                    )
             at[i]["h_ps"] = h_ps
+
+        def o_transpose(i):
+            if not is_t(i): return
+            o_ps = et_ring([P, E], F32, "o_ps")
+            for c in range(4):
+                nc.tensor.transpose(o_ps[:, c * P : (c + 1) * P], at[i]["prod"][:, c, :], ident_f[:])
+            at[i]["o_ps"] = o_ps
+
+        def o_evac(i):
+            if not is_t(i): return
+            b, h, ii = where(i)
+            o_sb = work.tile([P, E], F32, tag="o_sb", name="o_sb", bufs=OB)
+            nc.scalar.activation(out=o_sb[:], in_=at[i]["o_ps"][:], func=ACT.Copy, scale=rinv_all[:, i : i + 1])
+            dst = out[512 * h : 512 * h + 512, b, :].rearrange("(p i) e -> p i e", i=4)
+            nc.sync.dma_start(out=dst[:, ii, :], in_=o_sb[:])
 
         def row_adds(i0):
             rsum = work.tile([P, RS], F32, tag="rsum", name="rsum", bufs=2)
@@ -505,16 +584,23 @@ def tile_gatedcrossattention_pa_t_kernel(tc, q_scaled, k, key, query, Wv, bv, Wr
             nc.vector.reciprocal(out=rinv_all[:, i0 : i0 + RS], in_=at[i0]["rsum"][:])
 
         def finish(i):
-            b, h, ii = i // 8, (i % 8) // 4, i % 4
-            o_sb = work.tile([P, E], F32, tag="o_sb", name="o_sb", bufs=6)
-            if i in GFT or (i % GF in GFR and i < n_tiles - 4):
-                hs = work.tile([P, E], F32, tag="hs", name="hs", bufs=2)
-                nc.scalar.activation(out=hs[:], in_=at[i]["h_ps"][:], func=ACT.Copy, scale=rinv_all[:, i : i + 1])
-                nc.gpsimd.tensor_tensor(out=o_sb[:], in0=hs[:], in1=r_sb[:, i, :], op=ALU.mult)
-            else:
-                nc.vector.scalar_tensor_tensor(
-                    out=o_sb[:], in0=at[i]["h_ps"][:], scalar=rinv_all[:, i : i + 1], in1=r_sb[:, i, :], op0=ALU.mult, op1=ALU.mult
+            b, h, ii = where(i)
+            r0 = 4 * (2 * b + h)
+            if is_t(i):
+                prod = work.tile([P, 4, P], F32, tag="prod", name="prod", bufs=3)
+                rT = r_sb[:, r0 : r0 + 2, :].rearrange("p x e -> p (x e)").rearrange("p (c t) -> p c t", c=4)
+                nc.vector.tensor_tensor(
+                    out=prod[:],
+                    in0=at[i]["h_ps"][:].rearrange("p (c t) -> p c t", c=4),
+                    in1=rT[:, :, ii * P : (ii + 1) * P],
+                    op=ALU.mult,
                 )
+                at[i]["prod"] = prod
+                return
+            o_sb = work.tile([P, E], F32, tag="o_sb", name="o_sb", bufs=OB)
+            nc.vector.scalar_tensor_tensor(
+                out=o_sb[:], in0=at[i]["h_ps"][:], scalar=rinv_all[:, i : i + 1], in1=r_sb[:, r0 + ii, :], op0=ALU.mult, op1=ALU.mult
+            )
             dst = out[512 * h : 512 * h + 512, b, :].rearrange("(p i) e -> p i e", i=4)
             nc.sync.dma_start(out=dst[:, ii, :], in_=o_sb[:])
 
@@ -530,9 +616,10 @@ def tile_gatedcrossattention_pa_t_kernel(tc, q_scaled, k, key, query, Wv, bv, Wr
             elif n == "ke": qk_evac(m)
             elif n == "vt": v_transpose(KLAST, m)
             elif n == "ve": v_evac(KLAST, m, "v")
-        fns = dict(fin=finish, mx=e_times_v, exp=exps, sc=scores, ev=e_evac, et=e_transpose, quant=e_quant, rm=rowmax, ra=rmax_a, rb=rmax_b, rc=rmax_c)
-        lag = dict(LAGS, exp=0, et=0, rm=-1, ra=-1, rb=-1, rc=-1, sc=-LEAD)
-        for step in range(n_tiles if TAIL else n_tiles + 8):
+            elif n == "VE": v_evac(KLAST, m, "s")
+        fns = dict(fin=finish, mx=e_times_v, exp=exps, sc=scores, ev=e_evac, et=e_transpose, quant=e_quant, rm=rowmax, ra=rmax_a, rb=rmax_b, rc=rmax_c, ot=o_transpose, oe=o_evac)
+        lag = dict(LAGS, ot=OT, oe=OE, exp=0, et=0, rm=-1, ra=-1, rb=-1, rc=-1, sc=-LEAD)
+        for step in range(n_tiles + 8):
             for o in ORDER:
                 if o == "rs":
                     if (step - RSL) % RS == 0 and ok(step - RSL): row_sums(step - RSL)
@@ -554,62 +641,4 @@ def tile_gatedcrossattention_pa_t_kernel(tc, q_scaled, k, key, query, Wv, bv, Wr
                 i = step - lag[o]
                 if ok(i):
                     if (o, i) in done or (o in ("ra", "rb", "rc") and ("rm", i) in done): continue
-                    if TAIL and i == n_tiles - 1 and o in ("exp", "et", "ev"): continue
                     fns[o](i)
-
-        if TAIL:
-            n = n_tiles - 1
-            e_sb = work.tile([P, 2, 512], BF16, tag="e_sb", name="e_sb", bufs=3)
-            at[n]["e_sb"] = e_sb
-            et = et_ring([P, 2, 2, P], F32, "et")
-            eg = work.tile([P, 2, P, 4], BF16, tag="eg", name="eg", bufs=3, align_bytes=64)
-            at[n]["eg"] = eg
-            e_codes = work.tile([P, 2 * P], U32, tag="e_codes", name="e_codes", bufs=3, align_bytes=64)
-            e_scales = work.tile([P, 2 * P], U8, tag="e_scales", name="e_scales", bufs=3, align_bytes=64)
-            at[n]["e_codes"] = e_codes
-            at[n]["e_scales"] = e_scales
-
-            def exp_g(g):
-                nc.scalar.activation(out=e_sb[:, g, :], in_=at[n]["sc"][g][:], func=ACT.Exp, bias=at[n]["negm"][:], scale=1.0, accum_out=rs_all[:, n, g : g + 1])
-                words = e_sb[:, g, :].bitcast(F32)
-                for u in range(2):
-                    nc.tensor.transpose(et[:, g, u, :], words[:, u * P : (u + 1) * P], ident_f[:])
-
-            def ev_g(g, eng):
-                dst = eg[:, g].rearrange("p t j -> p (t j)").bitcast(F32)
-                copy_on(eng, dst.rearrange("p (t u) -> p t u", u=2), et[:, g].rearrange("p u t -> p t u"))
-
-            def quant_g(g):
-                nc.vector.quantize_mx(out=e_codes[:, g * P : (g + 1) * P].bitcast(FP8X4), scales=e_scales[:, g * P : (g + 1) * P], in_=eg[:, g].rearrange("p t j -> p (t j)"))
-
-            def sums(i0):
-                rsum = work.tile([P, 2], F32, tag="rsum2", name="rsum2", bufs=2)
-                nc.gpsimd.tensor_tensor(out=rsum[:], in0=rs_all[:, i0 : i0 + 2, 0], in1=rs_all[:, i0 : i0 + 2, 1], op=ALU.add)
-                nc.vector.reciprocal(out=rinv_all[:, i0 : i0 + 2], in_=rsum[:])
-
-            def mx(i, r):
-                h_ps = r([P, E], F32, "h_ps")
-                for g in range(2):
-                    cols = slice(g * P, (g + 1) * P)
-                    nc.tensor.matmul_mx(out=h_ps[:], lhsT=at[i]["e_codes"][:, cols].bitcast(FP8X4), lhsT_scale=at[i]["e_scales"][:, cols], rhs=v_codes[:, 2 * 3 + g, :].bitcast(FP8X4), rhs_scale=v_scales[:, 2 * 3 + g, :], start=(g == 0), stop=(g == 1))
-                at[i]["h_ps"] = h_ps
-
-            def fin_half(i, c):
-                o_half = work.tile([P, 256], F32, tag="o_half", name="o_half", bufs=2)
-                cs = slice(256 * c, 256 * c + 256)
-                nc.vector.scalar_tensor_tensor(out=o_half[:], in0=at[i]["h_ps"][:, cs], scalar=rinv_all[:, i : i + 1], in1=r_sb[:, i, cs], op0=ALU.mult, op1=ALU.mult)
-                dst = out[512:1024, 3, :].rearrange("(p i) e -> p i e", i=4)
-                nc.sync.dma_start(out=dst[:, 3, cs], in_=o_half[:])
-
-            exp_g(0)
-            exp_g(1)
-            for tok in TAILSEQ.split():
-                a, m = tok[:2], tok[2:]
-                if a == "qu": e_quant(int(m))
-                elif a == "mx": mx(int(m), h_ring)
-                elif a == "ms": mx(int(m), sc_ring)
-                elif a == "fi": finish(int(m))
-                elif a == "su": sums(int(m))
-                elif a == "ev": ev_g(int(m[0]), m[1])
-                elif a == "qg": quant_g(int(m))
-                elif a == "fh": fin_half(n, int(m))

@@ -16,54 +16,11 @@ P = 128
 T, S, B, E, Z = 1024, 1024, 4, 512, 128
 FLOPS = 2 * (2 * S * B * E * E + B * T * S * Z + B * T * S * E)
 
-MANUAL = True
-XT = 3
-QK_AT = {8: [1], 10: [2], 12: [3], 14: [4]}
-K2ND = False
-T0 = 4
-HEAD = "xt0.0 xt0.1 xe0.0s xe0.1v xt1.0 xt1.1 bv wu1 xq0 xe1.0s xe1.1v br xt2.0 xt2.1 xq1 xe2.0s xe2.1v xt3.0 xt3.1 pj1.0 pj1.1 pj1.2 pj1.3 xq2 si1.0 si1.1 xe3.0v xe3.1v kt0 si1.2 si1.3 xt4.0 xt4.1 xq3 pj3.0 pj3.1 pj3.2 pj3.3 ke0 xe4.0s xe4.1s vt1.0 xt5.0 xt5.1 vt1.1 ad3.0 ad3.1 xq4 pj4.0 pj4.1 ad3.2 ad3.3 pj4.2 pj4.3 ve1.0s xe5.0s xe5.1v ve1.1v xt6.0 xt6.1 qs3.0 vq1"
-KSTEP = "xq kt si0 pj0 si1 pj1 xe0v xe1v xt0 xt1 si2 pj2 si3 pj3 vq2 qs11 ke"
-QSTEP = "vt0 vt1 xq xe0s xe1s ve0s kt ad0 pj0 ad1 pj1 xt0 xt1 ad2 pj2 ad3 pj3 ve1v vq2 qs0 ke"
-QSTEPT = "vt0 vt1 xq ad0 pj0 ad1 pj1 xe0v xe1s xt0 xt1 ve0s ad2 pj2 ad3 pj3 ve1v vq2 kt qs0 ke"
-NWARM = 5
-PRO = "sc0 sc1 kt5 kt6 rm0 qs ex rm1 sc2 ke5 ke6 kt7 vq rm2 ke7"
-HT = 2
-ASG = {15: "vvsv"}
-OB = 8
-ETS = 31
-HS = 30
-VELATE = []
-TU = [3,5,7,9,11,13,15]
-OT = 6
-OE = 7
-SC = [0, 1, 2, 3]
-ETR = [4, 5]
-HR = [6, 7]
-LEAD = 2
-NQ1 = 5
-KQ2 = {}
-V2 = {}
-VDEF = []
-V2E = "s"
-QKS = "svvvvvvv"
-MISC = None
-LAGS = dict(ev=1, quant=3, mx=4, fin=5)
-PE = ["mx", "sc", "et"]
-VO = ["fin", "rm", "quant"]
-NEG = "g"
-ORDER = ["rs", "mx", "rm", "exp", "sc", "ev", "oe", "et", "ot", "kt", "ke", "quant", "fin"]
-PAIRQ = False
-PQN = 32
-EVE = "s"
-GF = 999
-GFR = [998]
-GFT = []
-RS = 4
-RSL = 5
-RGL = 5
-XIN_BUFS = 8
-K_AFTER = 3
-Q_AFTER = 6
+N_PAIRS = 2 * B
+N_TILES = 8 * B
+N_TURNED_UNITS = 6
+X_BUFFERS = 8
+OUT_BUFFERS = 8
 
 
 def tile_gatedcrossattention_pa_t_kernel(tc, q_scaled, k, key, query, Wv, bv, Wr, br, out):
@@ -72,8 +29,7 @@ def tile_gatedcrossattention_pa_t_kernel(tc, q_scaled, k, key, query, Wv, bv, Wr
         const = ctx.enter_context(tc.tile_pool(name="const", bufs=1))
         work = ctx.enter_context(tc.tile_pool(name="work", bufs=2))
         psum = ctx.enter_context(tc.psum_pool(name="psum", bufs=1))
-        if MANUAL:
-            ctx.enter_context(tc.manual_schedule())
+        ctx.enter_context(tc.manual_schedule())
 
         def ring(banks):
             taken = []
@@ -86,49 +42,59 @@ def tile_gatedcrossattention_pa_t_kernel(tc, q_scaled, k, key, query, Wv, bv, Wr
 
             return take
 
-        def copy_on(eng, dst, src):
-            if eng == "v":
-                nc.vector.tensor_copy(out=dst, in_=src)
-            else:
-                nc.scalar.copy(out=dst, in_=src)
+        project_banks = ring([0, 1, 2, 3])
+        turn_banks = ring([4, 5, 6, 7])
+        score_banks = ring([0, 1, 2, 3])
+        e_banks = ring([4, 5])
+        h_banks = ring([6, 7])
 
-        big = ring([0, 1, 2, 3])
-        aux = ring([4, 5, 6, 7])
+        def on_vector(dst, src):
+            nc.vector.tensor_copy(out=dst, in_=src)
+
+        def on_scalar(dst, src):
+            nc.scalar.copy(out=dst, in_=src)
 
         ident_f = const.tile([P, P], F32, name="ident_f")
         ident_b = const.tile([P, P], BF16, name="ident_b")
         make_identity(nc, ident_f[:])
         make_identity(nc, ident_b[:])
         ones = const.tile([P, P], BF16, name="ones")
-        bias_rows = const.tile([P, E], BF16, name="bias_rows")
+        zeros = const.tile([P, E], BF16, name="zeros")
+        br_row = const.tile([P, E], BF16, name="br_row")
         bv_rows = const.tile([P, P], BF16, name="bv_rows")
+        br_rows = const.tile([P, P], BF16, name="br_rows")
         nc.vector.memset(ones[:], 1.0)
-        wrow = const.tile([P, E], BF16, name="wrow")
-        nc.vector.memset(wrow[:], 0.0)
-        nc.vector.memset(bias_rows[:], 0.0)
+        nc.vector.memset(zeros[:], 0.0)
+        nc.vector.memset(br_row[:], 0.0)
         nc.vector.memset(bv_rows[:], 0.0)
+        nc.vector.memset(br_rows[:], 0.0)
         nc.scalar.dma_start(out=bv_rows[0:4, :], in_=bv.rearrange("(j p) -> j p", p=P))
-        br_cols = const.tile([P, P], BF16, name="br_cols")
-        nc.vector.memset(br_cols[:], 0.0)
-        nc.scalar.dma_start(out=br_cols[0:4, :], in_=br.rearrange("(j p) -> j p", p=P))
-        nc.scalar.dma_start(out=bias_rows[0:1, :], in_=br.unsqueeze(0))
-        for i in range(NWARM):
-            warm_ps = big([P, E], F32, "warm_ps")
-            nc.tensor.matmul(warm_ps[:], lhsT=ones[:], rhs=wrow[:], start=True, stop=True)
-        warm = const.tile([P, 1], F32, name="warm")
-        nc.scalar.activation(out=warm[:], in_=ones[:, 0:1], func=ACT.Silu)
-        bias_r = const.tile([P, E], F32, name="bias_r")
-        bias_v = const.tile([P, 8], F32, name="bias_v")
+        nc.scalar.dma_start(out=br_rows[0:4, :], in_=br.rearrange("(j p) -> j p", p=P))
+        nc.scalar.dma_start(out=br_row[0:1, :], in_=br.unsqueeze(0))
 
-        def spread_bv():
-            bv_ps = big([P, 2, P], BF16, "bv_ps")
-            nc.tensor.transpose(bv_ps[:, 0, :], bv_rows[:], ident_b[:])
-            nc.tensor.transpose(bv_ps[:, 1, :], br_cols[:], ident_b[:])
-            nc.vector.tensor_copy(out=bias_v[:].rearrange("p (w j) -> p w j", w=2), in_=bv_ps[:, :, 0:4])
-        def spread_br():
-            br_ps = big([P, E], F32, "br_ps")
-            nc.tensor.matmul(br_ps[:], lhsT=ones[:], rhs=bias_rows[:], start=True, stop=True)
-            nc.scalar.copy(out=bias_r[:], in_=br_ps[:])
+        def keep_tensor_busy(n):
+            for i in range(n):
+                idle_ps = project_banks([P, E], F32, "idle_ps")
+                nc.tensor.matmul(idle_ps[:], lhsT=ones[:], rhs=zeros[:], start=True, stop=True)
+
+        table_out = const.tile([P, 1], F32, name="table_out")
+
+        def load_table(func):
+            nc.scalar.activation(out=table_out[:], in_=ones[:, 0:1], func=func)
+
+        br_all = const.tile([P, E], F32, name="br_all")
+        bias_cols = const.tile([P, 2, 4], F32, name="bias_cols")
+
+        def bias_columns():
+            cols_ps = project_banks([P, 2, P], BF16, "cols_ps")
+            nc.tensor.transpose(cols_ps[:, 0, :], bv_rows[:], ident_b[:])
+            nc.tensor.transpose(cols_ps[:, 1, :], br_rows[:], ident_b[:])
+            nc.vector.tensor_copy(out=bias_cols[:], in_=cols_ps[:, :, 0:4])
+
+        def bias_everywhere():
+            row_ps = project_banks([P, E], F32, "row_ps")
+            nc.tensor.matmul(row_ps[:], lhsT=ones[:], rhs=br_row[:], start=True, stop=True)
+            nc.scalar.copy(out=br_all[:], in_=row_ps[:])
 
         q_sb = const.tile([P, 2, 4, B * Z], BF16, name="q_sb")
         k_sb = const.tile([P, 2, 4, B * Z], BF16, name="k_sb")
@@ -138,55 +104,52 @@ def tile_gatedcrossattention_pa_t_kernel(tc, q_scaled, k, key, query, Wv, bv, Wr
         w_scales = [const.tile([P, E], U8, name="w_scales%d" % i, align_bytes=64) for i in range(2)]
         v_codes = const.tile([P, 2 * B, E], U32, name="v_codes", align_bytes=64)
         v_scales = const.tile([P, 2 * B, E], U8, name="v_scales", align_bytes=64)
-        r_sb = const.tile([P, 8 * B, E], F32, name="r_sb")
-        rs_all = const.tile([P, 8 * B, 2], F32, name="rs_all")
-        rinv_all = const.tile([P, 8 * B], F32, name="rinv_all")
+        r_sb = const.tile([P, N_PAIRS, 4, E], F32, name="r_sb")
+        sums = const.tile([P, N_TILES, 2], F32, name="sums")
+        inverse = const.tile([P, N_TILES], F32, name="inverse")
 
-        k_units = [("k", b, g) for b in range(B) for g in range(2)]
-        q_units = [("q", b, h) for b in range(B) for h in range(2)]
-        units = [("w", 0, 0), k_units[0], k_units[1], ("w", 1, 0), q_units[0]] if K2ND else [("w", 0, 0), k_units[0], ("w", 1, 0), q_units[0]]
-        for i in range(2 if K2ND else 1, 2 * B):
-            units += [k_units[i], q_units[i - 1 if K2ND else i]]
-        if K2ND: units += [q_units[2 * B - 1]]
+        units = [("w", 0), ("k", 0), ("w", 1), ("q", 0)]
+        for i in range(1, N_PAIRS):
+            units += [("k", i), ("q", i)]
         n_units = len(units)
+        last_key, last_query = n_units - 2, n_units - 1
         st = [dict() for u in range(n_units)]
-        KLAST = max(u for u in range(n_units) if units[u][0] == "k")
-
-        def load(u):
-            if u < 0 or u >= n_units:
-                return
-            kind, a, c = units[u]
-            xin = work.tile([P, 4, E], BF16, tag="xin", name="xin", bufs=XIN_BUFS)
-            if kind == "w":
-                src = (Wv, Wr)[a].rearrange("(m p) c -> p m c", p=P)
-            else:
-                src = (key if kind == "k" else query)[512 * c : 512 * c + 512, a, :].rearrange(
-                    "(p j) e -> p j e", j=4
-                )
-            pieces = 4 if u == 0 else 2 if u == 1 else 1
-            n = 4 // pieces
-            for i in range(pieces):
-                nc.sync.dma_start(out=xin[:, i * n : (i + 1) * n, :], in_=src[:, i * n : (i + 1) * n, :])
-            st[u]["xin"] = xin
 
         def is_kind(u, kind):
             return 0 <= u < n_units and units[u][0] == kind
 
-        def x_transpose(u, half):
-            if u < 0 or u >= n_units:
+        def is_turned(u):
+            return is_kind(u, "q") and units[u][1] < N_TURNED_UNITS
+
+        def load(u):
+            if u >= n_units:
                 return
-            xin = st[u]["xin"]
-            tp = aux([P, 2, 2, P], F32, "tp")
+            kind, i = units[u]
+            xin = work.tile([P, 4, E], BF16, tag="xin", name="xin", bufs=X_BUFFERS)
+            if kind == "w":
+                src = (Wv, Wr)[i].rearrange("(m p) c -> p m c", p=P)
+            else:
+                rows = slice(512 * (i % 2), 512 * (i % 2) + 512)
+                src = (key if kind == "k" else query)[rows, i // 2, :].rearrange("(p j) e -> p j e", j=4)
+            blocks = 1 if u == 0 else 2 if u == 1 else 4
+            for j in range(0, 4, blocks):
+                nc.sync.dma_start(out=xin[:, j : j + blocks, :], in_=src[:, j : j + blocks, :])
+            st[u]["xin"] = xin
+
+        def x_transpose(u, half):
+            if u >= n_units:
+                return
+            tp = turn_banks([P, 2, 2, P], F32, "tp")
             for r in range(2):
-                words = xin[:, 2 * half + r, :].bitcast(F32)
+                words = st[u]["xin"][:, 2 * half + r, :].bitcast(F32)
                 for w in range(2):
                     nc.tensor.transpose(tp[:, r, w, :], words[:, w * P : (w + 1) * P], ident_f[:])
             st[u]["tp%d" % half] = tp
             if half == 1:
-                load(u + XIN_BUFS)
+                load(u + X_BUFFERS)
 
-        def x_evac(u, half, eng):
-            if u < 0 or u >= n_units:
+        def x_copy(u, half, copy):
+            if u >= n_units:
                 return
             if half == 0:
                 grouped = work.tile([P, 4 * E], BF16, tag="grouped", name="grouped", bufs=3, align_bytes=64)
@@ -194,247 +157,258 @@ def tile_gatedcrossattention_pa_t_kernel(tc, q_scaled, k, key, query, Wv, bv, Wr
             words = st[u]["grouped"][:].bitcast(F32)[:, half * E : (half + 1) * E]
             tp = st[u]["tp%d" % half]
             if units[u][0] == "k":
-                copy_on(eng, words.rearrange("p (c r w) -> p c r w", r=2, w=2), tp[:].rearrange("p r w c -> p c r w"))
+                copy(words.rearrange("p (c r w) -> p c r w", r=2, w=2), tp[:].rearrange("p r w c -> p c r w"))
             else:
-                copy_on(eng, words.rearrange("p (r c w) -> p r c w", r=2, w=2), tp[:].rearrange("p r w c -> p r c w"))
+                copy(words.rearrange("p (r c w) -> p r c w", r=2, w=2), tp[:].rearrange("p r w c -> p r c w"))
 
-        def x_quant(u):
-            if u < 0 or u >= n_units:
+        def x_quantise(u):
+            if u >= n_units:
                 return
-            kind, a, c = units[u]
+            kind, i = units[u]
             if kind == "w":
-                codes, scales = w_codes[a], w_scales[a]
+                codes, scales = w_codes[i], w_scales[i]
             else:
                 codes = work.tile([P, E], U32, tag="x_codes", name="x_codes", bufs=2, align_bytes=64)
                 scales = work.tile([P, E], U8, tag="x_scales", name="x_scales", bufs=2, align_bytes=64)
             nc.vector.quantize_mx(out=codes[:].bitcast(FP8X4), scales=scales[:], in_=st[u]["grouped"][:])
-            st[u]["codes"] = codes
-            st[u]["scales"] = scales
+            st[u]["x"] = (codes, scales)
+
+        def mx(dst, stationary, s_cols, moving, m_cols, start=True, stop=True):
+            nc.tensor.matmul_mx(
+                out=dst,
+                lhsT=stationary[0][:, s_cols].bitcast(FP8X4),
+                lhsT_scale=stationary[1][:, s_cols],
+                rhs=moving[0][:, m_cols].bitcast(FP8X4),
+                rhs_scale=moving[1][:, m_cols],
+                start=start,
+                stop=stop,
+            )
 
         def project(u, j):
-            if not (is_kind(u, "k") or is_kind(u, "q")):
+            if u >= n_units or units[u][0] == "w":
                 return
-            pj = big([P, E], F32, "pj")
+            pj = project_banks([P, E], F32, "pj")
+            x = st[u]["x"]
             cols = slice(j * P, (j + 1) * P)
-            x = (st[u]["codes"], st[u]["scales"])
-            w = (w_codes[0], w_scales[0]) if units[u][0] == "k" else (w_codes[1], w_scales[1])
-            sta, mov = (w, x) if units[u][0] == "k" else (x, w)
-            if u in TU and j < 2:
-                for k2 in range(2):
-                    c = slice((2 * j + k2) * P, (2 * j + k2 + 1) * P)
-                    nc.tensor.matmul_mx(
-                        out=pj[:, k2 * 256 : k2 * 256 + 256],
-                        lhsT=w[0][:, c].bitcast(FP8X4),
-                        lhsT_scale=w[1][:, c],
-                        rhs=x[0][:, 0:256].bitcast(FP8X4),
-                        rhs_scale=x[1][:, 0:256],
-                        start=True,
-                        stop=True,
+            if units[u][0] == "k":
+                mx(pj[:], (w_codes[0], w_scales[0]), cols, x, slice(0, E))
+            elif is_turned(u) and j < 2:
+                for i in range(2):
+                    c = 2 * j + i
+                    mx(
+                        pj[:, i * 256 : (i + 1) * 256],
+                        (w_codes[1], w_scales[1]),
+                        slice(c * P, (c + 1) * P),
+                        x,
+                        slice(0, 256),
                     )
-                st[u]["pj%d" % j] = pj
-                return
-            nc.tensor.matmul_mx(
-                out=pj[:],
-                lhsT=sta[0][:, cols].bitcast(FP8X4),
-                lhsT_scale=sta[1][:, cols],
-                rhs=mov[0][:].bitcast(FP8X4),
-                rhs_scale=mov[1][:],
-                start=True,
-                stop=True,
-            )
+            else:
+                mx(pj[:], x, cols, (w_codes[1], w_scales[1]), slice(0, E))
             st[u]["pj%d" % j] = pj
 
         def key_silu(u, j):
-            if not is_kind(u, "k"):
-                return
             if j == 0:
-                yT = work.tile([P, 4, E], BF16, tag="yT", name="yT", bufs=2 + len(VDEF))
-                st[u]["yT"] = yT
+                vT = work.tile([P, 4, E], BF16, tag="vT", name="vT", bufs=2)
+                st[u]["vT"] = vT
             nc.scalar.activation(
-                out=st[u]["yT"][:, j, :], in_=st[u]["pj%d" % j][:], func=ACT.Silu, bias=bias_v[:, j : j + 1], scale=1.0
+                out=st[u]["vT"][:, j, :],
+                in_=st[u]["pj%d" % j][:],
+                func=ACT.Silu,
+                bias=bias_cols[:, 0, j : j + 1],
+                scale=1.0,
             )
+
+        def query_bias(u, j):
+            pj = st[u]["pj%d" % j]
+            r = r_sb[:, units[u][1]]
+            if is_turned(u) and j < 2:
+                rT = r[:, 0:2, :].rearrange("p x e -> p (x e)")
+                for i in range(2):
+                    c = 2 * j + i
+                    nc.scalar.activation(
+                        out=rT[:, c * 256 : (c + 1) * 256],
+                        in_=pj[:, i * 256 : (i + 1) * 256],
+                        func=ACT.Silu,
+                        bias=bias_cols[:, 1, c : c + 1],
+                        scale=1.0,
+                    )
+            else:
+                nc.vector.tensor_tensor(out=r[:, j, :], in0=pj[:], in1=br_all[:], op=ALU.add)
+
+        def query_silu(u, half):
+            if not is_kind(u, "q") or (is_turned(u) and half == 0):
+                return
+            r = r_sb[:, units[u][1], 2 * half : 2 * half + 2, :]
+            nc.scalar.activation(out=r, in_=r, func=ACT.Silu)
 
         def v_transpose(u, half):
             if not is_kind(u, "k"):
                 return
-            vp = (misc if u in VDEF else aux)([P, 2, 2, P], F32, "vp")
-            for jj in range(2):
-                words = st[u]["yT"][:, 2 * half + jj, :].bitcast(F32)
+            vp = turn_banks([P, 2, 2, P], F32, "vp")
+            for j in range(2):
+                words = st[u]["vT"][:, 2 * half + j, :].bitcast(F32)
                 for w in range(2):
-                    nc.tensor.transpose(vp[:, jj, w, :], words[:, w * P : (w + 1) * P], ident_f[:])
+                    nc.tensor.transpose(vp[:, j, w, :], words[:, w * P : (w + 1) * P], ident_f[:])
             st[u]["vp%d" % half] = vp
 
-        def v_evac(u, half, eng):
+        def v_copy(u, half, copy):
             if not is_kind(u, "k"):
                 return
             if half == 0:
                 vg = work.tile([P, 4 * E], BF16, tag="vg", name="vg", bufs=2, align_bytes=64)
                 st[u]["vg"] = vg
             words = st[u]["vg"][:].bitcast(F32)[:, half * E : (half + 1) * E]
-            copy_on(
-                eng,
+            copy(
                 words.rearrange("p (j c w) -> p j c w", j=2, w=2),
                 st[u]["vp%d" % half][:].rearrange("p j w c -> p j c w"),
             )
 
-        def v_quant(u):
+        def v_quantise(u):
             if not is_kind(u, "k"):
                 return
-            kind, a, c = units[u]
+            i = units[u][1]
             nc.vector.quantize_mx(
-                out=v_codes[:, 2 * a + c, :].bitcast(FP8X4),
-                scales=v_scales[:, 2 * a + c, :],
-                in_=st[u]["vg"][:],
+                out=v_codes[:, i, :].bitcast(FP8X4), scales=v_scales[:, i, :], in_=st[u]["vg"][:]
             )
 
-        def query_add(u, j):
-            if not is_kind(u, "q"):
-                return
-            kind, a, c = units[u]
-            if u in TU and j < 2:
-                i0 = 4 * (2 * a + c)
-                rT = r_sb[:, i0 : i0 + 2, :].rearrange("p x e -> p (x e)")
-                for k2 in range(2):
-                    c2 = 2 * j + k2
-                    nc.scalar.activation(
-                        out=rT[:, c2 * 256 : c2 * 256 + 256],
-                        in_=st[u]["pj%d" % j][:, k2 * 256 : k2 * 256 + 256],
-                        func=ACT.Silu,
-                        bias=bias_v[:, 4 + c2 : 5 + c2],
-                        scale=1.0,
-                    )
-                return
-            nc.vector.tensor_tensor(
-                out=r_sb[:, 4 * (2 * a + c) + j, :], in0=st[u]["pj%d" % j][:], in1=bias_r[:], op=ALU.add
-            )
-
-        def query_silu(u, half):
-            if not is_kind(u, "q"):
-                return
-            kind, a, c = units[u]
-            if u in TU and half == 0:
-                return
-            i0 = 4 * (2 * a + c) + 2 * half
-            rr = r_sb[:, i0 : i0 + 2, :]
-            nc.scalar.activation(out=rr, in_=rr, func=ACT.Silu)
-
-        qk_items = [(w, b) for b in range(B) for w in (1, 0)]
+        qk = []
+        for b in range(B):
+            qk += [(kT, k_sb, b), (qT, q_sb, b)]
         qk_ps = dict()
 
-        def qk_transpose(m):
-            if m < 0 or m >= len(qk_items):
-                return
-            w, b = qk_items[m]
-            src = (q_sb, k_sb)[w]
-            tq = (aux if m < NQ1 else misc)([P, 8, P], BF16, "tq")
+        def qk_transpose(m, banks):
+            dst, src, b = qk[m]
+            tq = banks([P, 8, P], BF16, "tq")
             for h in range(2):
                 for i in range(4):
                     nc.tensor.transpose(tq[:, 4 * h + i, :], src[:, h, i, b * Z : (b + 1) * Z], ident_b[:])
             qk_ps[m] = tq
 
-        def qk_evac(m):
-            if m < 0 or m >= len(qk_items):
-                return
-            w, b = qk_items[m]
-            dst = (qT, kT)[w][b]
-            if w == 0:
-                src = qk_ps[m][:].rearrange("p n c -> p (n c)")
-                if NEG == "acc":
-                    nc.vector.tensor_scalar(out=dst[:], in0=src, scalar1=-1.0, scalar2=0.0, op0=ALU.mult, op1=ALU.add)
-                else:
-                    copy_on(QKS[m], dst[:], src)
+        def qk_copy(m, copy):
+            dst, src, b = qk[m]
+            if dst is qT:
+                copy(dst[b][:], qk_ps[m][:].rearrange("z n p -> z (n p)"))
             else:
-                copy_on(
-                    QKS[m],
-                    dst[:].rearrange("z (x p e) -> z x p e", x=4, e=2),
+                copy(
+                    dst[b][:].rearrange("z (x p e) -> z x p e", x=4, e=2),
                     qk_ps[m][:].rearrange("z (x e) p -> z x p e", e=2),
                 )
 
-        for u in range(XIN_BUFS):
+        def both(function, u, copy=None):
+            for half in range(2):
+                if copy is None:
+                    function(u, half)
+                else:
+                    function(u, half, copy)
+
+        for u in range(X_BUFFERS):
             load(u)
-            if u == K_AFTER:
+            if u == 3:
                 nc.sync.dma_start(out=k_sb[:], in_=k.rearrange("(h p i) b z -> p h i (b z)", p=P, i=4))
-            if u == Q_AFTER:
+            if u == 6:
                 nc.sync.dma_start(out=q_sb[:], in_=q_scaled.rearrange("(h p i) b z -> p h i (b z)", p=P, i=4))
 
-        def run(t, tokens):
-            for tok in tokens.split():
-                n, rest = tok[:2], tok[2:]
-                if n == "xq": x_quant(t + 1)
-                elif n == "xt": x_transpose(t + XT, int(rest))
-                elif n == "xe": x_evac(t + 2, int(rest[0]), ASG[t][int(rest[0])] if t in ASG else rest[1])
-                elif n == "si": key_silu(t, int(rest))
-                elif n == "ad": query_add(t, int(rest))
-                elif n == "pj": project(t + 1, int(rest))
-                elif n == "vt":
-                    if t - 1 - int(rest[1:] or "0") not in VDEF: v_transpose(t - 1 - int(rest[1:] or "0"), int(rest[0]))
-                elif n == "ve":
-                    if t - 1 - int(rest[2:] or "0") not in VDEF + VELATE: v_evac(t - 1 - int(rest[2:] or "0"), int(rest[0]), ASG[t][2 + int(rest[0])] if t in ASG else rest[1])
-                elif n == "vq":
-                    if t - int(rest) not in VDEF: v_quant(t - int(rest))
-                elif n == "qs": query_silu(t - int(rest[1:] or "0"), int(rest[0]))
-                elif n == "wu":
-                    for i in range(int(rest)):
-                        warm_ps = big([P, E], F32, "warm_ps")
-                        nc.tensor.matmul(warm_ps[:], lhsT=ones[:], rhs=wrow[:], start=True, stop=True)
-                elif n == "kt":
-                    for m in qk_at.get(t, []): qk_transpose(m)
-                elif n == "ke":
-                    for m in qk_at.get(t, []): qk_evac(m)
+        keep_tensor_busy(5)
+        load_table(ACT.Silu)
+        both(x_transpose, 0)
+        x_copy(0, 0, on_scalar)
+        x_copy(0, 1, on_vector)
+        both(x_transpose, 1)
+        x_quantise(0)
+        bias_columns()
+        keep_tensor_busy(1)
+        x_copy(1, 0, on_scalar)
+        x_copy(1, 1, on_vector)
+        bias_everywhere()
+        both(x_transpose, 2)
+        x_quantise(1)
+        x_copy(2, 0, on_scalar)
+        x_copy(2, 1, on_vector)
+        both(x_transpose, 3)
+        for j in range(4):
+            project(1, j)
+        x_quantise(2)
+        for j in range(4):
+            key_silu(1, j)
+        both(x_copy, 3, on_vector)
+        qk_transpose(0, turn_banks)
+        both(x_transpose, 4)
+        x_quantise(3)
+        for j in range(4):
+            project(3, j)
+        qk_copy(0, on_scalar)
+        x_copy(4, 0, on_scalar)
+        x_copy(4, 1, on_vector)
+        v_transpose(1, 0)
+        both(x_transpose, 5)
+        v_transpose(1, 1)
+        query_bias(3, 0)
+        query_bias(3, 1)
+        x_quantise(4)
+        project(4, 0)
+        project(4, 1)
+        query_bias(3, 2)
+        query_bias(3, 3)
+        project(4, 2)
+        project(4, 3)
+        v_copy(1, 0, on_scalar)
+        x_copy(5, 0, on_vector)
+        x_copy(5, 1, on_scalar)
+        v_copy(1, 1, on_vector)
+        both(x_transpose, 6)
+        query_silu(3, 0)
+        v_quantise(1)
 
-        qk_at = QK_AT
-        for tok in HEAD.split():
-            n, rest = tok[:2], tok[2:].split(".")
-            u = int(rest[0] or "0")
-            h = int(rest[1][0]) if len(rest) > 1 else 0
-            e = rest[1][1:] if len(rest) > 1 else ""
-            if n == "xt": x_transpose(u, h)
-            elif n == "xe": x_evac(u, h, e)
-            elif n == "xq": x_quant(u)
-            elif n == "pj": project(u, h)
-            elif n == "si": key_silu(u, h)
-            elif n == "ad": query_add(u, h)
-            elif n == "vt": v_transpose(u, h)
-            elif n == "ve": v_evac(u, h, e)
-            elif n == "vq": v_quant(u)
-            elif n == "qs": query_silu(u, h)
-            elif n == "bv": spread_bv()
-            elif n == "br": spread_br()
-            elif n == "kt": qk_transpose(u)
-            elif n == "ke": qk_evac(u)
-            elif n == "wu":
-                for i in range(u):
-                    warm_ps = big([P, E], F32, "warm_ps")
-                    nc.tensor.matmul(warm_ps[:], lhsT=ones[:], rhs=wrow[:], start=True, stop=True)
-        for t in range(T0, n_units):
-            run(t, KSTEP if is_kind(t, "k") else QSTEPT if t in TU else QSTEP)
+        def key_step(t, m):
+            x_quantise(t + 1)
+            if m > 0:
+                qk_transpose(m, turn_banks)
+            for j in range(2):
+                key_silu(t, j)
+                project(t + 1, j)
+            both(x_copy, t + 2, on_vector)
+            both(x_transpose, t + 3)
+            for j in range(2, 4):
+                key_silu(t, j)
+                project(t + 1, j)
+            v_quantise(t - 2)
+            query_silu(t - 1, 1)
+            if m > 0:
+                qk_copy(m, on_vector)
 
-        n_tiles = 8 * B
-        sc_ring = ring(SC)
-        et_ring = ring(ETR)
-        h_ring = et_ring if HR is None else ring(HR)
-        misc = et_ring if MISC is None else ring(MISC)
-        at = [dict() for i in range(n_tiles)]
-        u_of = dict(((units[u][1], units[u][2]), u) for u in range(n_units) if units[u][0] == "q")
-        II = [0, 2, 1, 3]
+        def query_step(t):
+            both(v_transpose, t - 1)
+            x_quantise(t + 1)
+            for j in range(2):
+                query_bias(t, j)
+                project(t + 1, j)
+            x_copy(t + 2, 0, on_vector if is_turned(t) else on_scalar)
+            x_copy(t + 2, 1, on_scalar)
+            both(x_transpose, t + 3)
+            v_copy(t - 1, 0, on_scalar)
+            for j in range(2, 4):
+                query_bias(t, j)
+                project(t + 1, j)
+            v_copy(t - 1, 1, on_vector)
+            query_silu(t, 0)
 
-        def where(i):
-            return i // 8, (i % 8) // 4, II[i % 4]
+        for i in range(1, N_PAIRS):
+            key_step(2 + 2 * i, i - 2 if 3 <= i < 7 else 0)
+            query_step(3 + 2 * i)
 
-        def is_t(i):
-            b, h, ii = where(i)
-            return u_of[(b, h)] in TU and ii < 2
+        at = [dict() for i in range(N_TILES)]
 
+        def query_unit(i):
+            return 3 + 2 * (i // 4)
 
-        def ok(i):
-            return 0 <= i < n_tiles
+        def tile_is_turned(i):
+            return is_turned(query_unit(i)) and i % 4 < 2
 
-        def scores(i):
-            b, h, ii = where(i)
-            n = 4 * h + ii
+        def scores(i, banks):
+            b, n = i // 8, i % 8
             at[i]["sc"] = []
             for g in range(2):
-                sc = (h_ring if i == HT else sc_ring)([P, 512], F32, "sc")
+                sc = banks([P, 512], F32, "sc")
                 nc.tensor.matmul(
                     sc[:],
                     lhsT=qT[b][:, n * P : (n + 1) * P],
@@ -444,31 +418,14 @@ def tile_gatedcrossattention_pa_t_kernel(tc, q_scaled, k, key, query, Wv, bv, Wr
                 )
                 at[i]["sc"].append(sc)
 
-        def rowmax(i):
-            rmax_a(i)
-            rmax_b(i)
-            if NEG != "acc": rmax_c(i)
-
-        def rmax_a(i):
+        def row_max(i):
             m2 = work.tile([P, 2], F32, tag="m2", name="m2", bufs=4)
-            at[i]["m2"] = m2
-            nc.vector.tensor_reduce(out=m2[:, 0:1], in_=at[i]["sc"][0][:], axis=AX.X, op=ALU.min if NEG == "acc" else ALU.max)
-
-        def rmax_b(i):
-            m2 = at[i]["m2"]
-            if NEG == "acc":
-                junk = work.tile([P, 512], BF16, tag="junk", name="junk", bufs=1)
-                negm = work.tile([P, 1], F32, tag="negm", name="negm", bufs=4)
-                nc.vector.tensor_scalar(out=junk[:], in0=at[i]["sc"][1][:], scalar1=1.0, scalar2=m2[:, 0:1], op0=ALU.mult, op1=ALU.min, accum_out=negm[:])
-                at[i]["negm"] = negm
-            else:
-                nc.vector.tensor_reduce(out=m2[:, 1:2], in_=at[i]["sc"][1][:], axis=AX.X, op=ALU.max)
-
-        def rmax_c(i):
-            m2 = at[i]["m2"]
+            for g in range(2):
+                nc.vector.tensor_reduce(out=m2[:, g : g + 1], in_=at[i]["sc"][g][:], axis=AX.X, op=ALU.max)
             negm = work.tile([P, 1], F32, tag="negm", name="negm", bufs=4)
-            eng = nc.gpsimd if NEG == "g" else nc.vector
-            eng.tensor_scalar(out=negm[:], in0=m2[:, 0:1], scalar1=m2[:, 1:2], scalar2=-1.0, op0=ALU.max, op1=ALU.mult)
+            nc.gpsimd.tensor_scalar(
+                out=negm[:], in0=m2[:, 0:1], scalar1=m2[:, 1:2], scalar2=-1.0, op0=ALU.max, op1=ALU.mult
+            )
             at[i]["negm"] = negm
 
         def exps(i):
@@ -479,166 +436,133 @@ def tile_gatedcrossattention_pa_t_kernel(tc, q_scaled, k, key, query, Wv, bv, Wr
                     in_=at[i]["sc"][g][:],
                     func=ACT.Exp,
                     bias=at[i]["negm"][:],
-                    scale=-1.0 if NEG == "acc" else 1.0,
-                    accum_out=rs_all[:, i, g : g + 1],
+                    scale=1.0,
+                    accum_out=sums[:, i, g : g + 1],
                 )
             at[i]["e_sb"] = e_sb
 
-        def e_transpose(i):
-            et = (sc_ring if i >= ETS else et_ring)([P, 2, 2, P], F32, "et")
+        def e_transpose(i, banks):
+            et = banks([P, 2, 2, P], F32, "et")
             for g in range(2):
                 words = at[i]["e_sb"][:, g, :].bitcast(F32)
                 for u in range(2):
                     nc.tensor.transpose(et[:, g, u, :], words[:, u * P : (u + 1) * P], ident_f[:])
             at[i]["et"] = et
 
-        def e_evac(i):
-            if PAIRQ and i < PQN:
-                if i % 2 == 0:
-                    eg = work.tile([P, 2, 2, P, 4], BF16, tag="eg", name="eg", bufs=2, align_bytes=64)
-                    at[i]["egp"] = eg
-                at[i]["egp"] = at[i - i % 2]["egp"]
-                dst = at[i]["egp"][:, i % 2].rearrange("p g t j -> p (g t j)").bitcast(F32)
-            else:
-                eg = work.tile([P, 2, P, 4], BF16, tag="eg1", name="eg1", bufs=2 if PAIRQ else 3, align_bytes=64)
-                at[i]["eg"] = eg
-                dst = eg[:].rearrange("p g t j -> p (g t j)").bitcast(F32)
-            copy_on(EVE[i % len(EVE)], dst.rearrange("p (g t u) -> p g t u", g=2, u=2), at[i]["et"][:].rearrange("p g u t -> p g t u"))
-
-        def e_quant(i):
-            if PAIRQ and i < PQN:
-                if i % 2 == 0: return
-                e_codes = work.tile([P, 4 * P], U32, tag="e_codes", name="e_codes", bufs=2, align_bytes=64)
-                e_scales = work.tile([P, 4 * P], U8, tag="e_scales", name="e_scales", bufs=2, align_bytes=64)
-                nc.vector.quantize_mx(out=e_codes[:].bitcast(FP8X4), scales=e_scales[:], in_=at[i]["egp"][:].rearrange("p a g t j -> p (a g t j)"))
-                for d in range(2):
-                    at[i - 1 + d]["e_codes"] = e_codes[:, 2 * P * d : 2 * P * d + 2 * P]
-                    at[i - 1 + d]["e_scales"] = e_scales[:, 2 * P * d : 2 * P * d + 2 * P]
-                return
-            e_codes = work.tile([P, 2 * P], U32, tag="e_codes1", name="e_codes1", bufs=2 if PAIRQ else 3, align_bytes=64)
-            e_scales = work.tile([P, 2 * P], U8, tag="e_scales1", name="e_scales1", bufs=2 if PAIRQ else 3, align_bytes=64)
-            nc.vector.quantize_mx(
-                out=e_codes[:].bitcast(FP8X4),
-                scales=e_scales[:],
-                in_=at[i]["eg"][:].rearrange("p g t j -> p (g t j)"),
+        def e_copy(i, copy):
+            eg = work.tile([P, 2 * P * 4], BF16, tag="eg", name="eg", bufs=3, align_bytes=64)
+            copy(
+                eg[:].bitcast(F32).rearrange("p (g t u) -> p g t u", g=2, u=2),
+                at[i]["et"][:].rearrange("p g u t -> p g t u"),
             )
-            at[i]["e_codes"] = e_codes
-            at[i]["e_scales"] = e_scales
+            at[i]["eg"] = eg
 
-        def e_times_v(i):
-            b = i // 8
-            h_ps = (sc_ring if i >= HS else h_ring)([P, E], F32, "h_ps")
-            if is_t(i):
+        def e_quantise(i):
+            e_codes = work.tile([P, 2 * P], U32, tag="e_codes", name="e_codes", bufs=3, align_bytes=64)
+            e_scales = work.tile([P, 2 * P], U8, tag="e_scales", name="e_scales", bufs=3, align_bytes=64)
+            nc.vector.quantize_mx(out=e_codes[:].bitcast(FP8X4), scales=e_scales[:], in_=at[i]["eg"][:])
+            at[i]["e"] = (e_codes, e_scales)
+
+        def e_times_v(i, banks):
+            h = banks([P, E], F32, "h")
+            e = at[i]["e"]
+            v = [(v_codes[:, 2 * (i // 8) + g, :], v_scales[:, 2 * (i // 8) + g, :]) for g in range(2)]
+            halves = [slice(g * P, (g + 1) * P) for g in range(2)]
+            if tile_is_turned(i):
                 for c in range(4):
                     cols = slice(c * P, (c + 1) * P)
                     for g in range(2):
-                        q = slice(g * P, (g + 1) * P)
-                        nc.tensor.matmul_mx(
-                            out=h_ps[:, cols],
-                            lhsT=v_codes[:, 2 * b + g, cols].bitcast(FP8X4),
-                            lhsT_scale=v_scales[:, 2 * b + g, cols],
-                            rhs=at[i]["e_codes"][:, q].bitcast(FP8X4),
-                            rhs_scale=at[i]["e_scales"][:, q],
-                            start=(g == 0),
-                            stop=(g == 1),
-                        )
+                        mx(h[:, cols], v[g], cols, e, halves[g], start=(g == 0), stop=(g == 1))
             else:
                 for g in range(2):
-                    cols = slice(g * P, (g + 1) * P)
-                    nc.tensor.matmul_mx(
-                        out=h_ps[:],
-                        lhsT=at[i]["e_codes"][:, cols].bitcast(FP8X4),
-                        lhsT_scale=at[i]["e_scales"][:, cols],
-                        rhs=v_codes[:, 2 * b + g, :].bitcast(FP8X4),
-                        rhs_scale=v_scales[:, 2 * b + g, :],
-                        start=(g == 0),
-                        stop=(g == 1),
-                    )
-            at[i]["h_ps"] = h_ps
-
-        def o_transpose(i):
-            if not is_t(i): return
-            o_ps = et_ring([P, E], F32, "o_ps")
-            for c in range(4):
-                nc.tensor.transpose(o_ps[:, c * P : (c + 1) * P], at[i]["prod"][:, c, :], ident_f[:])
-            at[i]["o_ps"] = o_ps
-
-        def o_evac(i):
-            if not is_t(i): return
-            b, h, ii = where(i)
-            o_sb = work.tile([P, E], F32, tag="o_sb", name="o_sb", bufs=OB)
-            nc.scalar.activation(out=o_sb[:], in_=at[i]["o_ps"][:], func=ACT.Copy, scale=rinv_all[:, i : i + 1])
-            dst = out[512 * h : 512 * h + 512, b, :].rearrange("(p i) e -> p i e", i=4)
-            nc.sync.dma_start(out=dst[:, ii, :], in_=o_sb[:])
-
-        def row_adds(i0):
-            rsum = work.tile([P, RS], F32, tag="rsum", name="rsum", bufs=2)
-            if NEG == "g":
-                nc.gpsimd.tensor_tensor(out=rsum[:], in0=rs_all[:, i0 : i0 + RS, 0], in1=rs_all[:, i0 : i0 + RS, 1], op=ALU.add)
-            else:
-                nc.vector.tensor_reduce(out=rsum[:], in_=rs_all[:, i0 : i0 + RS, :], axis=AX.X, op=ALU.add)
-            at[i0]["rsum"] = rsum
+                    mx(h[:], e, halves[g], v[g], slice(0, E), start=(g == 0), stop=(g == 1))
+            at[i]["h"] = h
 
         def row_sums(i0):
-            if "rsum" not in at[i0]: row_adds(i0)
-            nc.vector.reciprocal(out=rinv_all[:, i0 : i0 + RS], in_=at[i0]["rsum"][:])
+            total = work.tile([P, 4], F32, tag="total", name="total", bufs=2)
+            four = slice(i0, i0 + 4)
+            nc.gpsimd.tensor_tensor(out=total[:], in0=sums[:, four, 0], in1=sums[:, four, 1], op=ALU.add)
+            nc.vector.reciprocal(out=inverse[:, four], in_=total[:])
 
-        def finish(i):
-            b, h, ii = where(i)
-            r0 = 4 * (2 * b + h)
-            if is_t(i):
-                prod = work.tile([P, 4, P], F32, tag="prod", name="prod", bufs=3)
-                rT = r_sb[:, r0 : r0 + 2, :].rearrange("p x e -> p (x e)").rearrange("p (c t) -> p c t", c=4)
+        def store(i, o_sb):
+            b, h, j = i // 8, (i % 8) // 4, i % 4
+            rows = out[512 * h : 512 * h + 512, b, :].rearrange("(p j) e -> p j e", j=4)
+            nc.sync.dma_start(out=rows[:, j, :], in_=o_sb[:])
+
+        def times_r(i):
+            r = r_sb[:, i // 4]
+            if tile_is_turned(i):
+                rT = r[:, 0:2, :].rearrange("p x e -> p (x e)").rearrange("p (c t) -> p c t", c=4)
+                hr = work.tile([P, 4, P], F32, tag="hr", name="hr", bufs=3)
                 nc.vector.tensor_tensor(
-                    out=prod[:],
-                    in0=at[i]["h_ps"][:].rearrange("p (c t) -> p c t", c=4),
-                    in1=rT[:, :, ii * P : (ii + 1) * P],
+                    out=hr[:],
+                    in0=at[i]["h"][:].rearrange("p (c t) -> p c t", c=4),
+                    in1=rT[:, :, (i % 4) * P : (i % 4 + 1) * P],
                     op=ALU.mult,
                 )
-                at[i]["prod"] = prod
-                return
-            o_sb = work.tile([P, E], F32, tag="o_sb", name="o_sb", bufs=OB)
-            nc.vector.scalar_tensor_tensor(
-                out=o_sb[:], in0=at[i]["h_ps"][:], scalar=rinv_all[:, i : i + 1], in1=r_sb[:, r0 + ii, :], op0=ALU.mult, op1=ALU.mult
-            )
-            dst = out[512 * h : 512 * h + 512, b, :].rearrange("(p i) e -> p i e", i=4)
-            nc.sync.dma_start(out=dst[:, ii, :], in_=o_sb[:])
+                at[i]["hr"] = hr
+            else:
+                o_sb = work.tile([P, E], F32, tag="o_sb", name="o_sb", bufs=OUT_BUFFERS)
+                nc.vector.scalar_tensor_tensor(
+                    out=o_sb[:],
+                    in0=at[i]["h"][:],
+                    scalar=inverse[:, i : i + 1],
+                    in1=r[:, i % 4, :],
+                    op0=ALU.mult,
+                    op1=ALU.mult,
+                )
+                store(i, o_sb)
 
-        done = set()
-        for tok in PRO.split():
-            n, m = tok[:2], int(tok[2:] or "0")
-            if n == "sc": scores(m); done.add(("sc", m))
-            elif n == "rm": rowmax(m); done.add(("rm", m))
-            elif n == "qs": query_silu(n_units - 1, 1)
-            elif n == "ex": nc.scalar.activation(out=warm[:], in_=ones[:, 0:1], func=ACT.Exp)
-            elif n == "vq": v_quant(KLAST)
-            elif n == "kt": qk_transpose(m)
-            elif n == "ke": qk_evac(m)
-            elif n == "vt": v_transpose(KLAST, m)
-            elif n == "ve": v_evac(KLAST, m, "v")
-            elif n == "VE": v_evac(KLAST, m, "s")
-        fns = dict(fin=finish, mx=e_times_v, exp=exps, sc=scores, ev=e_evac, et=e_transpose, quant=e_quant, rm=rowmax, ra=rmax_a, rb=rmax_b, rc=rmax_c, ot=o_transpose, oe=o_evac)
-        lag = dict(LAGS, ot=OT, oe=OE, exp=0, et=0, rm=-1, ra=-1, rb=-1, rc=-1, sc=-LEAD)
-        for step in range(n_tiles + 8):
-            for o in ORDER:
-                if o == "rs":
-                    if (step - RSL) % RS == 0 and ok(step - RSL): row_sums(step - RSL)
-                    continue
-                if o == "rg":
-                    if (step - RGL) % RS == 0 and ok(step - RGL): row_adds(step - RGL)
-                    continue
-                if o == "kt":
-                    if step in KQ2: qk_transpose(KQ2[step])
-                    if step in V2: v_transpose(*V2[step])
-                    continue
-                if o == "ke":
-                    if step - 1 in KQ2: qk_evac(KQ2[step - 1])
-                    if step - 1 in V2:
-                        v_evac(*V2[step - 1], V2E)
-                    if step - 2 in V2 and V2[step - 2][1] == 1:
-                        v_quant(V2[step - 2][0])
-                    continue
-                i = step - lag[o]
-                if ok(i):
-                    if (o, i) in done or (o in ("ra", "rb", "rc") and ("rm", i) in done): continue
-                    fns[o](i)
+        def turn_back(i):
+            o_ps = e_banks([P, E], F32, "o_ps")
+            for c in range(4):
+                nc.tensor.transpose(o_ps[:, c * P : (c + 1) * P], at[i]["hr"][:, c, :], ident_f[:])
+            at[i]["o_ps"] = o_ps
+
+        def divide(i):
+            o_sb = work.tile([P, E], F32, tag="o_sb", name="o_sb", bufs=OUT_BUFFERS)
+            nc.scalar.activation(out=o_sb[:], in_=at[i]["o_ps"][:], func=ACT.Copy, scale=inverse[:, i : i + 1])
+            store(i, o_sb)
+
+        scores(0, score_banks)
+        scores(1, score_banks)
+        qk_transpose(5, e_banks)
+        qk_transpose(6, e_banks)
+        row_max(0)
+        query_silu(last_query, 1)
+        load_table(ACT.Exp)
+        row_max(1)
+        scores(2, h_banks)
+        qk_copy(5, on_vector)
+        qk_copy(6, on_vector)
+        qk_transpose(7, e_banks)
+        v_quantise(last_key)
+        row_max(2)
+        qk_copy(7, on_vector)
+
+        def ok(i):
+            return 0 <= i < N_TILES
+
+        for step in range(N_TILES + 6):
+            if ok(step - 5) and (step - 5) % 4 == 0:
+                row_sums(step - 5)
+            if ok(step - 4):
+                e_times_v(step - 4, h_banks if step - 4 < N_TILES - 2 else score_banks)
+            if 3 <= step + 1 < N_TILES:
+                row_max(step + 1)
+            if ok(step):
+                exps(step)
+            if 3 <= step + 2 < N_TILES:
+                scores(step + 2, score_banks)
+            if ok(step - 1):
+                e_copy(step - 1, on_vector if step - 1 == 1 else on_scalar)
+            if ok(step - 7) and tile_is_turned(step - 7):
+                divide(step - 7)
+            if ok(step):
+                e_transpose(step, e_banks if step < N_TILES - 1 else score_banks)
+            if ok(step - 6) and tile_is_turned(step - 6):
+                turn_back(step - 6)
+            if ok(step - 3):
+                e_quantise(step - 3)
+            if ok(step - 5):
+                times_r(step - 5)

@@ -421,10 +421,12 @@ def tile_gatedcrossattention_pa_t_kernel(tc, q_scaled, k, key, query, Wv, bv, Wr
         def row_max(i):
             m2 = work.tile([P, 2], F32, tag="m2", name="m2", bufs=4)
             for g in range(2):
-                nc.vector.tensor_reduce(out=m2[:, g : g + 1], in_=at[i]["sc"][g][:], axis=AX.X, op=ALU.max)
+                nc.vector.tensor_reduce(
+                    out=m2[:, g : g + 1], in_=at[i]["sc"][g][:], axis=AX.X, op=ALU.max, negate=True
+                )
             negm = work.tile([P, 1], F32, tag="negm", name="negm", bufs=4)
             nc.gpsimd.tensor_scalar(
-                out=negm[:], in0=m2[:, 0:1], scalar1=m2[:, 1:2], scalar2=-1.0, op0=ALU.max, op1=ALU.mult
+                out=negm[:], in0=m2[:, 0:1], scalar1=m2[:, 1:2], scalar2=-3.4028234e38, op0=ALU.min, op1=ALU.max
             )
             at[i]["negm"] = negm
 
@@ -482,7 +484,10 @@ def tile_gatedcrossattention_pa_t_kernel(tc, q_scaled, k, key, query, Wv, bv, Wr
             total = work.tile([P, 4], F32, tag="total", name="total", bufs=2)
             four = slice(i0, i0 + 4)
             nc.gpsimd.tensor_tensor(out=total[:], in0=sums[:, four, 0], in1=sums[:, four, 1], op=ALU.add)
-            nc.vector.reciprocal(out=inverse[:, four], in_=total[:])
+            at[i0]["total"] = total
+
+        def inv(i0):
+            nc.vector.reciprocal(out=inverse[:, i0 : i0 + 4], in_=at[i0]["total"][:])
 
         def store(i, o_sb):
             b, h, j = i // 8, (i % 8) // 4, i % 4
@@ -562,6 +567,8 @@ def tile_gatedcrossattention_pa_t_kernel(tc, q_scaled, k, key, query, Wv, bv, Wr
                 e_transpose(step, e_banks if step < N_TILES - 1 else score_banks)
             if ok(step - 6) and tile_is_turned(step - 6):
                 turn_back(step - 6)
+            if ok(step - 5) and (step - 5) % 4 == 0:
+                inv(step - 5)
             if ok(step - 3):
                 e_quantise(step - 3)
             if ok(step - 5):

from contextlib import ExitStack

import concourse.mybir as mybir
from concourse.masks import make_identity

F32 = mybir.dt.float32
BF16 = mybir.dt.bfloat16
U32 = mybir.dt.uint32
U8 = mybir.dt.uint8
FP8X4 = mybir.dt.float8_e4m3fn_x4
ACT = mybir.ActivationFunctionType
ALU = mybir.AluOpType
AX = mybir.AxisListType

P = 128
T, S, B, E, Z = 1024, 1024, 4, 512, 128
FLOPS = 2 * (2 * S * B * E * E + B * T * S * Z + B * T * S * E)

N_PAIRS = 2 * B
N_TILES = 8 * B
N_TURNED_UNITS = 6
X_BUFFERS = 8
OUT_BUFFERS = 8


def tile_gatedcrossattention_pa_t_kernel(tc, q_scaled, k, key, query, Wv, bv, Wr, br, out):
    nc = tc.nc
    with ExitStack() as ctx:
        const = ctx.enter_context(tc.tile_pool(name="const", bufs=1))
        work = ctx.enter_context(tc.tile_pool(name="work", bufs=2))
        psum = ctx.enter_context(tc.psum_pool(name="psum", bufs=1))
        ctx.enter_context(tc.manual_schedule())

        def ring(banks):
            taken = []

            def take(shape, dtype, name):
                b = banks[len(taken) % len(banks)]
                taken.append(b)
                bank = psum.tile(shape, dtype, tag="bank%d" % b, name=name, bufs=1)
                return bank

            return take

        project_banks = ring([0, 1, 2, 3])
        turn_banks = ring([4, 5, 6, 7])
        score_banks = ring([0, 1, 2, 3])
        e_banks = ring([4, 5])
        h_banks = ring([6, 7])

        def on_vector(dst, src):
            nc.vector.tensor_copy(out=dst, in_=src)

        def on_scalar(dst, src):
            nc.scalar.copy(out=dst, in_=src)

        ident_f = const.tile([P, P], F32, name="ident_f")
        ident_b = const.tile([P, P], BF16, name="ident_b")
        make_identity(nc, ident_f[:])
        make_identity(nc, ident_b[:])
        ones = const.tile([P, P], BF16, name="ones")
        zeros = const.tile([P, E], BF16, name="zeros")
        br_row = const.tile([P, E], BF16, name="br_row")
        bv_rows = const.tile([P, P], BF16, name="bv_rows")
        br_rows = const.tile([P, P], BF16, name="br_rows")
        nc.vector.memset(ones[:], 1.0)
        nc.vector.memset(zeros[:], 0.0)
        nc.vector.memset(br_row[:], 0.0)
        nc.vector.memset(bv_rows[:], 0.0)
        nc.vector.memset(br_rows[:], 0.0)
        nc.scalar.dma_start(out=bv_rows[0:4, :], in_=bv.rearrange("(j p) -> j p", p=P))
        nc.scalar.dma_start(out=br_rows[0:4, :], in_=br.rearrange("(j p) -> j p", p=P))
        nc.scalar.dma_start(out=br_row[0:1, :], in_=br.unsqueeze(0))

        def keep_tensor_busy(n):
            for i in range(n):
                idle_ps = project_banks([P, E], F32, "idle_ps")
                nc.tensor.matmul(idle_ps[:], lhsT=ones[:], rhs=zeros[:], start=True, stop=True)

        table_out = const.tile([P, 1], F32, name="table_out")

        def load_table(func):
            nc.scalar.activation(out=table_out[:], in_=ones[:, 0:1], func=func)

        br_all = const.tile([P, E], F32, name="br_all")
        bias_cols = const.tile([P, 2, 4], F32, name="bias_cols")

        def bias_columns():
            cols_ps = project_banks([P, 2, P], BF16, "cols_ps")
            nc.tensor.transpose(cols_ps[:, 0, :], bv_rows[:], ident_b[:])
            nc.tensor.transpose(cols_ps[:, 1, :], br_rows[:], ident_b[:])
            nc.vector.tensor_copy(out=bias_cols[:], in_=cols_ps[:, :, 0:4])

        def bias_everywhere():
            row_ps = project_banks([P, E], F32, "row_ps")
            nc.tensor.matmul(row_ps[:], lhsT=ones[:], rhs=br_row[:], start=True, stop=True)
            nc.scalar.copy(out=br_all[:], in_=row_ps[:])

        q_sb = const.tile([P, 2, 4, B * Z], BF16, name="q_sb")
        k_sb = const.tile([P, 2, 4, B * Z], BF16, name="k_sb")
        qT = [const.tile([P, T], BF16, name="qT%d" % b) for b in range(B)]
        kT = [const.tile([P, S], BF16, name="kT%d" % b) for b in range(B)]
        w_codes = [const.tile([P, E], U32, name="w_codes%d" % i, align_bytes=64) for i in range(2)]
        w_scales = [const.tile([P, E], U8, name="w_scales%d" % i, align_bytes=64) for i in range(2)]
        v_codes = const.tile([P, 2 * B, E], U32, name="v_codes", align_bytes=64)
        v_scales = const.tile([P, 2 * B, E], U8, name="v_scales", align_bytes=64)
        r_sb = const.tile([P, N_PAIRS, 4, E], F32, name="r_sb")
        sums = const.tile([P, N_TILES, 2], F32, name="sums")
        inverse = const.tile([P, N_TILES], F32, name="inverse")

        units = [("w", 0), ("k", 0), ("w", 1), ("q", 0)]
        for i in range(1, N_PAIRS):
            units += [("k", i), ("q", i)]
        n_units = len(units)
        last_key, last_query = n_units - 2, n_units - 1
        st = [dict() for u in range(n_units)]

        def is_kind(u, kind):
            return 0 <= u < n_units and units[u][0] == kind

        def is_turned(u):
            return is_kind(u, "q") and units[u][1] < N_TURNED_UNITS

        def load(u):
            if u >= n_units:
                return
            kind, i = units[u]
            xin = work.tile([P, 4, E], BF16, tag="xin", name="xin", bufs=X_BUFFERS)
            if kind == "w":
                src = (Wv, Wr)[i].rearrange("(m p) c -> p m c", p=P)
            else:
                rows = slice(512 * (i % 2), 512 * (i % 2) + 512)
                src = (key if kind == "k" else query)[rows, i // 2, :].rearrange("(p j) e -> p j e", j=4)
            blocks = 1 if u == 0 else 2 if u == 1 else 4
            for j in range(0, 4, blocks):
                nc.sync.dma_start(out=xin[:, j : j + blocks, :], in_=src[:, j : j + blocks, :])
            st[u]["xin"] = xin

        def x_transpose(u, half):
            if u >= n_units:
                return
            tp = turn_banks([P, 2, 2, P], F32, "tp")
            for r in range(2):
                words = st[u]["xin"][:, 2 * half + r, :].bitcast(F32)
                for w in range(2):
                    nc.tensor.transpose(tp[:, r, w, :], words[:, w * P : (w + 1) * P], ident_f[:])
            st[u]["tp%d" % half] = tp
            if half == 1:
                load(u + X_BUFFERS)

        def x_copy(u, half, copy):
            if u >= n_units:
                return
            if half == 0:
                grouped = work.tile([P, 4 * E], BF16, tag="grouped", name="grouped", bufs=3, align_bytes=64)
                st[u]["grouped"] = grouped
            words = st[u]["grouped"][:].bitcast(F32)[:, half * E : (half + 1) * E]
            tp = st[u]["tp%d" % half]
            if units[u][0] == "k":
                copy(words.rearrange("p (c r w) -> p c r w", r=2, w=2), tp[:].rearrange("p r w c -> p c r w"))
            else:
                copy(words.rearrange("p (r c w) -> p r c w", r=2, w=2), tp[:].rearrange("p r w c -> p r c w"))

        def x_quantise(u):
            if u >= n_units:
                return
            kind, i = units[u]
            if kind == "w":
                codes, scales = w_codes[i], w_scales[i]
            else:
                codes = work.tile([P, E], U32, tag="x_codes", name="x_codes", bufs=2, align_bytes=64)
                scales = work.tile([P, E], U8, tag="x_scales", name="x_scales", bufs=2, align_bytes=64)
            nc.vector.quantize_mx(out=codes[:].bitcast(FP8X4), scales=scales[:], in_=st[u]["grouped"][:])
            st[u]["x"] = (codes, scales)

        def mx(dst, stationary, s_cols, moving, m_cols, start=True, stop=True):
            nc.tensor.matmul_mx(
                out=dst,
                lhsT=stationary[0][:, s_cols].bitcast(FP8X4),
                lhsT_scale=stationary[1][:, s_cols],
                rhs=moving[0][:, m_cols].bitcast(FP8X4),
                rhs_scale=moving[1][:, m_cols],
                start=start,
                stop=stop,
            )

        def project(u, j):
            if u >= n_units or units[u][0] == "w":
                return
            pj = project_banks([P, E], F32, "pj")
            x = st[u]["x"]
            cols = slice(j * P, (j + 1) * P)
            if units[u][0] == "k":
                mx(pj[:], (w_codes[0], w_scales[0]), cols, x, slice(0, E))
            elif is_turned(u) and j < 2:
                for i in range(2):
                    c = 2 * j + i
                    mx(
                        pj[:, i * 256 : (i + 1) * 256],
                        (w_codes[1], w_scales[1]),
                        slice(c * P, (c + 1) * P),
                        x,
                        slice(0, 256),
                    )
            else:
                mx(pj[:], x, cols, (w_codes[1], w_scales[1]), slice(0, E))
            st[u]["pj%d" % j] = pj

        def key_silu(u, j):
            if j == 0:
                vT = work.tile([P, 4, E], BF16, tag="vT", name="vT", bufs=2)
                st[u]["vT"] = vT
            nc.scalar.activation(
                out=st[u]["vT"][:, j, :],
                in_=st[u]["pj%d" % j][:],
                func=ACT.Silu,
                bias=bias_cols[:, 0, j : j + 1],
                scale=1.0,
            )

        def query_bias(u, j):
            pj = st[u]["pj%d" % j]
            r = r_sb[:, units[u][1]]
            if is_turned(u) and j < 2:
                rT = r[:, 0:2, :].rearrange("p x e -> p (x e)")
                for i in range(2):
                    c = 2 * j + i
                    nc.scalar.activation(
                        out=rT[:, c * 256 : (c + 1) * 256],
                        in_=pj[:, i * 256 : (i + 1) * 256],
                        func=ACT.Silu,
                        bias=bias_cols[:, 1, c : c + 1],
                        scale=1.0,
                    )
            else:
                nc.vector.tensor_tensor(out=r[:, j, :], in0=pj[:], in1=br_all[:], op=ALU.add)

        def query_silu(u, half):
            if not is_kind(u, "q") or (is_turned(u) and half == 0):
                return
            r = r_sb[:, units[u][1], 2 * half : 2 * half + 2, :]
            nc.scalar.activation(out=r, in_=r, func=ACT.Silu)

        def v_transpose(u, half):
            if not is_kind(u, "k"):
                return
            vp = turn_banks([P, 2, 2, P], F32, "vp")
            for j in range(2):
                words = st[u]["vT"][:, 2 * half + j, :].bitcast(F32)
                for w in range(2):
                    nc.tensor.transpose(vp[:, j, w, :], words[:, w * P : (w + 1) * P], ident_f[:])
            st[u]["vp%d" % half] = vp

        def v_copy(u, half, copy):
            if not is_kind(u, "k"):
                return
            if half == 0:
                vg = work.tile([P, 4 * E], BF16, tag="vg", name="vg", bufs=2, align_bytes=64)
                st[u]["vg"] = vg
            words = st[u]["vg"][:].bitcast(F32)[:, half * E : (half + 1) * E]
            copy(
                words.rearrange("p (j c w) -> p j c w", j=2, w=2),
                st[u]["vp%d" % half][:].rearrange("p j w c -> p j c w"),
            )

        def v_quantise(u):
            if not is_kind(u, "k"):
                return
            i = units[u][1]
            nc.vector.quantize_mx(
                out=v_codes[:, i, :].bitcast(FP8X4), scales=v_scales[:, i, :], in_=st[u]["vg"][:]
            )

        qk = []
        for b in range(B):
            qk += [(kT, k_sb, b), (qT, q_sb, b)]
        qk_ps = dict()

        def qk_transpose(m, banks):
            dst, src, b = qk[m]
            tq = banks([P, 8, P], BF16, "tq")
            for h in range(2):
                for i in range(4):
                    nc.tensor.transpose(tq[:, 4 * h + i, :], src[:, h, i, b * Z : (b + 1) * Z], ident_b[:])
            qk_ps[m] = tq

        def qk_copy(m, copy):
            dst, src, b = qk[m]
            if dst is qT:
                copy(dst[b][:], qk_ps[m][:].rearrange("z n p -> z (n p)"))
            else:
                copy(
                    dst[b][:].rearrange("z (x p e) -> z x p e", x=4, e=2),
                    qk_ps[m][:].rearrange("z (x e) p -> z x p e", e=2),
                )

        def both(function, u, copy=None):
            for half in range(2):
                if copy is None:
                    function(u, half)
                else:
                    function(u, half, copy)

        for u in range(X_BUFFERS):
            load(u)
            if u == 3:
                nc.sync.dma_start(out=k_sb[:], in_=k.rearrange("(h p i) b z -> p h i (b z)", p=P, i=4))
            if u == 6:
                nc.sync.dma_start(out=q_sb[:], in_=q_scaled.rearrange("(h p i) b z -> p h i (b z)", p=P, i=4))

        keep_tensor_busy(5)
        load_table(ACT.Silu)
        both(x_transpose, 0)
        x_copy(0, 0, on_scalar)
        x_copy(0, 1, on_vector)
        both(x_transpose, 1)
        x_quantise(0)
        bias_columns()
        keep_tensor_busy(1)
        x_copy(1, 0, on_scalar)
        x_copy(1, 1, on_vector)
        bias_everywhere()
        both(x_transpose, 2)
        x_quantise(1)
        x_copy(2, 0, on_scalar)
        x_copy(2, 1, on_vector)
        both(x_transpose, 3)
        for j in range(4):
            project(1, j)
        x_quantise(2)
        for j in range(4):
            key_silu(1, j)
        both(x_copy, 3, on_vector)
        qk_transpose(0, turn_banks)
        both(x_transpose, 4)
        x_quantise(3)
        for j in range(4):
            project(3, j)
        qk_copy(0, on_scalar)
        x_copy(4, 0, on_scalar)
        x_copy(4, 1, on_vector)
        v_transpose(1, 0)
        both(x_transpose, 5)
        v_transpose(1, 1)
        query_bias(3, 0)
        query_bias(3, 1)
        x_quantise(4)
        project(4, 0)
        project(4, 1)
        query_bias(3, 2)
        query_bias(3, 3)
        project(4, 2)
        project(4, 3)
        v_copy(1, 0, on_scalar)
        x_copy(5, 0, on_vector)
        x_copy(5, 1, on_scalar)
        v_copy(1, 1, on_vector)
        both(x_transpose, 6)
        query_silu(3, 0)
        v_quantise(1)

        def key_step(t, m):
            x_quantise(t + 1)
            if m > 0:
                qk_transpose(m, turn_banks)
            for j in range(2):
                key_silu(t, j)
                project(t + 1, j)
            both(x_copy, t + 2, on_vector)
            both(x_transpose, t + 3)
            for j in range(2, 4):
                key_silu(t, j)
                project(t + 1, j)
            v_quantise(t - 2)
            query_silu(t - 1, 1)
            if m > 0:
                qk_copy(m, on_vector)

        def query_step(t):
            both(v_transpose, t - 1)
            x_quantise(t + 1)
            for j in range(2):
                query_bias(t, j)
                project(t + 1, j)
            x_copy(t + 2, 0, on_vector if is_turned(t) else on_scalar)
            x_copy(t + 2, 1, on_scalar)
            both(x_transpose, t + 3)
            v_copy(t - 1, 0, on_scalar)
            for j in range(2, 4):
                query_bias(t, j)
                project(t + 1, j)
            v_copy(t - 1, 1, on_vector)
            query_silu(t, 0)

        for i in range(1, N_PAIRS):
            key_step(2 + 2 * i, i - 2 if 3 <= i < 7 else 0)
            query_step(3 + 2 * i)

        at = [dict() for i in range(N_TILES)]

        def query_unit(i):
            return 3 + 2 * (i // 4)

        def tile_is_turned(i):
            return is_turned(query_unit(i)) and i % 4 < 2

        def scores(i, banks):
            b, n = i // 8, i % 8
            at[i]["sc"] = []
            for g in range(2):
                sc = banks([P, 512], F32, "sc")
                nc.tensor.matmul(
                    sc[:],
                    lhsT=qT[b][:, n * P : (n + 1) * P],
                    rhs=kT[b][:, g * 512 : (g + 1) * 512],
                    start=True,
                    stop=True,
                )
                at[i]["sc"].append(sc)

        def row_max(i):
            m2 = work.tile([P, 2], F32, tag="m2", name="m2", bufs=4)
            for g in range(2):
                nc.vector.tensor_reduce(
                    out=m2[:, g : g + 1], in_=at[i]["sc"][g][:], axis=AX.X, op=ALU.max, negate=True
                )
            negm = work.tile([P, 1], F32, tag="negm", name="negm", bufs=4)
            nc.gpsimd.tensor_scalar(
                out=negm[:], in0=m2[:, 0:1], scalar1=m2[:, 1:2], scalar2=-3.4028234e38, op0=ALU.min, op1=ALU.max
            )
            at[i]["negm"] = negm

        def exps(i):
            e_sb = work.tile([P, 2, 512], BF16, tag="e_sb", name="e_sb", bufs=3)
            for g in range(2):
                nc.scalar.activation(
                    out=e_sb[:, g, :],
                    in_=at[i]["sc"][g][:],
                    func=ACT.Exp,
                    bias=at[i]["negm"][:],
                    scale=1.0,
                    accum_out=sums[:, i, g : g + 1],
                )
            at[i]["e_sb"] = e_sb

        def e_transpose(i, banks):
            et = banks([P, 2, 2, P], F32, "et")
            for g in range(2):
                words = at[i]["e_sb"][:, g, :].bitcast(F32)
                for u in range(2):
                    nc.tensor.transpose(et[:, g, u, :], words[:, u * P : (u + 1) * P], ident_f[:])
            at[i]["et"] = et

        def e_copy(i, copy):
            eg = work.tile([P, 2 * P * 4], BF16, tag="eg", name="eg", bufs=3, align_bytes=64)
            copy(
                eg[:].bitcast(F32).rearrange("p (g t u) -> p g t u", g=2, u=2),
                at[i]["et"][:].rearrange("p g u t -> p g t u"),
            )
            at[i]["eg"] = eg

        def e_quantise(i):
            e_codes = work.tile([P, 2 * P], U32, tag="e_codes", name="e_codes", bufs=3, align_bytes=64)
            e_scales = work.tile([P, 2 * P], U8, tag="e_scales", name="e_scales", bufs=3, align_bytes=64)
            nc.vector.quantize_mx(out=e_codes[:].bitcast(FP8X4), scales=e_scales[:], in_=at[i]["eg"][:])
            at[i]["e"] = (e_codes, e_scales)

        def e_times_v(i, banks):
            h = banks([P, E], F32, "h")
            e = at[i]["e"]
            v = [(v_codes[:, 2 * (i // 8) + g, :], v_scales[:, 2 * (i // 8) + g, :]) for g in range(2)]
            halves = [slice(g * P, (g + 1) * P) for g in range(2)]
            if tile_is_turned(i):
                for c in range(4):
                    cols = slice(c * P, (c + 1) * P)
                    for g in range(2):
                        mx(h[:, cols], v[g], cols, e, halves[g], start=(g == 0), stop=(g == 1))
            else:
                for g in range(2):
                    mx(h[:], e, halves[g], v[g], slice(0, E), start=(g == 0), stop=(g == 1))
            at[i]["h"] = h

        def row_sums(i0):
            total = work.tile([P, 4], F32, tag="total", name="total", bufs=2)
            four = slice(i0, i0 + 4)
            nc.gpsimd.tensor_tensor(out=total[:], in0=sums[:, four, 0], in1=sums[:, four, 1], op=ALU.add)
            at[i0]["total"] = total

        def inv(i0):
            nc.vector.reciprocal(out=inverse[:, i0 : i0 + 4], in_=at[i0]["total"][:])

        def store(i, o_sb):
            b, h, j = i // 8, (i % 8) // 4, i % 4
            rows = out[512 * h : 512 * h + 512, b, :].rearrange("(p j) e -> p j e", j=4)
            nc.sync.dma_start(out=rows[:, j, :], in_=o_sb[:])

        def times_r(i):
            r = r_sb[:, i // 4]
            if tile_is_turned(i):
                rT = r[:, 0:2, :].rearrange("p x e -> p (x e)").rearrange("p (c t) -> p c t", c=4)
                hr = work.tile([P, 4, P], F32, tag="hr", name="hr", bufs=3)
                nc.vector.tensor_tensor(
                    out=hr[:],
                    in0=at[i]["h"][:].rearrange("p (c t) -> p c t", c=4),
                    in1=rT[:, :, (i % 4) * P : (i % 4 + 1) * P],
                    op=ALU.mult,
                )
                at[i]["hr"] = hr
            else:
                o_sb = work.tile([P, E], F32, tag="o_sb", name="o_sb", bufs=OUT_BUFFERS)
                nc.vector.scalar_tensor_tensor(
                    out=o_sb[:],
                    in0=at[i]["h"][:],
                    scalar=inverse[:, i : i + 1],
                    in1=r[:, i % 4, :],
                    op0=ALU.mult,
                    op1=ALU.mult,
                )
                store(i, o_sb)

        def turn_back(i):
            o_ps = e_banks([P, E], F32, "o_ps")
            for c in range(4):
                nc.tensor.transpose(o_ps[:, c * P : (c + 1) * P], at[i]["hr"][:, c, :], ident_f[:])
            at[i]["o_ps"] = o_ps

        def divide(i):
            o_sb = work.tile([P, E], F32, tag="o_sb", name="o_sb", bufs=OUT_BUFFERS)
            nc.scalar.activation(out=o_sb[:], in_=at[i]["o_ps"][:], func=ACT.Copy, scale=inverse[:, i : i + 1])
            store(i, o_sb)

        scores(0, score_banks)
        scores(1, score_banks)
        qk_transpose(5, e_banks)
        qk_transpose(6, e_banks)
        row_max(0)
        query_silu(last_query, 1)
        load_table(ACT.Exp)
        row_max(1)
        scores(2, h_banks)
        qk_copy(5, on_vector)
        qk_copy(6, on_vector)
        qk_transpose(7, e_banks)
        v_quantise(last_key)
        row_max(2)
        qk_copy(7, on_vector)

        def ok(i):
            return 0 <= i < N_TILES

        for step in range(N_TILES + 6):
            if ok(step - 5) and (step - 5) % 4 == 0:
                row_sums(step - 5)
            if ok(step - 4):
                e_times_v(step - 4, h_banks if step - 4 < N_TILES - 2 else score_banks)
            if 3 <= step + 1 < N_TILES:
                row_max(step + 1)
            if ok(step):
                exps(step)
            if 3 <= step + 2 < N_TILES:
                scores(step + 2, score_banks)
            if ok(step - 1):
                e_copy(step - 1, on_vector if step - 1 == 1 else on_scalar)
            if ok(step - 7) and tile_is_turned(step - 7):
                divide(step - 7)
            if ok(step):
                e_transpose(step, e_banks if step < N_TILES - 1 else score_banks)
            if ok(step - 6) and tile_is_turned(step - 6):
                turn_back(step - 6)
            if ok(step - 5) and (step - 5) % 4 == 0:
                inv(step - 5)
            if ok(step - 3):
                e_quantise(step - 3)
            if ok(step - 5):
                times_r(step - 5)
